import numpy as np
import ml_dtypes


def mxq(x, axis, fmt="e4m3"):
    dtype, down = {"e4m3": (ml_dtypes.float8_e4m3fn, 7), "e5m2": (ml_dtypes.float8_e5m2, 14)}[fmt]
    v = np.moveaxis(np.asarray(x, np.float32).astype(ml_dtypes.bfloat16).astype(np.float64), axis, -1)
    blocks = v.reshape(v.shape[:-1] + (-1, 32))
    amax = np.abs(blocks).max(-1, keepdims=True)
    byte = np.maximum(np.where(amax > 0, np.frexp(amax)[1] - 1 + 127, 0) - down, 1)
    scale = np.exp2(byte - 127.0)
    codes = (blocks / scale).astype(np.float32).astype(dtype).astype(np.float64)
    return np.moveaxis((codes * scale).reshape(v.shape), -1, axis)


WIDE = False


def mx_kscale(k):
    if not WIDE:
        return np.ones(k)
    levels = np.array([10, -10, 5, -5, 0])
    a = np.random.permutation(np.resize(levels, k // 512 * 4)).reshape(k // 512, 4)
    idx = np.arange(k)
    return np.exp2(a[idx // 512, idx % 128 // 32])


BF16 = ml_dtypes.bfloat16


def bf(x):
    return np.asarray(x, np.float32).astype(BF16)


def f64(x):
    return np.asarray(x).astype(np.float64)


B, C, H, W, OC = 1, 999, 64, 64, 1024
CS = 5
PAD = CS // 2
EPS = 1e-12
INC = C + CS * CS
BLK = 32
CELL = 4


def setup_inputs():
    s = np.array(mx_kscale(INC), dtype=np.float64)
    s[(C // BLK) * BLK:] = 1.0
    coarse = np.random.standard_normal((B, C, H // CELL, W // CELL))
    feature = 0.7 * (np.random.standard_normal((B, C, H, W)) + np.repeat(np.repeat(coarse, CELL, axis=2), CELL, axis=3))
    wsc = np.concatenate([np.full(C, 1.0 / np.sqrt(C)), np.full(CS * CS, 0.3)])
    conv_w = np.random.standard_normal((OC, INC)) * wsc / s
    return {"feature": bf(feature * s[:C][None, :, None, None]), "conv_w": bf(conv_w), "conv_b": bf(np.random.standard_normal(OC) * 0.3)}


def reference(feature, conv_w, conv_b):
    feature, conv_w, conv_b = f64(feature), f64(conv_w), f64(conv_b)
    b, c, h, w = feature.shape
    norm = np.sqrt(np.sum(feature * feature, axis=1, keepdims=True))
    fn = feature / np.maximum(norm, EPS)
    fp = np.pad(fn, ((0, 0), (0, 0), (PAD, PAD), (PAD, PAD)))
    sims = []
    for cc in range(CS):
        for r in range(CS):
            sims.append(np.sum(fp[:, :, r:h + r, cc:w + cc] * fn, axis=1))
    vol = np.stack(sims, axis=1)
    x = np.concatenate([feature, vol], axis=1)
    xq = mxq(x, 1, "e4m3").reshape(b, c + CS * CS, h * w)
    out = (mxq(conv_w, 1, "e4m3") @ xq).reshape(b, conv_w.shape[0], h, w) + conv_b[None, :, None, None]
    return np.maximum(out, 0.0)

@@ -1,0 +1,325 @@
+from contextlib import ExitStack
+
+import concourse.mybir as mybir
+from concourse.masks import make_identity
+
+FLOPS = 2 * 1024 * 1024 * 4096 + 2 * 25 * 999 * 4096
+
+BF16 = mybir.dt.bfloat16
+F32 = mybir.dt.float32
+U32 = mybir.dt.uint32
+U8 = mybir.dt.uint8
+I32 = mybir.dt.int32
+FP8X4 = mybir.dt.float8_e4m3fn_x4
+ACT = mybir.ActivationFunctionType
+ALU = mybir.AluOpType
+
+P = 128
+HW = 4096
+HWP = 4112
+OC = 1024
+NB = 512
+NWIN = 22
+SBI = 46
+TCW = 36
+WPITCH = 4 * TCW
+PN = NWIN * WPITCH
+EPS2 = 1e-24
+
+S1B = 896 * HW
+VPB = S1B + 409600
+
+ROW_OFF = (1, 2, 4, 5)
+COMBOS = ((0, 0, 1), (0, 1, 2), (1, 0, 0), (1, 1, 1), (2, 0, -2), (2, 1, -1), (3, 1, -2))
+LOAD_ROWS = (0, 8, 16, 32, 48, 64)
+STAGES = ((0, 24, 0, 9), (24, 48, 9, 17), (48, 64, 17, 22))
+
+
+def tile_spatialcontext_kernel(tc, feature, conv_w, conv_b, out):
+    nc = tc.nc
+    feat = feature.rearrange("b c h w -> (b c) (h w)")
+    out2 = out.rearrange("b o h w -> (b o) (h w)")
+    flat = out.rearrange("b o h w -> (b o h w)")
+
+    with ExitStack() as ctx:
+        keep = ctx.enter_context(tc.tile_pool(name="keep", bufs=1))
+        stage = ctx.enter_context(tc.tile_pool(name="stage", bufs=2))
+        codes = ctx.enter_context(tc.tile_pool(name="codes", bufs=3))
+        outs = ctx.enter_context(tc.tile_pool(name="outs", bufs=7))
+        lan = ctx.enter_context(tc.tile_pool(name="lan", bufs=1))
+        lan2 = ctx.enter_context(tc.tile_pool(name="lan2", bufs=2))
+        ps_acc = ctx.enter_context(tc.psum_pool(name="ps_acc", bufs=3))
+        ps_g = ctx.enter_context(tc.psum_pool(name="ps_g", bufs=1))
+        ps_x0 = ctx.enter_context(tc.psum_pool(name="ps_x0", bufs=2))
+        ps_x = ctx.enter_context(tc.psum_pool(name="ps_x", bufs=1))
+
+        ident_f = keep.tile([P, P], F32, name="ident_f")
+        make_identity(nc, ident_f[:])
+        ident_b = keep.tile([P, P], BF16, name="ident_b")
+        make_identity(nc, ident_b[:])
+
+        raw0 = keep.tile([P, 4, HWP], BF16, name="raw0")
+        raw1 = keep.tile([P, 4, HWP], BF16, name="raw1")
+        raws = [raw0, raw1]
+        sb = keep.tile([P, 8, 2, SBI, 32], BF16, name="sb")
+        ti = keep.tile([P, P], F32, name="ti")
+        gi = keep.tile([64, 5, 64, 5], F32, name="gi")
+        gq = keep.tile([64, 5, 5, 64], F32, name="gq")
+        gm = keep.tile([64, 5, 5, 64], F32, name="gm")
+        vv = keep.tile([64, 5, 5, 64], F32, name="vv")
+        rin = keep.tile([64, 68], F32, name="rin")
+        r5 = keep.tile([64, 5, 72], F32, name="r5")
+        n2 = keep.tile([64, 64], F32, name="n2")
+        nrm = keep.tile([64, 64], F32, name="nrm")
+        w_codes = keep.tile([P, 2, OC], U32, name="w_codes", align_bytes=64)
+        w_scales = keep.tile([P, 2, OC], U8, name="w_scales", align_bytes=64)
+        bias = keep.tile([P, 8], F32, name="bias")
+        b_in = keep.tile([P, P], BF16, name="b_in")
+
+        nc.vector.memset(raw1[0:8].rearrange("p j w -> p (j w)").bitcast(I32), 0)
+        nc.vector.memset(raw0[:, :, HW:HWP], 0.0)
+        nc.vector.memset(raw1[:, :, HW:HWP], 0.0)
+        sbf = sb[:].rearrange("p s k i x -> p (s k) (i x)")
+        nc.vector.memset(sbf[:, :, 0:64], 0.0)
+        nc.vector.memset(sbf[:, :, 44 * 32 : 46 * 32], 0.0)
+        nc.gpsimd.memset(ti[:], 0.0)
+        nc.gpsimd.memset(gi[:], 0.0)
+        nc.gpsimd.memset(gq[:], 0.0)
+        nc.gpsimd.memset(gm[:], 0.0)
+        nc.gpsimd.memset(rin[:], 0.0)
+        nc.gpsimd.memset(r5[:], 0.0)
+        nc.gpsimd.memset(b_in[:], 0.0)
+
+        for c in range(5):
+            cols = slice(LOAD_ROWS[c] * 64, LOAD_ROWS[c + 1] * 64)
+            nc.sync.dma_start(out=raw0[:, :, cols], in_=feat[0:512, cols].rearrange("(p j) w -> p j w", j=4))
+            nc.sync.dma_start(out=raw1[8:128, :, cols], in_=feat[512:992, cols].rearrange("(p j) w -> p j w", j=4))
+            nc.sync.dma_start(out=raw1[1:8, 0, cols], in_=feat[992:999, cols])
+        for c in range(5):
+            j0 = 0 if c == 0 else (LOAD_ROWS[c] - 3) // 3 + 1
+            j1 = (LOAD_ROWS[c + 1] - 3) // 3 + 1
+            for g in range(2):
+                rows = raws[g][:, :, 64:HW].rearrange("p t (j r x) -> p t j r x", r=3, x=64)
+                for k in range(2):
+                    nc.vector.tensor_copy(
+                        out=sb[:, 4 * g : 4 * g + 4, k, 2 + 2 * j0 : 2 + 2 * j1, :].rearrange("p t (j r) x -> p t j r x", r=2),
+                        in_=rows[:, :, j0:j1, 0:2, 32 * k : 32 * k + 32],
+                    )
+
+        wv = conv_w.rearrange("(m p) k -> p m k", p=P)
+        nc.sync.dma_start(out=b_in[0:8, :], in_=conv_b.rearrange("(m p) -> m p", p=P))
+        b_ps = ps_g.tile([P, P], BF16, name="b_ps", tag="gps")
+        nc.tensor.transpose(b_ps[:], b_in[:], ident_b[:])
+        nc.vector.tensor_copy(out=bias[:], in_=b_ps[:, 0:8])
+        for mp in range(4):
+            w_sb = stage.tile([P, 2, OC], BF16, name="w_sb", tag="grouped", align_bytes=64)
+            w_tail = stage.tile([P, 2, 32], BF16, name="w_tail")
+            ms = slice(2 * mp, 2 * mp + 2)
+            nc.sync.dma_start(out=w_sb[:, :, 0:512], in_=wv[:, ms, 0:512])
+            nc.sync.dma_start(out=w_sb[:, :, 544:1024], in_=wv[:, ms, 512:992])
+            nc.sync.dma_start(out=w_tail[:], in_=wv[:, ms, 992:1024])
+            oct_w = w_sb[:, :, 512:544].rearrange("p m (q t) -> p m q t", t=4)
+            nc.vector.tensor_copy(out=oct_w[:, :, :, 1:4], in_=w_tail[:, :, 8:32].rearrange("p m (q t) -> p m q t", t=3))
+            nc.vector.tensor_copy(out=oct_w[:, :, 1:8, 0], in_=w_tail[:, :, 0:7])
+            nc.vector.tensor_copy(out=oct_w[:, :, 0:1, 0], in_=w_tail[:, :, 7:8])
+            w32 = w_sb[:].rearrange("p m k -> p (m k)").bitcast(F32).rearrange("p (m k) -> p m k", m=2)
+            wg = stage.tile([P, 2, 1024], BF16, name="wg", tag="grouped", align_bytes=64)
+            for g in range(2):
+                wt = ps_acc.tile([P, 2, 2, P], F32, name="wt", tag="acc")
+                for m2 in range(2):
+                    for u in range(2):
+                        nc.tensor.transpose(wt[:, m2, u, :], w32[:, m2, 256 * g + u : 256 * (g + 1) : 2], ident_f[:])
+                nc.scalar.copy(
+                    out=wg[:, g, :].bitcast(F32).rearrange("p (m o u) -> p m o u", m=2, u=2),
+                    in_=wt[:].rearrange("p m u o -> p m o u"),
+                )
+                nc.vector.quantize_mx(
+                    out=w_codes[:, g, 256 * mp : 256 * (mp + 1)].bitcast(FP8X4),
+                    scales=w_scales[:, g, 256 * mp : 256 * (mp + 1)],
+                    in_=wg[:, g, :],
+                )
+
+        gps_box = [None]
+        gs_box = [None]
+
+        def gram_window(wi, first, last):
+            if first:
+                gps_new = ps_g.tile([P, 3, 2, 2, TCW], F32, name="gps", tag="gps")
+                gps_box[0] = (gps_new, wi)
+            gps, wi0 = gps_box[0]
+            gs, gs0 = gs_box[0]
+            sl = wi - wi0
+            ts0 = 1 if wi == 0 else 0
+            t_row = 3 * (wi - 1) + 2
+            for k in range(2):
+                c0 = 2 if k == 0 else 0
+                x0 = 0 if k == 0 else 30
+                for s in range(8):
+                    img = raws[s // 4][:, s % 4, 0:HW].rearrange("p (y x) -> p y x", x=64)
+                    nc.tensor.matmul(
+                        gps[:, sl, k, ts0:2, c0 : c0 + 34],
+                        lhsT=sb[:, s, k, 2 * wi : 2 * wi + 4, :].rearrange("p i x -> p (i x)"),
+                        rhs=img[:, t_row + ts0 : t_row + 2, x0 : x0 + 34],
+                        start=(s == 0),
+                        stop=(s == 7),
+                    )
+            if last:
+                for k in range(2):
+                    c0 = 2 if k == 0 else 0
+                    lo = 0
+                    if wi0 == 0:
+                        nc.scalar.copy(out=gs[:, 0, k, 1:2, c0 : c0 + 34], in_=gps[:, 0, k, 1:2, c0 : c0 + 34])
+                        lo = 1
+                    nc.scalar.copy(out=gs[:, wi0 - gs0 + lo : wi - gs0 + 1, k, :, c0 : c0 + 34], in_=gps[:, lo : sl + 1, k, :, c0 : c0 + 34])
+
+        def lane_tile(m):
+            b = 192 * m if m < 21 else 3968
+            xs = []
+            for d in range(3):
+                pool = ps_x0 if d == 0 else ps_x
+                xt = pool.tile([P, 1024], BF16, name="x%d" % d)
+                for s in range(8):
+                    nc.tensor.transpose(xt[:, P * s : P * (s + 1)], raws[s // 4][:, s % 4, b + d : b + d + P], ident_b[:])
+                xs.append(xt)
+            x0s = lan2.tile([P, 1024], BF16, name="x0s")
+            nc.scalar.copy(out=x0s[:], in_=xs[0][:])
+            js = lan.tile([P, 1024], BF16, name="js")
+            nc.scalar.activation(out=js[:], in_=xs[0][:], func=ACT.Square, accum_out=ti[:, m : m + 1])
+            for d in (1, 2):
+                jv = lan.tile([P, 1024], F32, name="jv")
+                nc.vector.scalar_tensor_tensor(
+                    out=jv[:], in0=xs[d][:], scalar=1.0, in1=x0s[:], op0=ALU.mult, op1=ALU.mult,
+                    accum_out=ti[:, 32 * d + m : 32 * d + m + 1],
+                )
+
+        def chain(ylo, yhi, i0, i1):
+            nc.sync.dma_start(
+                out=flat[S1B : S1B + P * PN].rearrange("(i c) -> i c", c=PN)[:, i0 * WPITCH : i1 * WPITCH],
+                in_=gs_box[0][0][:, 0 : i1 - i0].rearrange("p a k b c -> p (a k b c)"),
+            )
+            for rho, ts, dy in COMBOS:
+                ws = [w for w in range(i0 - 1, i1 - 1) if 0 <= 3 * w + ROW_OFF[rho] <= 63 and 0 <= 3 * w + 2 + ts <= 63]
+                w0 = ws[0]
+                nw = len(ws)
+                r0 = 3 * w0 + ROW_OFF[rho]
+                for k in range(2):
+                    base = S1B + 32 * rho * PN + (w0 + 1) * WPITCH + k * 2 * TCW + ts * TCW
+                    src = flat[base : base + 32 * (PN + 1)].rearrange("(x c) -> x c", c=PN + 1)
+                    src = src[:, 0 : nw * WPITCH].rearrange("x (w c) -> w x c", c=WPITCH)[:, :, 0:5]
+                    nc.sync.dma_start(out=gi[r0 : r0 + 3 * (nw - 1) + 1 : 3, dy + 2, 32 * k : 32 * k + 32, :], in_=src)
+            lt = ps_g.tile([P, P], F32, name="lt", tag="gps")
+            nc.tensor.transpose(lt[:], ti[:], ident_f[:])
+            lts = stage.tile([P, P], F32, name="lts")
+            nc.scalar.copy(out=lts[:], in_=lt[:])
+            m1 = min(i1, 21)
+            for s in range(3):
+                for yy in range(2):
+                    nc.sync.dma_start(
+                        out=gm[3 * i0 + yy : 3 * (m1 - 1) + yy + 1 : 3, 2, 2 + s, :],
+                        in_=lts[32 * s + i0 : 32 * s + m1, 64 * yy : 64 * yy + 64],
+                    )
+                if i1 == 22:
+                    nc.sync.dma_start(out=gm[63:64, 2, 2 + s, :], in_=lts[32 * s + 21 : 32 * s + 22, 64:128])
+            nc.vector.memset(gq[:, :, 0:2, 0:2], 0.0)
+            nc.vector.memset(gq[:, :, 3:5, 62:64], 0.0)
+            for em in range(5):
+                sh = em - 2
+                xlo = max(0, -sh)
+                xhi = min(64, 64 - sh)
+                nc.vector.tensor_copy(out=gq[:, :, em, xlo:xhi], in_=gi[:, :, xlo + sh : xhi + sh, 4 - em])
+            for dym in (-2, -1, 1, 2):
+                y0 = max(ylo, -dym)
+                y1 = min(yhi, 64 - dym)
+                nc.sync.dma_start(out=gm[y0:y1, dym + 2, :, :], in_=gq[y0 + dym : y1 + dym, 2 - dym, :, :])
+            ga = gq
+            nc.vector.tensor_tensor(out=ga[:], in0=gi[:].rearrange("p d x e -> p d e x"), in1=gm[:], op=ALU.add)
+            nc.vector.memset(ga[:, 2, 3, 63:64], 0.0)
+            nc.vector.memset(ga[:, 2, 4, 62:64], 0.0)
+            nc.vector.tensor_copy(out=ga[:, 2, 1, 1:64], in_=ga[:, 2, 3, 0:63])
+            nc.vector.tensor_copy(out=ga[:, 2, 0, 2:64], in_=ga[:, 2, 4, 0:62])
+            nc.vector.tensor_scalar_max(out=n2[:], in0=ga[:, 2, 2, :], scalar1=EPS2)
+            nc.scalar.activation(out=nrm[:], in_=n2[:], func=ACT.Sqrt)
+            nc.vector.reciprocal(out=rin[:, 2:66], in_=nrm[:])
+            for dy in (-2, -1, 1, 2):
+                y0 = max(ylo, -dy)
+                y1 = min(yhi, 64 - dy)
+                nc.sync.dma_start(out=r5[y0:y1, dy + 2, 0:68], in_=rin[y0 + dy : y1 + dy, :])
+            nc.vector.tensor_copy(out=r5[:, 2, 0:68], in_=rin[:])
+            ga25 = ga[:].rearrange("p d e x -> p (d e) x")
+            nc.vector.tensor_tensor(out=ga25, in0=ga25, in1=rin[:, 2:66].unsqueeze(1).to_broadcast([64, 25, 64]), op=ALU.mult)
+            for e in range(5):
+                nc.vector.tensor_tensor(out=vv[:, e, :, :], in0=ga[:, :, e, :], in1=r5[:, :, e : e + 64], op=ALU.mult)
+            nc.sync.dma_start(
+                out=flat[VPB : VPB + 25 * HW].rearrange("(j y x) -> y j x", j=25, x=64)[ylo:yhi],
+                in_=vv[ylo:yhi].rearrange("p e d x -> p (e d) x"),
+            )
+            vp24 = flat[VPB + HW : VPB + 25 * HW].rearrange("(q t w) -> q t w", q=8, t=3)
+            vp0 = flat[VPB : VPB + HW].rearrange("(o w) -> o w", o=1)
+            for n in range(ylo // 8, yhi // 8):
+                cols = slice(n * NB, (n + 1) * NB)
+                vt = stage.tile([8, 4, NB], F32, name="vt")
+                nc.sync.dma_start(out=vt[0:8, 1:4, :], in_=vp24[:, :, cols])
+                nc.sync.dma_start(out=vt[0:1, 0, :], in_=vp0[:, cols])
+                nc.vector.tensor_copy(out=raw1[0:8, 1:4, cols], in_=vt[0:8, 1:4, :])
+                nc.scalar.copy(out=raw1[0:1, 0, cols], in_=vt[0:1, 0, :])
+
+        held = keep.tile([P, 6, NB], F32, name="held")
+
+        def conv_block(n, hold_last):
+            cols = slice(n * NB, (n + 1) * NB)
+            x_codes = codes.tile([P, 2, NB], U32, name="x_codes", align_bytes=64)
+            x_scales = codes.tile([P, 2, NB], U8, name="x_scales", align_bytes=64)
+            for g in range(2):
+                grouped = stage.tile([P, NB, 4], BF16, name="grouped", tag="grouped", align_bytes=64)
+                view = raws[g][:, :, cols].rearrange("p j w -> p w j")
+                if g == 0:
+                    nc.gpsimd.tensor_scalar(out=grouped[:], in0=view, scalar1=1.0, scalar2=0.0, op0=ALU.mult, op1=ALU.add)
+                else:
+                    nc.vector.tensor_copy(out=grouped[:], in_=view)
+                nc.vector.quantize_mx(
+                    out=x_codes[:, g, :].bitcast(FP8X4), scales=x_scales[:, g, :], in_=grouped[:].rearrange("p w j -> p (w j)")
+                )
+            for m in range(8):
+                acc = ps_acc.tile([P, NB], F32, name="acc", tag="acc")
+                for g in range(2):
+                    nc.tensor.matmul_mx(
+                        out=acc[:],
+                        lhsT=w_codes[:, g, m * P : (m + 1) * P].bitcast(FP8X4),
+                        lhsT_scale=w_scales[:, g, m * P : (m + 1) * P],
+                        rhs=x_codes[:, g, :].bitcast(FP8X4),
+                        rhs_scale=x_scales[:, g, :],
+                        start=(g == 0),
+                        stop=(g == 1),
+                    )
+                if m == 7 and hold_last:
+                    nc.scalar.activation(out=held[:, n, :], in_=acc[:], func=ACT.Relu, bias=bias[:, m : m + 1], scale=1.0)
+                else:
+                    ot = outs.tile([P, NB], F32, name="ot")
+                    nc.scalar.activation(out=ot[:], in_=acc[:], func=ACT.Relu, bias=bias[:, m : m + 1], scale=1.0)
+                    nc.scalar.dma_start(out=out2[m * P : (m + 1) * P, cols], in_=ot[:])
+
+        def steps(i0, i1, blocks):
+            gs_new = lan.tile([P, 9, 2, 2, TCW], F32, name="gs")
+            nc.gpsimd.memset(gs_new[:], 0.0)
+            gs_box[0] = (gs_new, i0)
+            done = 0
+            for i in range(i0, i1):
+                gram_window(i, (i - i0) % 3 == 0, (i - i0) % 3 == 2 or i == i1 - 1)
+                lane_tile(i)
+                if done < len(blocks) and (i - i0) % 3 == 2:
+                    conv_block(blocks[done], True)
+                    done += 1
+            for n in blocks[done:]:
+                conv_block(n, True)
+
+        steps(0, 9, [])
+        chain(*STAGES[0])
+        steps(9, 17, [])
+        chain(*STAGES[1])
+        steps(17, 22, [0, 1])
+        chain(*STAGES[2])
+        for n in range(2, 6):
+            conv_block(n, True)
+        nc.scalar.dma_start(out=out2[7 * P : 8 * P, 0 : 6 * NB], in_=held[:].rearrange("p n w -> p (n w)"))
+        conv_block(6, False)
+        conv_block(7, False)

@@ -273,7 +273,7 @@ def tile_spatialcontext_kernel(tc, feature, conv_w, conv_b, out):
                 grouped = stage.tile([P, NB, 4], BF16, name="grouped", tag="grouped", align_bytes=64)
                 view = raws[g][:, :, cols].rearrange("p j w -> p w j")
                 if g == 0:
-                    nc.gpsimd.tensor_scalar(out=grouped[:], in0=view, scalar1=1.0, scalar2=0.0, op0=ALU.mult, op1=ALU.add)
+                    nc.scalar.copy(out=grouped[:], in_=view)
                 else:
                     nc.vector.tensor_copy(out=grouped[:], in_=view)
                 nc.vector.quantize_mx(

@@ -13,26 +13,35 @@ I32 = mybir.dt.int32
 FP8X4 = mybir.dt.float8_e4m3fn_x4
 ACT = mybir.ActivationFunctionType
 ALU = mybir.AluOpType
+AX = mybir.AxisListType
 
 P = 128
 HW = 4096
 HWP = 4112
 OC = 1024
 NB = 512
-NWIN = 22
-SBI = 46
-TCW = 36
-WPITCH = 4 * TCW
-PN = NWIN * WPITCH
-EPS2 = 1e-24
+EPS = 1e-12
 
-S1B = 896 * HW
-VPB = S1B + 409600
+SW = 24
+X0 = (0, 20, 40)
+CLO = (0, 2, 2)
+CHI = (22, 22, 24)
+CP = 25
+NG = 10
 
-ROW_OFF = (1, 2, 4, 5)
-COMBOS = ((0, 0, 1), (0, 1, 2), (1, 0, 0), (1, 1, 1), (2, 0, -2), (2, 1, -1), (3, 1, -2))
-LOAD_ROWS = (0, 8, 16, 32, 48, 64)
-STAGES = ((0, 24, 0, 9), (24, 48, 9, 17), (48, 64, 17, 22))
+RP = 80
+LP = 8
+IMG = 68 * RP
+S0 = 896 * HW
+RIB = S0
+VRB = S0 + 5 * IMG
+ZW = 1616
+
+LOAD_ROWS = (0, 12, 22, 36, 53, 64)
+STAGES = ((0, 4, 0, 2, (0,)), (4, 7, 2, 3, (1,)), (7, 12, 3, 6, (2, 3)), (12, 17, 6, 9, (4, 5)), (17, 22, 9, 11, (6, 7)))
+NWMAX = 5
+NMMAX = 3
+NRMAX = 16
 
 
 def tile_spatialcontext_kernel(tc, feature, conv_w, conv_b, out):
@@ -44,13 +53,15 @@ def tile_spatialcontext_kernel(tc, feature, conv_w, conv_b, out):
     with ExitStack() as ctx:
         keep = ctx.enter_context(tc.tile_pool(name="keep", bufs=1))
         stage = ctx.enter_context(tc.tile_pool(name="stage", bufs=2))
-        codes = ctx.enter_context(tc.tile_pool(name="codes", bufs=3))
-        outs = ctx.enter_context(tc.tile_pool(name="outs", bufs=7))
+        patch = ctx.enter_context(tc.tile_pool(name="patch", bufs=2))
+        chain = ctx.enter_context(tc.tile_pool(name="chain", bufs=2))
+        codes = ctx.enter_context(tc.tile_pool(name="codes", bufs=2))
+        outs = ctx.enter_context(tc.tile_pool(name="outs", bufs=4))
         lan = ctx.enter_context(tc.tile_pool(name="lan", bufs=1))
         lan2 = ctx.enter_context(tc.tile_pool(name="lan2", bufs=2))
-        ps_acc = ctx.enter_context(tc.psum_pool(name="ps_acc", bufs=3))
-        ps_g = ctx.enter_context(tc.psum_pool(name="ps_g", bufs=1))
-        ps_x0 = ctx.enter_context(tc.psum_pool(name="ps_x0", bufs=2))
+        ps_acc = ctx.enter_context(tc.psum_pool(name="ps_acc", bufs=2))
+        ps_g = ctx.enter_context(tc.psum_pool(name="ps_g", bufs=2))
+        ps_v = ctx.enter_context(tc.psum_pool(name="ps_v", bufs=1))
         ps_x = ctx.enter_context(tc.psum_pool(name="ps_x", bufs=1))
 
         ident_f = keep.tile([P, P], F32, name="ident_f")
@@ -61,209 +72,308 @@ def tile_spatialcontext_kernel(tc, feature, conv_w, conv_b, out):
         raw0 = keep.tile([P, 4, HWP], BF16, name="raw0")
         raw1 = keep.tile([P, 4, HWP], BF16, name="raw1")
         raws = [raw0, raw1]
-        sb = keep.tile([P, 8, 2, SBI, 32], BF16, name="sb")
-        ti = keep.tile([P, P], F32, name="ti")
-        gi = keep.tile([64, 5, 64, 5], F32, name="gi")
-        gq = keep.tile([64, 5, 5, 64], F32, name="gq")
-        gm = keep.tile([64, 5, 5, 64], F32, name="gm")
-        vv = keep.tile([64, 5, 5, 64], F32, name="vv")
-        rin = keep.tile([64, 68], F32, name="rin")
-        r5 = keep.tile([64, 5, 72], F32, name="r5")
-        n2 = keep.tile([64, 64], F32, name="n2")
-        nrm = keep.tile([64, 64], F32, name="nrm")
+        vraw = keep.tile([P, 44, 64], F32, name="vraw")
+        gm0 = keep.tile([P, NG, 2, CP], F32, name="gm0")
+        gm1 = keep.tile([P, NG, 2, CP], F32, name="gm1")
+        gms = [gm0, gm1]
+        held = keep.tile([P, 6, NB], F32, name="held")
         w_codes = keep.tile([P, 2, OC], U32, name="w_codes", align_bytes=64)
         w_scales = keep.tile([P, 2, OC], U8, name="w_scales", align_bytes=64)
         bias = keep.tile([P, 8], F32, name="bias")
         b_in = keep.tile([P, P], BF16, name="b_in")
 
         nc.vector.memset(raw1[0:8].rearrange("p j w -> p (j w)").bitcast(I32), 0)
-        nc.vector.memset(raw0[:, :, HW:HWP], 0.0)
-        nc.vector.memset(raw1[:, :, HW:HWP], 0.0)
-        sbf = sb[:].rearrange("p s k i x -> p (s k) (i x)")
-        nc.vector.memset(sbf[:, :, 0:64], 0.0)
-        nc.vector.memset(sbf[:, :, 44 * 32 : 46 * 32], 0.0)
-        nc.gpsimd.memset(ti[:], 0.0)
-        nc.gpsimd.memset(gi[:], 0.0)
-        nc.gpsimd.memset(gq[:], 0.0)
-        nc.gpsimd.memset(gm[:], 0.0)
-        nc.gpsimd.memset(rin[:], 0.0)
-        nc.gpsimd.memset(r5[:], 0.0)
+        heldf = held[:].rearrange("p n w -> p (n w)")
+        nc.gpsimd.memset(heldf[:, 0:ZW], 0.0)
+        nc.gpsimd.memset(gm0[:], 0.0)
+        nc.gpsimd.memset(gm1[:], 0.0)
         nc.gpsimd.memset(b_in[:], 0.0)
 
-        for c in range(5):
+        def load(c):
             cols = slice(LOAD_ROWS[c] * 64, LOAD_ROWS[c + 1] * 64)
             nc.sync.dma_start(out=raw0[:, :, cols], in_=feat[0:512, cols].rearrange("(p j) w -> p j w", j=4))
             nc.sync.dma_start(out=raw1[8:128, :, cols], in_=feat[512:992, cols].rearrange("(p j) w -> p j w", j=4))
             nc.sync.dma_start(out=raw1[1:8, 0, cols], in_=feat[992:999, cols])
-        for c in range(5):
-            j0 = 0 if c == 0 else (LOAD_ROWS[c] - 3) // 3 + 1
-            j1 = (LOAD_ROWS[c + 1] - 3) // 3 + 1
+
+        load(0)
+        nc.sync.dma_start(out=flat[S0 : S0 + P * ZW].rearrange("(p c) -> p c", c=ZW), in_=heldf[:, 0:ZW])
+        for c in range(1, 5):
+            load(c)
+
+        iop = keep.tile([P, 1], F32, name="iop")
+        nc.gpsimd.iota(iop[:], pattern=[[0, 1]], base=0, channel_multiplier=1, allow_small_or_imprecise_dtypes=True)
+        t24 = keep.tile([P, 5], F32, name="t24")
+        nc.gpsimd.iota(t24[:], pattern=[[24, 5]], base=24, channel_multiplier=0, allow_small_or_imprecise_dtypes=True)
+        th = keep.tile([P, 5, 6], F32, name="th")
+        nc.gpsimd.iota(th[:], pattern=[[1, 5], [5, 6]], base=-2, channel_multiplier=0, allow_small_or_imprecise_dtypes=True)
+        brow = keep.tile([P, 5], F32, name="brow")
+        nc.gpsimd.iota(brow[:], pattern=[[-1, 5]], base=7, channel_multiplier=0, allow_small_or_imprecise_dtypes=True)
+        crow = keep.tile([P, CP], F32, name="crow")
+        nc.gpsimd.iota(crow[:], pattern=[[1, CP]], base=0, channel_multiplier=0, allow_small_or_imprecise_dtypes=True)
+        j1 = keep.tile([P, P], F32, name="j1")
+        nc.gpsimd.memset(j1[:], -1.0)
+        nc.gpsimd.iota(j1[:, 0:25], pattern=[[1, 25]], base=0, channel_multiplier=0, allow_small_or_imprecise_dtypes=True)
+        nc.gpsimd.iota(j1[:, 64:89], pattern=[[-5, 5], [1, 5]], base=20, channel_multiplier=0, allow_small_or_imprecise_dtypes=True)
+        nc.gpsimd.memset(j1[:, 32:37], 11.0)
+        nc.gpsimd.memset(j1[:, 96:101], 12.0)
+
+        ge = keep.tile([P, 5], F32, name="ge")
+        nc.vector.tensor_scalar(out=ge[:], in0=t24[:], scalar1=iop[:, 0:1], scalar2=None, op0=ALU.is_le)
+        s5 = keep.tile([P, 1], F32, name="s5")
+        nc.vector.tensor_reduce(out=s5[:], in_=ge[:], axis=AX.X, op=ALU.add)
+        ii = keep.tile([P, 1], F32, name="ii")
+        nc.vector.scalar_tensor_tensor(out=ii[:], in0=s5[:], scalar=-24.0, in1=iop[:], op0=ALU.mult, op1=ALU.add)
+        ge2 = keep.tile([P, 5, 6], F32, name="ge2")
+        nc.vector.tensor_scalar(out=ge2[:], in0=th[:], scalar1=ii[:, 0:1], scalar2=None, op0=ALU.is_le)
+        cnt = keep.tile([P, 5], F32, name="cnt")
+        nc.vector.tensor_reduce(out=cnt[:], in_=ge2[:], axis=AX.X, op=ALU.add)
+        tmp = keep.tile([P, 5], F32, name="tmp")
+        nc.vector.tensor_scalar(out=tmp[:], in0=brow[:], scalar1=ii[:, 0:1], scalar2=None, op0=ALU.add)
+        ee = keep.tile([P, 5], F32, name="ee")
+        nc.vector.scalar_tensor_tensor(out=ee[:], in0=cnt[:], scalar=-5.0, in1=tmp[:], op0=ALU.mult, op1=ALU.add)
+        pen = keep.tile([P, 1], F32, name="pen")
+        nc.vector.tensor_scalar(out=pen[:], in0=s5[:], scalar1=5.0, scalar2=1000.0, op0=ALU.is_ge, op1=ALU.mult)
+        sp = keep.tile([P, 1], F32, name="sp")
+        nc.vector.tensor_tensor(out=sp[:], in0=s5[:], in1=pen[:], op=ALU.add)
+        k1 = keep.tile([P, 5], F32, name="k1")
+        nc.vector.tensor_scalar(out=k1[:], in0=ee[:], scalar1=5.0, scalar2=sp[:, 0:1], op0=ALU.mult, op1=ALU.add)
+        fall = keep.tile([P, 5, P], F32, name="fall")
+        nc.vector.tensor_tensor(
+            out=fall[:], in0=j1[:].unsqueeze(1).to_broadcast([P, 5, P]), in1=k1[:].unsqueeze(2).to_broadcast([P, 5, P]), op=ALU.is_equal
+        )
+        dd = keep.tile([P, CP], F32, name="dd")
+        nc.vector.tensor_scalar(out=dd[:], in0=crow[:], scalar1=ii[:, 0:1], scalar2=None, op0=ALU.subtract)
+        d2 = keep.tile([P, CP], F32, name="d2")
+        nc.vector.tensor_tensor(out=d2[:], in0=dd[:], in1=dd[:], op=ALU.mult)
+        lt96 = keep.tile([P, 1], F32, name="lt96")
+        nc.vector.tensor_scalar(out=lt96[:], in0=iop[:], scalar1=96.0, scalar2=None, op0=ALU.is_lt)
+        mask = keep.tile([P, 2, CP], F32, name="mask")
+        nc.vector.tensor_scalar(out=mask[:, 0, :], in0=d2[:], scalar1=4.5, scalar2=lt96[:, 0:1], op0=ALU.is_le, op1=ALU.mult)
+        nc.vector.tensor_scalar(out=mask[:, 1, :], in0=d2[:], scalar1=4.5, scalar2=None, op0=ALU.is_le)
+
+        sbts = {}
+        ubts = {}
+
+        def prep(si):
+            w0, w1, m0, m1, blocks = STAGES[si]
+            ylo = 3 * w0 - 2
+            nr = 3 * (w1 - w0) + 2
+            ya = max(0, ylo)
+            yb = min(64, ylo + nr)
+            sbt = patch.tile([P, 8, 3, (3 * NWMAX + 2) * SW + 8], BF16, name="sbt")
+            if ya > ylo:
+                nc.vector.memset(sbt[:, :, :, 0 : (ya - ylo) * SW], 0.0)
+            nc.vector.memset(sbt[:, :, :, (yb - ylo) * SW : nr * SW + 8], 0.0)
             for g in range(2):
-                rows = raws[g][:, :, 64:HW].rearrange("p t (j r x) -> p t j r x", r=3, x=64)
-                for k in range(2):
+                img = raws[g][:, :, 0:HW].rearrange("p t (y x) -> p t y x", x=64)
+                for sg in range(3):
                     nc.vector.tensor_copy(
-                        out=sb[:, 4 * g : 4 * g + 4, k, 2 + 2 * j0 : 2 + 2 * j1, :].rearrange("p t (j r) x -> p t j r x", r=2),
-                        in_=rows[:, :, j0:j1, 0:2, 32 * k : 32 * k + 32],
+                        out=sbt[:, 4 * g : 4 * g + 4, sg, (ya - ylo) * SW : (yb - ylo) * SW].rearrange("p t (y x) -> p t y x", x=SW),
+                        in_=img[:, :, ya:yb, X0[sg] : X0[sg] + SW],
                     )
-
-        wv = conv_w.rearrange("(m p) k -> p m k", p=P)
-        nc.sync.dma_start(out=b_in[0:8, :], in_=conv_b.rearrange("(m p) -> m p", p=P))
-        b_ps = ps_g.tile([P, P], BF16, name="b_ps", tag="gps")
-        nc.tensor.transpose(b_ps[:], b_in[:], ident_b[:])
-        nc.vector.tensor_copy(out=bias[:], in_=b_ps[:, 0:8])
-        for mp in range(4):
-            w_sb = stage.tile([P, 2, OC], BF16, name="w_sb", tag="grouped", align_bytes=64)
-            w_tail = stage.tile([P, 2, 32], BF16, name="w_tail")
-            ms = slice(2 * mp, 2 * mp + 2)
-            nc.sync.dma_start(out=w_sb[:, :, 0:512], in_=wv[:, ms, 0:512])
-            nc.sync.dma_start(out=w_sb[:, :, 544:1024], in_=wv[:, ms, 512:992])
-            nc.sync.dma_start(out=w_tail[:], in_=wv[:, ms, 992:1024])
-            oct_w = w_sb[:, :, 512:544].rearrange("p m (q t) -> p m q t", t=4)
-            nc.vector.tensor_copy(out=oct_w[:, :, :, 1:4], in_=w_tail[:, :, 8:32].rearrange("p m (q t) -> p m q t", t=3))
-            nc.vector.tensor_copy(out=oct_w[:, :, 1:8, 0], in_=w_tail[:, :, 0:7])
-            nc.vector.tensor_copy(out=oct_w[:, :, 0:1, 0], in_=w_tail[:, :, 7:8])
-            w32 = w_sb[:].rearrange("p m k -> p (m k)").bitcast(F32).rearrange("p (m k) -> p m k", m=2)
-            wg = stage.tile([P, 2, 1024], BF16, name="wg", tag="grouped", align_bytes=64)
+            sbts[si] = sbt
+            k0 = 2 * m0
+            k1_ = min(2 * m1, 21)
+            ubt = patch.tile([P, 8, NMMAX * P + 8], BF16, name="ubt")
+            nc.vector.memset(ubt[:, :, (k1_ - k0) * 64 : (m1 - m0) * P + 8], 0.0)
             for g in range(2):
-                wt = ps_acc.tile([P, 2, 2, P], F32, name="wt", tag="acc")
-                for m2 in range(2):
-                    for u in range(2):
-                        nc.tensor.transpose(wt[:, m2, u, :], w32[:, m2, 256 * g + u : 256 * (g + 1) : 2], ident_f[:])
-                nc.scalar.copy(
-                    out=wg[:, g, :].bitcast(F32).rearrange("p (m o u) -> p m o u", m=2, u=2),
-                    in_=wt[:].rearrange("p m u o -> p m o u"),
+                rows = raws[g][:, :, 64:HW].rearrange("p t (k r) -> p t k r", r=192)
+                nc.vector.tensor_copy(
+                    out=ubt[:, 4 * g : 4 * g + 4, 0 : (k1_ - k0) * 64].rearrange("p t (k x) -> p t k x", x=64),
+                    in_=rows[:, :, k0:k1_, 0:64],
                 )
-                nc.vector.quantize_mx(
-                    out=w_codes[:, g, 256 * mp : 256 * (mp + 1)].bitcast(FP8X4),
-                    scales=w_scales[:, g, 256 * mp : 256 * (mp + 1)],
-                    in_=wg[:, g, :],
-                )
+            ubts[si] = ubt
 
-        gps_box = [None]
-        gs_box = [None]
+        chunk_no = [0]
 
-        def gram_window(wi, first, last):
-            if first:
-                gps_new = ps_g.tile([P, 3, 2, 2, TCW], F32, name="gps", tag="gps")
-                gps_box[0] = (gps_new, wi)
-            gps, wi0 = gps_box[0]
-            gs, gs0 = gs_box[0]
-            sl = wi - wi0
-            ts0 = 1 if wi == 0 else 0
-            t_row = 3 * (wi - 1) + 2
-            for k in range(2):
-                c0 = 2 if k == 0 else 0
-                x0 = 0 if k == 0 else 30
-                for s in range(8):
-                    img = raws[s // 4][:, s % 4, 0:HW].rearrange("p (y x) -> p y x", x=64)
-                    nc.tensor.matmul(
-                        gps[:, sl, k, ts0:2, c0 : c0 + 34],
-                        lhsT=sb[:, s, k, 2 * wi : 2 * wi + 4, :].rearrange("p i x -> p (i x)"),
-                        rhs=img[:, t_row + ts0 : t_row + 2, x0 : x0 + 34],
-                        start=(s == 0),
-                        stop=(s == 7),
+        def gram_fold(si):
+            w0, w1, m0, m1, blocks = STAGES[si]
+            nw = w1 - w0
+            sbt = sbts[si]
+            groups = [(sg, wi) for sg in range(3) for wi in range(w0, w1)]
+            nch = -(-len(groups) // NG)
+            per = -(-len(groups) // nch)
+            for c0 in range(0, len(groups), per):
+                grp = groups[c0 : c0 + per]
+                ng = len(grp)
+                gp = ps_g.tile([P, NG, 2, CP], F32, name="gp")
+                gm = gms[chunk_no[0] % 2]
+                chunk_no[0] += 1
+                for lo, (sg, wi) in enumerate(grp):
+                    t0 = 1 if wi == 0 else 0
+                    off = 3 * (wi - w0) * SW
+                    for s in range(8):
+                        img = raws[s // 4][:, s % 4, 0:HW].rearrange("p (y x) -> p y x", x=64)
+                        nc.tensor.matmul(
+                            gp[:, lo, t0:2, CLO[sg] : CHI[sg]],
+                            lhsT=sbt[:, s, sg, off : off + P],
+                            rhs=img[:, 3 * wi - 1 + t0 : 3 * wi + 1, X0[sg] + CLO[sg] : X0[sg] + CHI[sg]],
+                            start=(s == 0),
+                            stop=(s == 7),
+                        )
+                parts = []
+                for sg in range(3):
+                    los = [lo for lo, (a, b) in enumerate(grp) if a == sg]
+                    if los:
+                        parts.append((sg, los[0], los[-1] + 1, grp[los[0]][1]))
+                for sg, la, lb, wa in parts:
+                    cs = slice(CLO[sg], CHI[sg])
+                    ln = CHI[sg] - CLO[sg]
+                    if wa == 0:
+                        nc.vector.tensor_tensor(out=gm[:, la, 1, cs], in0=gp[:, la, 1, cs], in1=mask[:, 1, cs], op=ALU.mult)
+                        la += 1
+                    nc.vector.tensor_tensor(
+                        out=gm[:, la:lb, :, cs], in0=gp[:, la:lb, :, cs],
+                        in1=mask[:, :, cs].unsqueeze(1).to_broadcast([P, lb - la, 2, ln]), op=ALU.mult,
                     )
-            if last:
-                for k in range(2):
-                    c0 = 2 if k == 0 else 0
-                    lo = 0
-                    if wi0 == 0:
-                        nc.scalar.copy(out=gs[:, 0, k, 1:2, c0 : c0 + 34], in_=gps[:, 0, k, 1:2, c0 : c0 + 34])
-                        lo = 1
-                    nc.scalar.copy(out=gs[:, wi0 - gs0 + lo : wi - gs0 + 1, k, :, c0 : c0 + 34], in_=gps[:, lo : sl + 1, k, :, c0 : c0 + 34])
+                vp = ps_v.tile([P, NG, 2, CP], F32, name="vp", tag="vp")
+                gmv = gm[:, 0:ng].rearrange("p g t c -> p (g t) c")
+                vpv = vp[:, 0:ng].rearrange("p g t c -> p (g t) c")
+                for b in range(5):
+                    nc.tensor.matmul(vpv[:, :, b:CP:5], lhsT=fall[:, b, :], rhs=gmv[:, :, b:CP:5], start=True, stop=True)
+                for sg, la, lb, wa in parts:
+                    cs = slice(CLO[sg], CHI[sg])
+                    nc.scalar.copy(
+                        out=vraw[0:101, 2 * wa : 2 * (wa + lb - la), X0[sg] + CLO[sg] : X0[sg] + CHI[sg]],
+                        in_=vp[0:101, la:lb, :, cs].rearrange("p g t c -> p (g t) c"),
+                    )
 
-        def lane_tile(m):
-            b = 192 * m if m < 21 else 3968
-            xs = []
-            for d in range(3):
-                pool = ps_x0 if d == 0 else ps_x
-                xt = pool.tile([P, 1024], BF16, name="x%d" % d)
-                for s in range(8):
-                    nc.tensor.transpose(xt[:, P * s : P * (s + 1)], raws[s // 4][:, s % 4, b + d : b + d + P], ident_b[:])
-                xs.append(xt)
-            x0s = lan2.tile([P, 1024], BF16, name="x0s")
-            nc.scalar.copy(out=x0s[:], in_=xs[0][:])
-            js = lan.tile([P, 1024], BF16, name="js")
-            nc.scalar.activation(out=js[:], in_=xs[0][:], func=ACT.Square, accum_out=ti[:, m : m + 1])
-            for d in (1, 2):
-                jv = lan.tile([P, 1024], F32, name="jv")
-                nc.vector.scalar_tensor_tensor(
-                    out=jv[:], in0=xs[d][:], scalar=1.0, in1=x0s[:], op0=ALU.mult, op1=ALU.mult,
-                    accum_out=ti[:, 32 * d + m : 32 * d + m + 1],
+        tiss = {}
+
+        def lanes(si):
+            w0, w1, m0, m1, blocks = STAGES[si]
+            ubt = ubts[si]
+            tis = lan2.tile([P, 3, P], F32, name="tis")
+            nc.gpsimd.memset(tis[:], 0.0)
+            for ml in range(m1 - m0):
+                xs = []
+                for d in range(3):
+                    xt = ps_x.tile([P, 1024], BF16, name="x%d" % d)
+                    for s in range(8):
+                        nc.tensor.transpose(xt[:, P * s : P * (s + 1)], ubt[:, s, P * ml + d : P * ml + d + P], ident_b[:])
+                    xs.append(xt)
+                x0s = lan2.tile([P, 1024], BF16, name="x0s")
+                nc.scalar.copy(out=x0s[:], in_=xs[0][:])
+                js = lan.tile([P, 1024], BF16, name="js")
+                nc.scalar.activation(out=js[:], in_=xs[0][:], func=ACT.Square, accum_out=tis[:, 0, ml : ml + 1])
+                for d in (1, 2):
+                    jv = lan.tile([P, 1024], F32, name="jv")
+                    nc.vector.scalar_tensor_tensor(
+                        out=jv[:], in0=xs[d][:], scalar=1.0, in1=x0s[:], op0=ALU.mult, op1=ALU.mult,
+                        accum_out=tis[:, d, ml : ml + 1],
+                    )
+            tiss[si] = tis
+
+        def rows3(base, n, lead, pitch):
+            v = flat[base : base + lead * pitch].rearrange("(v c) -> v c", c=pitch)
+            return v[:, 0 : n * 3 * RP].rearrange("v (w c) -> v w c", c=3 * RP)[:, :, 0:64]
+
+        def writes(si):
+            w0, w1, m0, m1, blocks = STAGES[si]
+            nm = m1 - m0
+            wa = max(w0, 1)
+            rt = chain.tile([P, NWMAX, 64], F32, name="rt")
+            for pp, tt, wf in ((32, 0, wa), (96, 1, w0)):
+                n = w1 - wf
+                r = rt[pp : pp + 5, 0:n, :]
+                nc.scalar.activation(out=r, in_=vraw[pp : pp + 5, 2 * wf + tt : 2 * w1 : 2, :], func=ACT.Sqrt)
+                nc.vector.tensor_scalar_max(out=r, in0=r, scalar1=EPS)
+                nc.vector.reciprocal(out=r, in_=r)
+                nc.sync.dma_start(
+                    out=rows3(RIB + (3 * wf - 1 + tt + 4) * RP + LP, n, 5, IMG - RP),
+                    in_=r,
+                )
+            lt = ps_v.tile([P, 3, P], F32, name="lt", tag="vp")
+            for ty in range(3):
+                nc.tensor.transpose(lt[:, ty, :], tiss[si][:, ty, :], ident_f[:])
+            lts = chain.tile([P, 3, P], F32, name="lts")
+            nc.scalar.copy(out=lts[0:nm], in_=lt[0:nm])
+            ru = chain.tile([P, P], F32, name="ru")
+            nc.scalar.activation(out=ru[0:nm], in_=lts[0:nm, 0, :], func=ACT.Sqrt)
+            nc.vector.tensor_scalar_max(out=ru[0:nm], in0=ru[0:nm], scalar1=EPS)
+            nc.vector.reciprocal(out=ru[0:nm], in_=ru[0:nm])
+            for yy in range(2):
+                n = nm if 6 * (m1 - 1) + 3 * yy + 1 < 64 else nm - 1
+                b0 = RIB + (6 * m0 + 3 * yy + 1 + 4) * RP + LP
+                v = flat[b0 : b0 + 5 * (IMG - RP)].rearrange("(d c) -> d c", c=IMG - RP)
+                v = v[:, 0 : n * 6 * RP].rearrange("d (m c) -> m d c", c=6 * RP)[:, :, 0:64]
+                nc.sync.dma_start(out=v, in_=ru[0:n, 64 * yy : 64 * yy + 64].unsqueeze(1).to_broadcast([n, 5, 64]))
+            for ty, e, sh in ((0, 2, 0), (1, 3, 0), (1, 1, 1), (2, 4, 0), (2, 0, 2)):
+                b0 = VRB + (5 * e + 2) * IMG + (6 * m0 + 1 + 2) * RP + LP + sh
+                v = flat[b0 : b0 + nm * 6 * RP].rearrange("(m y c) -> m y c", y=2, c=3 * RP)[:, :, 0:64]
+                nc.sync.dma_start(out=v, in_=lts[0:nm, ty, :].rearrange("m (y x) -> m y x", x=64))
+            nc.sync.dma_start(out=rows3(VRB + (3 * w0 + 2) * RP + LP, w1 - w0, 32, IMG), in_=vraw[0:32, 2 * w0 + 1 : 2 * w1 : 2, :])
+            nc.sync.dma_start(out=rows3(VRB + IMG + (3 * wa - 1 + 2) * RP + LP, w1 - wa, 32, IMG), in_=vraw[0:32, 2 * wa : 2 * w1 : 2, :])
+            for tt, s, dyt, sh, wf, wl in (
+                (1, 0, 4, -2, w0, w1), (1, 3, 1, 1, w0, w1), (1, 4, 0, 2, max(w0 - 1, 0), w1 - 1), (0, 0, 3, -1, wa, w1), (0, 3, 0, 2, wa, w1),
+            ):
+                yt = 3 * wf - 1 + tt + sh
+                nc.sync.dma_start(
+                    out=rows3(VRB + dyt * IMG + (yt + 2) * RP + LP + 2, wl - wf, 5, 5 * IMG - 1),
+                    in_=vraw[64 + s : 64 + s + 21 : 5, 2 * wf + tt : 2 * wl : 2, :],
                 )
 
-        def chain(ylo, yhi, i0, i1):
-            nc.sync.dma_start(
-                out=flat[S1B : S1B + P * PN].rearrange("(i c) -> i c", c=PN)[:, i0 * WPITCH : i1 * WPITCH],
-                in_=gs_box[0][0][:, 0 : i1 - i0].rearrange("p a k b c -> p (a k b c)"),
-            )
-            for rho, ts, dy in COMBOS:
-                ws = [w for w in range(i0 - 1, i1 - 1) if 0 <= 3 * w + ROW_OFF[rho] <= 63 and 0 <= 3 * w + 2 + ts <= 63]
-                w0 = ws[0]
-                nw = len(ws)
-                r0 = 3 * w0 + ROW_OFF[rho]
-                for k in range(2):
-                    base = S1B + 32 * rho * PN + (w0 + 1) * WPITCH + k * 2 * TCW + ts * TCW
-                    src = flat[base : base + 32 * (PN + 1)].rearrange("(x c) -> x c", c=PN + 1)
-                    src = src[:, 0 : nw * WPITCH].rearrange("x (w c) -> w x c", c=WPITCH)[:, :, 0:5]
-                    nc.sync.dma_start(out=gi[r0 : r0 + 3 * (nw - 1) + 1 : 3, dy + 2, 32 * k : 32 * k + 32, :], in_=src)
-            lt = ps_g.tile([P, P], F32, name="lt", tag="gps")
-            nc.tensor.transpose(lt[:], ti[:], ident_f[:])
-            lts = stage.tile([P, P], F32, name="lts")
-            nc.scalar.copy(out=lts[:], in_=lt[:])
-            m1 = min(i1, 21)
-            for s in range(3):
-                for yy in range(2):
-                    nc.sync.dma_start(
-                        out=gm[3 * i0 + yy : 3 * (m1 - 1) + yy + 1 : 3, 2, 2 + s, :],
-                        in_=lts[32 * s + i0 : 32 * s + m1, 64 * yy : 64 * yy + 64],
-                    )
-                if i1 == 22:
-                    nc.sync.dma_start(out=gm[63:64, 2, 2 + s, :], in_=lts[32 * s + 21 : 32 * s + 22, 64:128])
-            nc.vector.memset(gq[:, :, 0:2, 0:2], 0.0)
-            nc.vector.memset(gq[:, :, 3:5, 62:64], 0.0)
-            for em in range(5):
-                sh = em - 2
-                xlo = max(0, -sh)
-                xhi = min(64, 64 - sh)
-                nc.vector.tensor_copy(out=gq[:, :, em, xlo:xhi], in_=gi[:, :, xlo + sh : xhi + sh, 4 - em])
-            for dym in (-2, -1, 1, 2):
-                y0 = max(ylo, -dym)
-                y1 = min(yhi, 64 - dym)
-                nc.sync.dma_start(out=gm[y0:y1, dym + 2, :, :], in_=gq[y0 + dym : y1 + dym, 2 - dym, :, :])
-            ga = gq
-            nc.vector.tensor_tensor(out=ga[:], in0=gi[:].rearrange("p d x e -> p d e x"), in1=gm[:], op=ALU.add)
-            nc.vector.memset(ga[:, 2, 3, 63:64], 0.0)
-            nc.vector.memset(ga[:, 2, 4, 62:64], 0.0)
-            nc.vector.tensor_copy(out=ga[:, 2, 1, 1:64], in_=ga[:, 2, 3, 0:63])
-            nc.vector.tensor_copy(out=ga[:, 2, 0, 2:64], in_=ga[:, 2, 4, 0:62])
-            nc.vector.tensor_scalar_max(out=n2[:], in0=ga[:, 2, 2, :], scalar1=EPS2)
-            nc.scalar.activation(out=nrm[:], in_=n2[:], func=ACT.Sqrt)
-            nc.vector.reciprocal(out=rin[:, 2:66], in_=nrm[:])
-            for dy in (-2, -1, 1, 2):
-                y0 = max(ylo, -dy)
-                y1 = min(yhi, 64 - dy)
-                nc.sync.dma_start(out=r5[y0:y1, dy + 2, 0:68], in_=rin[y0 + dy : y1 + dy, :])
-            nc.vector.tensor_copy(out=r5[:, 2, 0:68], in_=rin[:])
-            ga25 = ga[:].rearrange("p d e x -> p (d e) x")
-            nc.vector.tensor_tensor(out=ga25, in0=ga25, in1=rin[:, 2:66].unsqueeze(1).to_broadcast([64, 25, 64]), op=ALU.mult)
+        def back(si):
+            w0, w1, m0, m1, blocks = STAGES[si]
+            y0 = 8 * blocks[0]
+            nr = 8 * len(blocks)
+            r2 = chain.tile([32, NRMAX, 64], F32, name="r2")
             for e in range(5):
-                nc.vector.tensor_tensor(out=vv[:, e, :, :], in0=ga[:, :, e, :], in1=r5[:, :, e : e + 64], op=ALU.mult)
-            nc.sync.dma_start(
-                out=flat[VPB : VPB + 25 * HW].rearrange("(j y x) -> y j x", j=25, x=64)[ylo:yhi],
-                in_=vv[ylo:yhi].rearrange("p e d x -> p (e d) x"),
+                b0 = RIB + (y0 + 2) * RP + LP + e - 2
+                v = flat[b0 : b0 + 5 * IMG].rearrange("(d c) -> d c", c=IMG)[:, 0 : nr * RP].rearrange("d (r c) -> d r c", c=RP)[:, :, 0:64]
+                nc.sync.dma_start(out=r2[5 * e : 5 * e + 5, 0:nr, :], in_=v)
+            rb = chain.tile([32, NRMAX * RP], F32, name="rb")
+            b0 = RIB + 2 * IMG + (y0 + 2) * RP
+            nc.sync.dma_start(out=rb[:, 0 : nr * RP], in_=flat[b0 : b0 + nr * RP].partition_broadcast(32))
+            vf = chain.tile([32, NRMAX, 64], F32, name="vf")
+            b0 = VRB + (y0 + 2) * RP + LP
+            v = flat[b0 : b0 + 32 * IMG].rearrange("(v c) -> v c", c=IMG)[:, 0 : nr * RP].rearrange("v (r c) -> v r c", c=RP)[:, :, 0:64]
+            nc.sync.dma_start(out=vf[:, 0:nr, :], in_=v)
+            nc.vector.tensor_tensor(out=vf[0:25, 0:nr, :], in0=vf[0:25, 0:nr, :], in1=r2[0:25, 0:nr, :], op=ALU.mult)
+            vb = chain.tile([32, NRMAX, 64], BF16, name="vb")
+            nc.vector.tensor_tensor(
+                out=vb[0:25, 0:nr, :], in0=vf[0:25, 0:nr, :],
+                in1=rb[0:25, 0 : nr * RP].rearrange("p (r c) -> p r c", c=RP)[:, :, LP : LP + 64], op=ALU.mult,
             )
-            vp24 = flat[VPB + HW : VPB + 25 * HW].rearrange("(q t w) -> q t w", q=8, t=3)
-            vp0 = flat[VPB : VPB + HW].rearrange("(o w) -> o w", o=1)
-            for n in range(ylo // 8, yhi // 8):
-                cols = slice(n * NB, (n + 1) * NB)
-                vt = stage.tile([8, 4, NB], F32, name="vt")
-                nc.sync.dma_start(out=vt[0:8, 1:4, :], in_=vp24[:, :, cols])
-                nc.sync.dma_start(out=vt[0:1, 0, :], in_=vp0[:, cols])
-                nc.vector.tensor_copy(out=raw1[0:8, 1:4, cols], in_=vt[0:8, 1:4, :])
-                nc.scalar.copy(out=raw1[0:1, 0, cols], in_=vt[0:1, 0, :])
+            cols = slice(y0 * 64, (y0 + nr) * 64)
+            vbf = vb[:, 0:nr, :].rearrange("p r x -> p (r x)")
+            nc.sync.dma_start(out=raw1[0:1, 0, cols], in_=vbf[0:1, :])
+            for t in range(1, 4):
+                nc.sync.dma_start(out=raw1[0:8, t, cols], in_=vbf[t : t + 22 : 3, :])
 
-        held = keep.tile([P, 6, NB], F32, name="held")
+        def weights():
+            wv = conv_w.rearrange("(m p) k -> p m k", p=P)
+            nc.sync.dma_start(out=b_in[0:8, :], in_=conv_b.rearrange("(m p) -> m p", p=P))
+            b_ps = ps_v.tile([P, P], BF16, name="b_ps", tag="vp")
+            nc.tensor.transpose(b_ps[:], b_in[:], ident_b[:])
+            nc.vector.tensor_copy(out=bias[:], in_=b_ps[:, 0:8])
+            for mp in range(4):
+                w_sb = stage.tile([P, 2, OC], BF16, name="w_sb", tag="grouped", align_bytes=64)
+                w_tail = stage.tile([P, 2, 32], BF16, name="w_tail")
+                ms = slice(2 * mp, 2 * mp + 2)
+                nc.sync.dma_start(out=w_sb[:, :, 0:512], in_=wv[:, ms, 0:512])
+                nc.sync.dma_start(out=w_sb[:, :, 544:1024], in_=wv[:, ms, 512:992])
+                nc.sync.dma_start(out=w_tail[:], in_=wv[:, ms, 992:1024])
+                oct_w = w_sb[:, :, 512:544].rearrange("p m (q t) -> p m q t", t=4)
+                nc.vector.tensor_copy(out=oct_w[:, :, :, 1:4], in_=w_tail[:, :, 8:32].rearrange("p m (q t) -> p m q t", t=3))
+                nc.vector.tensor_copy(out=oct_w[:, :, 1:8, 0], in_=w_tail[:, :, 0:7])
+                nc.vector.tensor_copy(out=oct_w[:, :, 0:1, 0], in_=w_tail[:, :, 7:8])
+                w32 = w_sb[:].rearrange("p m k -> p (m k)").bitcast(F32).rearrange("p (m k) -> p m k", m=2)
+                wg = stage.tile([P, 2, 1024], BF16, name="wg", tag="grouped", align_bytes=64)
+                for g in range(2):
+                    wt = ps_acc.tile([P, 2, 2, P], F32, name="wt", tag="acc")
+                    for m2 in range(2):
+                        for u in range(2):
+                            nc.tensor.transpose(wt[:, m2, u, :], w32[:, m2, 256 * g + u : 256 * (g + 1) : 2], ident_f[:])
+                    nc.scalar.copy(
+                        out=wg[:, g, :].bitcast(F32).rearrange("p (m o u) -> p m o u", m=2, u=2),
+                        in_=wt[:].rearrange("p m u o -> p m o u"),
+                    )
+                    nc.vector.quantize_mx(
+                        out=w_codes[:, g, 256 * mp : 256 * (mp + 1)].bitcast(FP8X4),
+                        scales=w_scales[:, g, 256 * mp : 256 * (mp + 1)],
+                        in_=wg[:, g, :],
+                    )
 
         def conv_block(n, hold_last):
             cols = slice(n * NB, (n + 1) * NB)
@@ -298,28 +408,20 @@ def tile_spatialcontext_kernel(tc, feature, conv_w, conv_b, out):
                     nc.scalar.activation(out=ot[:], in_=acc[:], func=ACT.Relu, bias=bias[:, m : m + 1], scale=1.0)
                     nc.scalar.dma_start(out=out2[m * P : (m + 1) * P, cols], in_=ot[:])
 
-        def steps(i0, i1, blocks):
-            gs_new = lan.tile([P, 9, 2, 2, TCW], F32, name="gs")
-            nc.gpsimd.memset(gs_new[:], 0.0)
-            gs_box[0] = (gs_new, i0)
-            done = 0
-            for i in range(i0, i1):
-                gram_window(i, (i - i0) % 3 == 0, (i - i0) % 3 == 2 or i == i1 - 1)
-                lane_tile(i)
-                if done < len(blocks) and (i - i0) % 3 == 2:
-                    conv_block(blocks[done], True)
-                    done += 1
-            for n in blocks[done:]:
-                conv_block(n, True)
+        def front(si):
+            prep(si)
+            gram_fold(si)
+            lanes(si)
+            writes(si)
 
-        steps(0, 9, [])
-        chain(*STAGES[0])
-        steps(9, 17, [])
-        chain(*STAGES[1])
-        steps(17, 22, [0, 1])
-        chain(*STAGES[2])
-        for n in range(2, 6):
-            conv_block(n, True)
-        nc.scalar.dma_start(out=out2[7 * P : 8 * P, 0 : 6 * NB], in_=held[:].rearrange("p n w -> p (n w)"))
-        conv_block(6, False)
-        conv_block(7, False)
+        ns = len(STAGES)
+        front(0)
+        weights()
+        for si in range(ns):
+            if si + 1 < ns:
+                front(si + 1)
+            back(si)
+            if si == ns - 1:
+                nc.scalar.dma_start(out=out2[7 * P : 8 * P, 0 : 6 * NB], in_=held[:].rearrange("p n w -> p (n w)"))
+            for n in STAGES[si][4]:
+                conv_block(n, si < ns - 1)

@@ -42,6 +42,8 @@ STAGES = ((0, 4, 0, 2, (0,)), (4, 7, 2, 3, (1,)), (7, 12, 3, 6, (2, 3)), (12, 17
 NWMAX = 5
 NMMAX = 3
 NRMAX = 16
+AHEAD = 2
+NOUT = 10
 
 
 def tile_spatialcontext_kernel(tc, feature, conv_w, conv_b, out):
@@ -55,12 +57,13 @@ def tile_spatialcontext_kernel(tc, feature, conv_w, conv_b, out):
         stage = ctx.enter_context(tc.tile_pool(name="stage", bufs=2))
         patch = ctx.enter_context(tc.tile_pool(name="patch", bufs=2))
         chain = ctx.enter_context(tc.tile_pool(name="chain", bufs=2))
+        chain1 = ctx.enter_context(tc.tile_pool(name="chain1", bufs=1))
         codes = ctx.enter_context(tc.tile_pool(name="codes", bufs=2))
-        outs = ctx.enter_context(tc.tile_pool(name="outs", bufs=4))
+        outs = ctx.enter_context(tc.tile_pool(name="outs", bufs=NOUT))
         lan = ctx.enter_context(tc.tile_pool(name="lan", bufs=1))
         lan2 = ctx.enter_context(tc.tile_pool(name="lan2", bufs=2))
-        ps_acc = ctx.enter_context(tc.psum_pool(name="ps_acc", bufs=2))
-        ps_g = ctx.enter_context(tc.psum_pool(name="ps_g", bufs=2))
+        ps_acc = ctx.enter_context(tc.psum_pool(name="ps_acc", bufs=3))
+        ps_g = ctx.enter_context(tc.psum_pool(name="ps_g", bufs=1))
         ps_v = ctx.enter_context(tc.psum_pool(name="ps_v", bufs=1))
         ps_x = ctx.enter_context(tc.psum_pool(name="ps_x", bufs=1))
 
@@ -82,7 +85,6 @@ def tile_spatialcontext_kernel(tc, feature, conv_w, conv_b, out):
         bias = keep.tile([P, 8], F32, name="bias")
         b_in = keep.tile([P, P], BF16, name="b_in")
 
-        nc.vector.memset(raw1[0:8].rearrange("p j w -> p (j w)").bitcast(I32), 0)
         heldf = held[:].rearrange("p n w -> p (n w)")
         nc.gpsimd.memset(heldf[:, 0:ZW], 0.0)
         nc.gpsimd.memset(gm0[:], 0.0)
@@ -91,6 +93,7 @@ def tile_spatialcontext_kernel(tc, feature, conv_w, conv_b, out):
 
         def load(c):
             cols = slice(LOAD_ROWS[c] * 64, LOAD_ROWS[c + 1] * 64)
+            nc.vector.memset(raw1[0:8, :, cols].bitcast(I32), 0)
             nc.sync.dma_start(out=raw0[:, :, cols], in_=feat[0:512, cols].rearrange("(p j) w -> p j w", j=4))
             nc.sync.dma_start(out=raw1[8:128, :, cols], in_=feat[512:992, cols].rearrange("(p j) w -> p j w", j=4))
             nc.sync.dma_start(out=raw1[1:8, 0, cols], in_=feat[992:999, cols])
@@ -317,20 +320,20 @@ def tile_spatialcontext_kernel(tc, feature, conv_w, conv_b, out):
             w0, w1, m0, m1, blocks = STAGES[si]
             y0 = 8 * blocks[0]
             nr = 8 * len(blocks)
-            r2 = chain.tile([32, NRMAX, 64], F32, name="r2")
+            r2 = chain1.tile([32, NRMAX, 64], F32, name="r2")
             for e in range(5):
                 b0 = RIB + (y0 + 2) * RP + LP + e - 2
                 v = flat[b0 : b0 + 5 * IMG].rearrange("(d c) -> d c", c=IMG)[:, 0 : nr * RP].rearrange("d (r c) -> d r c", c=RP)[:, :, 0:64]
                 nc.sync.dma_start(out=r2[5 * e : 5 * e + 5, 0:nr, :], in_=v)
-            rb = chain.tile([32, NRMAX * RP], F32, name="rb")
+            rb = chain1.tile([32, NRMAX * RP], F32, name="rb")
             b0 = RIB + 2 * IMG + (y0 + 2) * RP
             nc.sync.dma_start(out=rb[:, 0 : nr * RP], in_=flat[b0 : b0 + nr * RP].partition_broadcast(32))
-            vf = chain.tile([32, NRMAX, 64], F32, name="vf")
+            vf = chain1.tile([32, NRMAX, 64], F32, name="vf")
             b0 = VRB + (y0 + 2) * RP + LP
             v = flat[b0 : b0 + 32 * IMG].rearrange("(v c) -> v c", c=IMG)[:, 0 : nr * RP].rearrange("v (r c) -> v r c", c=RP)[:, :, 0:64]
             nc.sync.dma_start(out=vf[:, 0:nr, :], in_=v)
             nc.vector.tensor_tensor(out=vf[0:25, 0:nr, :], in0=vf[0:25, 0:nr, :], in1=r2[0:25, 0:nr, :], op=ALU.mult)
-            vb = chain.tile([32, NRMAX, 64], BF16, name="vb")
+            vb = chain1.tile([32, NRMAX, 64], BF16, name="vb")
             nc.vector.tensor_tensor(
                 out=vb[0:25, 0:nr, :], in0=vf[0:25, 0:nr, :],
                 in1=rb[0:25, 0 : nr * RP].rearrange("p (r c) -> p r c", c=RP)[:, :, LP : LP + 64], op=ALU.mult,
@@ -417,9 +420,11 @@ def tile_spatialcontext_kernel(tc, feature, conv_w, conv_b, out):
         ns = len(STAGES)
         front(0)
         weights()
+        for si in range(1, min(AHEAD, ns)):
+            front(si)
         for si in range(ns):
-            if si + 1 < ns:
-                front(si + 1)
+            if si + AHEAD < ns:
+                front(si + AHEAD)
             back(si)
             if si == ns - 1:
                 nc.scalar.dma_start(out=out2[7 * P : 8 * P, 0 : 6 * NB], in_=held[:].rearrange("p n w -> p (n w)"))

@@ -384,11 +384,12 @@ def tile_spatialcontext_kernel(tc, feature, conv_w, conv_b, out):
             x_scales = codes.tile([P, 2, NB], U8, name="x_scales", align_bytes=64)
             for g in range(2):
                 grouped = stage.tile([P, NB, 4], BF16, name="grouped", tag="grouped", align_bytes=64)
-                view = raws[g][:, :, cols].rearrange("p j w -> p w j")
+                view = raws[g][:, :, cols].rearrange("p j (c i) -> p c j i", i=4)
+                gview = grouped[:].rearrange("p (c i) j -> p c j i", i=4)
                 if g == 0:
-                    nc.scalar.copy(out=grouped[:], in_=view)
+                    nc.scalar.copy(out=gview, in_=view)
                 else:
-                    nc.vector.tensor_copy(out=grouped[:], in_=view)
+                    nc.vector.tensor_copy(out=gview, in_=view)
                 nc.vector.quantize_mx(
                     out=x_codes[:, g, :].bitcast(FP8X4), scales=x_scales[:, g, :], in_=grouped[:].rearrange("p w j -> p (w j)")
                 )

@@ -34,8 +34,8 @@ LP = 8
 IMG = 68 * RP
 S0 = 896 * HW
 RIB = S0
-VRB = S0 + 5 * IMG
-ZW = 1616
+VRB = S0 + 8 * IMG
+ZW = 1744
 
 LOAD_ROWS = (0, 12, 22, 36, 53, 64)
 STAGES = ((0, 4, 0, 2, (0,)), (4, 7, 2, 3, (1,)), (7, 12, 3, 6, (2, 3)), (12, 17, 6, 9, (4, 5)), (17, 22, 9, 11, (6, 7)))
@@ -117,8 +117,8 @@ def tile_spatialcontext_kernel(tc, feature, conv_w, conv_b, out):
         nc.gpsimd.memset(j1[:], -1.0)
         nc.gpsimd.iota(j1[:, 0:25], pattern=[[1, 25]], base=0, channel_multiplier=0, allow_small_or_imprecise_dtypes=True)
         nc.gpsimd.iota(j1[:, 64:89], pattern=[[-5, 5], [1, 5]], base=20, channel_multiplier=0, allow_small_or_imprecise_dtypes=True)
-        nc.gpsimd.memset(j1[:, 32:37], 11.0)
-        nc.gpsimd.memset(j1[:, 96:101], 12.0)
+        nc.gpsimd.memset(j1[:, 32:40], 11.0)
+        nc.gpsimd.memset(j1[:, 96:104], 12.0)
 
         ge = keep.tile([P, 5], F32, name="ge")
         nc.vector.tensor_scalar(out=ge[:], in0=t24[:], scalar1=iop[:, 0:1], scalar2=None, op0=ALU.is_le)
@@ -237,8 +237,8 @@ def tile_spatialcontext_kernel(tc, feature, conv_w, conv_b, out):
                 for sg, la, lb, wa in parts:
                     cs = slice(CLO[sg], CHI[sg])
                     nc.scalar.copy(
-                        out=vraw[0:101, 2 * wa : 2 * (wa + lb - la), X0[sg] + CLO[sg] : X0[sg] + CHI[sg]],
-                        in_=vp[0:101, la:lb, :, cs].rearrange("p g t c -> p (g t) c"),
+                        out=vraw[0:104, 2 * wa : 2 * (wa + lb - la), X0[sg] + CLO[sg] : X0[sg] + CHI[sg]],
+                        in_=vp[0:104, la:lb, :, cs].rearrange("p g t c -> p (g t) c"),
                     )
 
         tiss = {}
@@ -278,12 +278,12 @@ def tile_spatialcontext_kernel(tc, feature, conv_w, conv_b, out):
             rt = chain.tile([P, NWMAX, 64], F32, name="rt")
             for pp, tt, wf in ((32, 0, wa), (96, 1, w0)):
                 n = w1 - wf
-                r = rt[pp : pp + 5, 0:n, :]
-                nc.scalar.activation(out=r, in_=vraw[pp : pp + 5, 2 * wf + tt : 2 * w1 : 2, :], func=ACT.Sqrt)
+                r = rt[pp : pp + 8, 0:n, :]
+                nc.scalar.activation(out=r, in_=vraw[pp : pp + 8, 2 * wf + tt : 2 * w1 : 2, :], func=ACT.Sqrt)
                 nc.vector.tensor_scalar_max(out=r, in0=r, scalar1=EPS)
                 nc.vector.reciprocal(out=r, in_=r)
                 nc.sync.dma_start(
-                    out=rows3(RIB + (3 * wf - 1 + tt + 4) * RP + LP, n, 5, IMG - RP),
+                    out=rows3(RIB + (3 * wf - 1 + tt + 4) * RP + LP, n, 8, IMG - RP),
                     in_=r,
                 )
             lt = ps_v.tile([P, 3, P], F32, name="lt", tag="vp")
@@ -312,8 +312,8 @@ def tile_spatialcontext_kernel(tc, feature, conv_w, conv_b, out):
             ):
                 yt = 3 * wf - 1 + tt + sh
                 nc.sync.dma_start(
-                    out=rows3(VRB + dyt * IMG + (yt + 2) * RP + LP + 2, wl - wf, 5, 5 * IMG - 1),
-                    in_=vraw[64 + s : 64 + s + 21 : 5, 2 * wf + tt : 2 * wl : 2, :],
+                    out=rows3(VRB + dyt * IMG + (yt + 2) * RP + LP + 2, wl - wf, 8, 5 * IMG - 1),
+                    in_=vraw[64 + s : 64 + s + 36 : 5, 2 * wf + tt : 2 * wl : 2, :],
                 )
 
         def back(si):

@@ -170,7 +170,8 @@ def tile_spatialcontext_kernel(tc, feature, conv_w, conv_b, out):
             for g in range(2):
                 img = raws[g][:, :, 0:HW].rearrange("p t (y x) -> p t y x", x=64)
                 for sg in range(3):
-                    nc.vector.tensor_copy(
+                    copy = nc.scalar.copy if (g, sg) == (1, 2) else nc.vector.tensor_copy
+                    copy(
                         out=sbt[:, 4 * g : 4 * g + 4, sg, (ya - ylo) * SW : (yb - ylo) * SW].rearrange("p t (y x) -> p t y x", x=SW),
                         in_=img[:, :, ya:yb, X0[sg] : X0[sg] + SW],
                     )
@@ -181,7 +182,7 @@ def tile_spatialcontext_kernel(tc, feature, conv_w, conv_b, out):
             nc.vector.memset(ubt[:, :, (k1_ - k0) * 64 : (m1 - m0) * P + 8], 0.0)
             for g in range(2):
                 rows = raws[g][:, :, 64:HW].rearrange("p t (k r) -> p t k r", r=192)
-                nc.vector.tensor_copy(
+                nc.scalar.copy(
                     out=ubt[:, 4 * g : 4 * g + 4, 0 : (k1_ - k0) * 64].rearrange("p t (k x) -> p t k x", x=64),
                     in_=rows[:, :, k0:k1_, 0:64],
                 )

@@ -24,47 +24,54 @@ EPS = 1e-12
 
 SW = 24
 X0 = (0, 20, 40)
-CLO = (0, 2, 2)
-CHI = (22, 22, 24)
-CP = 25
-NG = 10
+XLO = (0, 22, 42)
+XHI = (22, 42, 64)
+NWIN = 22
+NLAN = 11
 
-RP = 80
-LP = 8
-IMG = 68 * RP
-S0 = 896 * HW
-RIB = S0
-VRB = S0 + 8 * IMG
-ZW = 1744
-
-LOAD_ROWS = (0, 12, 22, 36, 53, 64)
-STAGES = ((0, 4, 0, 2, (0,)), (4, 7, 2, 3, (1,)), (7, 12, 3, 6, (2, 3)), (12, 17, 6, 9, (4, 5)), (17, 22, 9, 11, (6, 7)))
-NWMAX = 5
+LOAD_ROWS = (0, 15, 21, 39, 54, 64)
+FIN = ((0, 4, (0,)), (4, 6, (1,)), (6, 12, (2, 3)), (12, 17, (4, 5)), (17, 22, (6, 7)))
+NWMAX = 6
 NMMAX = 3
-NRMAX = 16
-AHEAD = 2
-NOUT = 10
+NSMAX = 7
+NOUT = 8
+
+
+def stage_ranges():
+    res = []
+    w0 = 0
+    m0 = 0
+    k0 = 0
+    for f0, f1, blocks in FIN:
+        w1 = min(f1 + 1, NWIN)
+        m1 = -(-f1 // 2)
+        k1 = f1 - 1 if f1 < NWIN else 21
+        res.append((w0, w1, m0, m1, k0, k1))
+        w0 = w1
+        m0 = m1
+        k0 = k1
+    return res
 
 
 def tile_spatialcontext_kernel(tc, feature, conv_w, conv_b, out):
     nc = tc.nc
     feat = feature.rearrange("b c h w -> (b c) (h w)")
     out2 = out.rearrange("b o h w -> (b o) (h w)")
-    flat = out.rearrange("b o h w -> (b o h w)")
+    ranges = stage_ranges()
 
     with ExitStack() as ctx:
         keep = ctx.enter_context(tc.tile_pool(name="keep", bufs=1))
         stage = ctx.enter_context(tc.tile_pool(name="stage", bufs=2))
         patch = ctx.enter_context(tc.tile_pool(name="patch", bufs=2))
         chain = ctx.enter_context(tc.tile_pool(name="chain", bufs=2))
-        chain1 = ctx.enter_context(tc.tile_pool(name="chain1", bufs=1))
         codes = ctx.enter_context(tc.tile_pool(name="codes", bufs=2))
         outs = ctx.enter_context(tc.tile_pool(name="outs", bufs=NOUT))
         lan = ctx.enter_context(tc.tile_pool(name="lan", bufs=1))
         lan2 = ctx.enter_context(tc.tile_pool(name="lan2", bufs=2))
-        ps_acc = ctx.enter_context(tc.psum_pool(name="ps_acc", bufs=3))
+        ps_acc = ctx.enter_context(tc.psum_pool(name="ps_acc", bufs=2))
         ps_g = ctx.enter_context(tc.psum_pool(name="ps_g", bufs=1))
-        ps_v = ctx.enter_context(tc.psum_pool(name="ps_v", bufs=1))
+        ps_s = ctx.enter_context(tc.psum_pool(name="ps_s", bufs=1))
+        ps_f = ctx.enter_context(tc.psum_pool(name="ps_f", bufs=1))
         ps_x = ctx.enter_context(tc.psum_pool(name="ps_x", bufs=1))
 
         ident_f = keep.tile([P, P], F32, name="ident_f")
@@ -75,21 +82,19 @@ def tile_spatialcontext_kernel(tc, feature, conv_w, conv_b, out):
         raw0 = keep.tile([P, 4, HWP], BF16, name="raw0")
         raw1 = keep.tile([P, 4, HWP], BF16, name="raw1")
         raws = [raw0, raw1]
-        vraw = keep.tile([P, 44, 64], F32, name="vraw")
-        gm0 = keep.tile([P, NG, 2, CP], F32, name="gm0")
-        gm1 = keep.tile([P, NG, 2, CP], F32, name="gm1")
-        gms = [gm0, gm1]
-        held = keep.tile([P, 6, NB], F32, name="held")
         w_codes = keep.tile([P, 2, OC], U32, name="w_codes", align_bytes=64)
         w_scales = keep.tile([P, 2, OC], U8, name="w_scales", align_bytes=64)
         bias = keep.tile([P, 8], F32, name="bias")
         b_in = keep.tile([P, P], BF16, name="b_in")
+        usum = keep.tile([P, NWIN, 25], F32, name="usum")
+        nbt = keep.tile([P, NWIN + 3 * NLAN], F32, name="nbt")
+        ris = keep.tile([P, 5, 23, 3], F32, name="ris")
+        asm = keep.tile([P, NWIN + NLAN, P], BF16, name="asm")
+        lrow = keep.tile([32, 69 * 64], BF16, name="lrow")
 
-        heldf = held[:].rearrange("p n w -> p (n w)")
-        nc.gpsimd.memset(heldf[:, 0:ZW], 0.0)
-        nc.gpsimd.memset(gm0[:], 0.0)
-        nc.gpsimd.memset(gm1[:], 0.0)
         nc.gpsimd.memset(b_in[:], 0.0)
+        nc.gpsimd.memset(nbt[:], 0.0)
+        nc.gpsimd.memset(ris[:], 0.0)
 
         def load(c):
             cols = slice(LOAD_ROWS[c] * 64, LOAD_ROWS[c + 1] * 64)
@@ -98,67 +103,104 @@ def tile_spatialcontext_kernel(tc, feature, conv_w, conv_b, out):
             nc.sync.dma_start(out=raw1[8:128, :, cols], in_=feat[512:992, cols].rearrange("(p j) w -> p j w", j=4))
             nc.sync.dma_start(out=raw1[1:8, 0, cols], in_=feat[992:999, cols])
 
-        load(0)
-        nc.sync.dma_start(out=flat[S0 : S0 + P * ZW].rearrange("(p c) -> p c", c=ZW), in_=heldf[:, 0:ZW])
-        for c in range(1, 5):
+        for c in range(5):
             load(c)
 
-        iop = keep.tile([P, 1], F32, name="iop")
-        nc.gpsimd.iota(iop[:], pattern=[[0, 1]], base=0, channel_multiplier=1, allow_small_or_imprecise_dtypes=True)
-        t24 = keep.tile([P, 5], F32, name="t24")
-        nc.gpsimd.iota(t24[:], pattern=[[24, 5]], base=24, channel_multiplier=0, allow_small_or_imprecise_dtypes=True)
-        th = keep.tile([P, 5, 6], F32, name="th")
-        nc.gpsimd.iota(th[:], pattern=[[1, 5], [5, 6]], base=-2, channel_multiplier=0, allow_small_or_imprecise_dtypes=True)
-        brow = keep.tile([P, 5], F32, name="brow")
-        nc.gpsimd.iota(brow[:], pattern=[[-1, 5]], base=7, channel_multiplier=0, allow_small_or_imprecise_dtypes=True)
-        crow = keep.tile([P, CP], F32, name="crow")
-        nc.gpsimd.iota(crow[:], pattern=[[1, CP]], base=0, channel_multiplier=0, allow_small_or_imprecise_dtypes=True)
-        j1 = keep.tile([P, P], F32, name="j1")
-        nc.gpsimd.memset(j1[:], -1.0)
-        nc.gpsimd.iota(j1[:, 0:25], pattern=[[1, 25]], base=0, channel_multiplier=0, allow_small_or_imprecise_dtypes=True)
-        nc.gpsimd.iota(j1[:, 64:89], pattern=[[-5, 5], [1, 5]], base=20, channel_multiplier=0, allow_small_or_imprecise_dtypes=True)
-        nc.gpsimd.memset(j1[:, 32:40], 11.0)
-        nc.gpsimd.memset(j1[:, 96:104], 12.0)
+        def row_iota(name, n, pattern, base):
+            t = keep.tile([P, n], F32, name=name)
+            nc.gpsimd.iota(t[:], pattern=pattern, base=base, channel_multiplier=0, allow_small_or_imprecise_dtypes=True)
+            return t
 
-        ge = keep.tile([P, 5], F32, name="ge")
-        nc.vector.tensor_scalar(out=ge[:], in0=t24[:], scalar1=iop[:, 0:1], scalar2=None, op0=ALU.is_le)
-        s5 = keep.tile([P, 1], F32, name="s5")
-        nc.vector.tensor_reduce(out=s5[:], in_=ge[:], axis=AX.X, op=ALU.add)
-        ii = keep.tile([P, 1], F32, name="ii")
-        nc.vector.scalar_tensor_tensor(out=ii[:], in0=s5[:], scalar=-24.0, in1=iop[:], op0=ALU.mult, op1=ALU.add)
-        ge2 = keep.tile([P, 5, 6], F32, name="ge2")
-        nc.vector.tensor_scalar(out=ge2[:], in0=th[:], scalar1=ii[:, 0:1], scalar2=None, op0=ALU.is_le)
-        cnt = keep.tile([P, 5], F32, name="cnt")
-        nc.vector.tensor_reduce(out=cnt[:], in_=ge2[:], axis=AX.X, op=ALU.add)
-        tmp = keep.tile([P, 5], F32, name="tmp")
-        nc.vector.tensor_scalar(out=tmp[:], in0=brow[:], scalar1=ii[:, 0:1], scalar2=None, op0=ALU.add)
-        ee = keep.tile([P, 5], F32, name="ee")
-        nc.vector.scalar_tensor_tensor(out=ee[:], in0=cnt[:], scalar=-5.0, in1=tmp[:], op0=ALU.mult, op1=ALU.add)
-        pen = keep.tile([P, 1], F32, name="pen")
+        def col(name, n=1):
+            return keep.tile([P, n], F32, name=name)
+
+        iop = col("iop")
+        nc.gpsimd.iota(iop[:], pattern=[[0, 1]], base=0, channel_multiplier=1, allow_small_or_imprecise_dtypes=True)
+        t24 = row_iota("t24", 5, [[24, 5]], 24)
+        t5 = row_iota("t5", 13, [[5, 13]], 5)
+        r5 = row_iota("r5", 5, [[1, 5]], 0)
+        j45 = keep.tile([P, 45], F32, name="j45")
+        nc.gpsimd.iota(j45[:, 0:25], pattern=[[1, 25]], base=0, channel_multiplier=0, allow_small_or_imprecise_dtypes=True)
+        nc.gpsimd.iota(j45[:, 25:45], pattern=[[1, 20]], base=0, channel_multiplier=0, allow_small_or_imprecise_dtypes=True)
+        xrel = keep.tile([P, 64], F32, name="xrel")
+        for sg in range(3):
+            nc.gpsimd.iota(
+                xrel[:, XLO[sg] : XHI[sg]], pattern=[[1, XHI[sg] - XLO[sg]]], base=XLO[sg] - X0[sg], channel_multiplier=0,
+                allow_small_or_imprecise_dtypes=True,
+            )
+        jsh = keep.tile([P, 5, 2, 64], F32, name="jsh")
+        nc.gpsimd.iota(jsh[:], pattern=[[1, 5], [0, 2], [1, 64]], base=0, channel_multiplier=0, allow_small_or_imprecise_dtypes=True)
+
+        def count_le(name, thresholds, value):
+            n = thresholds.shape[1]
+            g = col(name + "_g", n)
+            nc.vector.tensor_scalar(out=g[:], in0=thresholds[:], scalar1=value[:, 0:1], scalar2=None, op0=ALU.is_le)
+            c = col(name)
+            nc.vector.tensor_reduce(out=c[:], in_=g[:], axis=AX.X, op=ALU.add)
+            return c
+
+        def fma(name, a, k, b):
+            t = col(name)
+            nc.vector.scalar_tensor_tensor(out=t[:], in0=a[:], scalar=k, in1=b[:], op0=ALU.mult, op1=ALU.add)
+            return t
+
+        s5 = count_le("s5", t24, iop)
+        ii = fma("ii", s5, -24.0, iop)
+        c5 = count_le("c5", t5[:, 0:4], ii)
+        cls = fma("cls", c5, -5.0, ii)
+        pen = col("pen")
         nc.vector.tensor_scalar(out=pen[:], in0=s5[:], scalar1=5.0, scalar2=1000.0, op0=ALU.is_ge, op1=ALU.mult)
-        sp = keep.tile([P, 1], F32, name="sp")
+        sp = col("sp")
         nc.vector.tensor_tensor(out=sp[:], in0=s5[:], in1=pen[:], op=ALU.add)
-        k1 = keep.tile([P, 5], F32, name="k1")
-        nc.vector.tensor_scalar(out=k1[:], in0=ee[:], scalar1=5.0, scalar2=sp[:, 0:1], op0=ALU.mult, op1=ALU.add)
-        fall = keep.tile([P, 5, P], F32, name="fall")
-        nc.vector.tensor_tensor(
-            out=fall[:], in0=j1[:].unsqueeze(1).to_broadcast([P, 5, P]), in1=k1[:].unsqueeze(2).to_broadcast([P, 5, P]), op=ALU.is_equal
-        )
-        dd = keep.tile([P, CP], F32, name="dd")
-        nc.vector.tensor_scalar(out=dd[:], in0=crow[:], scalar1=ii[:, 0:1], scalar2=None, op0=ALU.subtract)
-        d2 = keep.tile([P, CP], F32, name="d2")
+        key = fma("key", cls, 5.0, sp)
+        sel = keep.tile([P, 45], F32, name="sel")
+        nc.vector.tensor_scalar(out=sel[:], in0=j45[:], scalar1=key[:, 0:1], scalar2=None, op0=ALU.is_equal)
+
+        dd = col("dd", 64)
+        nc.vector.tensor_scalar(out=dd[:], in0=xrel[:], scalar1=ii[:, 0:1], scalar2=None, op0=ALU.subtract)
+        d2 = col("d2", 64)
         nc.vector.tensor_tensor(out=d2[:], in0=dd[:], in1=dd[:], op=ALU.mult)
-        lt96 = keep.tile([P, 1], F32, name="lt96")
-        nc.vector.tensor_scalar(out=lt96[:], in0=iop[:], scalar1=96.0, scalar2=None, op0=ALU.is_lt)
-        mask = keep.tile([P, 2, CP], F32, name="mask")
-        nc.vector.tensor_scalar(out=mask[:, 0, :], in0=d2[:], scalar1=4.5, scalar2=lt96[:, 0:1], op0=ALU.is_le, op1=ALU.mult)
-        nc.vector.tensor_scalar(out=mask[:, 1, :], in0=d2[:], scalar1=4.5, scalar2=None, op0=ALU.is_le)
+        lt120 = col("lt120")
+        nc.vector.tensor_scalar(out=lt120[:], in0=iop[:], scalar1=120.0, scalar2=None, op0=ALU.is_lt)
+        mask = keep.tile([P, 2, 64], F32, name="mask")
+        for t in range(2):
+            nc.vector.tensor_scalar(out=mask[:, t, :], in0=d2[:], scalar1=4.5, scalar2=lt120[:, 0:1], op0=ALU.is_le, op1=ALU.mult)
+
+        h64 = col("h64")
+        nc.vector.tensor_scalar(out=h64[:], in0=iop[:], scalar1=64.0, scalar2=None, op0=ALU.is_ge)
+        px = fma("px", h64, -64.0, iop)
+        px3 = col("px3")
+        nc.vector.tensor_scalar(out=px3[:], in0=px[:], scalar1=3.0, scalar2=None, op0=ALU.add)
+        q5 = count_le("q5", t5, px3)
+        sx = fma("sx", q5, -5.0, px3)
+        ind = col("ind", 5)
+        nc.vector.tensor_scalar(out=ind[:], in0=r5[:], scalar1=sx[:, 0:1], scalar2=None, op0=ALU.is_equal)
+        room = col("room")
+        nc.vector.tensor_scalar(out=room[:], in0=px[:], scalar1=-1.0, scalar2=63.0, op0=ALU.mult, op1=ALU.add)
+        valid = col("valid", 3)
+        nc.vector.tensor_scalar(out=valid[:], in0=r5[:, 0:3], scalar1=room[:, 0:1], scalar2=None, op0=ALU.is_le)
+        tg0 = col("tg0")
+        nc.vector.tensor_scalar(out=tg0[:], in0=h64[:], scalar1=1000.0, scalar2=2.0, op0=ALU.mult, op1=ALU.add)
+        tga = col("tga")
+        nc.vector.tensor_tensor(out=tga[:], in0=tg0[:], in1=iop[:], op=ALU.add)
+        tgb = col("tgb")
+        nc.vector.tensor_scalar(out=tgb[:], in0=tga[:], scalar1=-1064.0, scalar2=None, op0=ALU.add)
+        shf = keep.tile([P, 2, 5, P], F32, name="shf")
+        shb = keep.tile([P, 2, 5, P], BF16, name="shb")
+        jshv = jsh[:].rearrange("p s h x -> p s (h x)")
+        for a, tg in ((0, tga), (1, tgb)):
+            nc.vector.tensor_scalar(out=shf[:, a], in0=jshv, scalar1=tg[:, 0:1], scalar2=None, op0=ALU.is_equal)
+            nc.vector.tensor_scalar(out=shb[:, a], in0=jshv, scalar1=tg[:, 0:1], scalar2=None, op0=ALU.is_equal)
+        shk = keep.tile([P, 2, P], BF16, name="shk")
+        for a in range(2):
+            nc.vector.tensor_copy(out=shk[:, :, 64 * a : 64 * a + 64], in_=shb[:, a, 0:2, 64 * a : 64 * a + 64])
+        nc.vector.memset(asm[:], 0.0)
 
         sbts = {}
         ubts = {}
 
         def prep(si):
-            w0, w1, m0, m1, blocks = STAGES[si]
+            w0, w1, m0, m1, k0, k1 = ranges[si]
             ylo = 3 * w0 - 2
             nr = 3 * (w1 - w0) + 2
             ya = max(0, ylo)
@@ -176,80 +218,75 @@ def tile_spatialcontext_kernel(tc, feature, conv_w, conv_b, out):
                         in_=img[:, :, ya:yb, X0[sg] : X0[sg] + SW],
                     )
             sbts[si] = sbt
-            k0 = 2 * m0
-            k1_ = min(2 * m1, 21)
+            ka = 2 * m0
+            kb = min(2 * m1, 21)
             ubt = patch.tile([P, 8, NMMAX * P + 8], BF16, name="ubt")
-            nc.vector.memset(ubt[:, :, (k1_ - k0) * 64 : (m1 - m0) * P + 8], 0.0)
+            nc.vector.memset(ubt[:, :, (kb - ka) * 64 : (m1 - m0) * P + 8], 0.0)
             for g in range(2):
                 rows = raws[g][:, :, 64:HW].rearrange("p t (k r) -> p t k r", r=192)
                 nc.scalar.copy(
-                    out=ubt[:, 4 * g : 4 * g + 4, 0 : (k1_ - k0) * 64].rearrange("p t (k x) -> p t k x", x=64),
-                    in_=rows[:, :, k0:k1_, 0:64],
+                    out=ubt[:, 4 * g : 4 * g + 4, 0 : (kb - ka) * 64].rearrange("p t (k x) -> p t k x", x=64),
+                    in_=rows[:, :, ka:kb, 0:64],
                 )
             ubts[si] = ubt
 
-        chunk_no = [0]
+        bases = {}
+        nbase = [0]
 
-        def gram_fold(si):
-            w0, w1, m0, m1, blocks = STAGES[si]
+        def gram(si):
+            w0, w1, m0, m1, k0, k1 = ranges[si]
             nw = w1 - w0
             sbt = sbts[si]
-            groups = [(sg, wi) for sg in range(3) for wi in range(w0, w1)]
-            nch = -(-len(groups) // NG)
-            per = -(-len(groups) // nch)
-            for c0 in range(0, len(groups), per):
-                grp = groups[c0 : c0 + per]
-                ng = len(grp)
-                gp = ps_g.tile([P, NG, 2, CP], F32, name="gp")
-                gm = gms[chunk_no[0] % 2]
-                chunk_no[0] += 1
-                for lo, (sg, wi) in enumerate(grp):
+            pp = ps_s.tile([P, NWMAX, 45], F32, name="pp", tag="s")
+            for c0 in range(w0, w1, 4):
+                c1 = min(c0 + 4, w1)
+                gp = ps_g.tile([P, 4, 2, 64], F32, name="gp")
+                gm = chain.tile([P, 4, 2, 64], F32, name="gm")
+                for wi in range(c0, c1):
                     t0 = 1 if wi == 0 else 0
                     off = 3 * (wi - w0) * SW
-                    for s in range(8):
-                        img = raws[s // 4][:, s % 4, 0:HW].rearrange("p (y x) -> p y x", x=64)
-                        nc.tensor.matmul(
-                            gp[:, lo, t0:2, CLO[sg] : CHI[sg]],
-                            lhsT=sbt[:, s, sg, off : off + P],
-                            rhs=img[:, 3 * wi - 1 + t0 : 3 * wi + 1, X0[sg] + CLO[sg] : X0[sg] + CHI[sg]],
-                            start=(s == 0),
-                            stop=(s == 7),
-                        )
-                parts = []
-                for sg in range(3):
-                    los = [lo for lo, (a, b) in enumerate(grp) if a == sg]
-                    if los:
-                        parts.append((sg, los[0], los[-1] + 1, grp[los[0]][1]))
-                for sg, la, lb, wa in parts:
-                    cs = slice(CLO[sg], CHI[sg])
-                    ln = CHI[sg] - CLO[sg]
-                    if wa == 0:
-                        nc.vector.tensor_tensor(out=gm[:, la, 1, cs], in0=gp[:, la, 1, cs], in1=mask[:, 1, cs], op=ALU.mult)
-                        la += 1
-                    nc.vector.tensor_tensor(
-                        out=gm[:, la:lb, :, cs], in0=gp[:, la:lb, :, cs],
-                        in1=mask[:, :, cs].unsqueeze(1).to_broadcast([P, lb - la, 2, ln]), op=ALU.mult,
+                    for sg in range(3):
+                        for s in range(8):
+                            img = raws[s // 4][:, s % 4, 0:HW].rearrange("p (y x) -> p y x", x=64)
+                            nc.tensor.matmul(
+                                gp[:, wi - c0, t0:2, XLO[sg] : XHI[sg]],
+                                lhsT=sbt[:, s, sg, off : off + P],
+                                rhs=img[:, 3 * wi - 1 + t0 : 3 * wi + 1, XLO[sg] : XHI[sg]],
+                                start=(s == 0),
+                                stop=(s == 7),
+                            )
+                la = 0
+                if c0 == 0:
+                    nc.vector.memset(gm[:, 0, 0, :], 0.0)
+                    nc.vector.tensor_tensor(out=gm[:, 0, 1, :], in0=gp[:, 0, 1, :], in1=mask[:, 1, :], op=ALU.mult)
+                    la = 1
+                n = c1 - c0 - la
+                nc.vector.tensor_tensor(
+                    out=gm[:, la : la + n], in0=gp[:, la : la + n], in1=mask[:].unsqueeze(1).to_broadcast([P, n, 2, 64]), op=ALU.mult
+                )
+                for wi in range(c0, c1):
+                    nc.tensor.matmul(
+                        pp[:, wi - w0, :], lhsT=gm[:, wi - c0].rearrange("p t x -> p (t x)"), rhs=sel[:], start=True, stop=True
                     )
-                vp = ps_v.tile([P, NG, 2, CP], F32, name="vp", tag="vp")
-                gmv = gm[:, 0:ng].rearrange("p g t c -> p (g t) c")
-                vpv = vp[:, 0:ng].rearrange("p g t c -> p (g t) c")
-                for b in range(5):
-                    nc.tensor.matmul(vpv[:, :, b:CP:5], lhsT=fall[:, b, :], rhs=gmv[:, :, b:CP:5], start=True, stop=True)
-                for sg, la, lb, wa in parts:
-                    cs = slice(CLO[sg], CHI[sg])
-                    nc.scalar.copy(
-                        out=vraw[0:104, 2 * wa : 2 * (wa + lb - la), X0[sg] + CLO[sg] : X0[sg] + CHI[sg]],
-                        in_=vp[0:104, la:lb, :, cs].rearrange("p g t c -> p (g t) c"),
-                    )
-
-        tiss = {}
+            u = usum[:, w0:w1, :]
+            nc.vector.tensor_scalar(out=u, in0=pp[:, 0:nw, 0:25], scalar1=ind[:, 0:1], scalar2=None, op0=ALU.mult)
+            for s in range(1, 5):
+                nc.vector.scalar_tensor_tensor(
+                    out=u, in0=pp[:, 0:nw, 5 * s : 5 * s + 25], scalar=ind[:, s : s + 1], in1=u, op0=ALU.mult, op1=ALU.add
+                )
+            b = nbase[0]
+            bases[si] = b
+            nbase[0] = b + nw + 3 * (m1 - m0)
+            for t in range(2):
+                hs = slice(64 * t, 64 * t + 64)
+                nc.vector.tensor_copy(out=nbt[hs, b : b + nw], in_=usum[hs, w0:w1, 11 + t])
 
         def lanes(si):
-            w0, w1, m0, m1, blocks = STAGES[si]
+            w0, w1, m0, m1, k0, k1 = ranges[si]
             ubt = ubts[si]
-            tis = lan2.tile([P, 3, P], F32, name="tis")
-            nc.gpsimd.memset(tis[:], 0.0)
-            for ml in range(m1 - m0):
+            nm = m1 - m0
+            b = bases[si] + (w1 - w0)
+            for ml in range(nm):
                 xs = []
                 for d in range(3):
                     xt = ps_x.tile([P, 1024], BF16, name="x%d" % d)
@@ -259,96 +296,122 @@ def tile_spatialcontext_kernel(tc, feature, conv_w, conv_b, out):
                 x0s = lan2.tile([P, 1024], BF16, name="x0s")
                 nc.scalar.copy(out=x0s[:], in_=xs[0][:])
                 js = lan.tile([P, 1024], BF16, name="js")
-                nc.scalar.activation(out=js[:], in_=xs[0][:], func=ACT.Square, accum_out=tis[:, 0, ml : ml + 1])
+                nc.scalar.activation(out=js[:], in_=xs[0][:], func=ACT.Square, accum_out=nbt[:, b + ml : b + ml + 1])
                 for d in (1, 2):
-                    jv = lan.tile([P, 1024], F32, name="jv")
+                    jv = lan.tile([P, 1024], BF16, name="jv")
                     nc.vector.scalar_tensor_tensor(
                         out=jv[:], in0=xs[d][:], scalar=1.0, in1=x0s[:], op0=ALU.mult, op1=ALU.mult,
-                        accum_out=tis[:, d, ml : ml + 1],
+                        accum_out=nbt[:, b + d * nm + ml : b + d * nm + ml + 1],
                     )
-            tiss[si] = tis
 
-        def rows3(base, n, lead, pitch):
-            v = flat[base : base + lead * pitch].rearrange("(v c) -> v c", c=pitch)
-            return v[:, 0 : n * 3 * RP].rearrange("v (w c) -> v w c", c=3 * RP)[:, :, 0:64]
-
-        def writes(si):
-            w0, w1, m0, m1, blocks = STAGES[si]
+        def norms(si):
+            w0, w1, m0, m1, k0, k1 = ranges[si]
+            nw = w1 - w0
             nm = m1 - m0
-            wa = max(w0, 1)
-            rt = chain.tile([P, NWMAX, 64], F32, name="rt")
-            for pp, tt, wf in ((32, 0, wa), (96, 1, w0)):
-                n = w1 - wf
-                r = rt[pp : pp + 8, 0:n, :]
-                nc.scalar.activation(out=r, in_=vraw[pp : pp + 8, 2 * wf + tt : 2 * w1 : 2, :], func=ACT.Sqrt)
-                nc.vector.tensor_scalar_max(out=r, in0=r, scalar1=EPS)
-                nc.vector.reciprocal(out=r, in_=r)
-                nc.sync.dma_start(
-                    out=rows3(RIB + (3 * wf - 1 + tt + 4) * RP + LP, n, 8, IMG - RP),
-                    in_=r,
+            ncol = nw + nm
+            b = bases[si]
+            rn = ps_s.tile([P, 5, 2, NWMAX + NMMAX], F32, name="rn", tag="s")
+            for s in range(5):
+                for a in range(2):
+                    nc.tensor.matmul(rn[:, s, a, 0:ncol], lhsT=shf[:, a, s, :], rhs=nbt[:, b : b + ncol], start=True, stop=True)
+            rs = chain.tile([P, 5, 2, NWMAX + NMMAX], F32, name="rs")
+            r = rs[:, :, :, 0:ncol]
+            nc.scalar.activation(out=r, in_=rn[:, :, :, 0:ncol], func=ACT.Sqrt)
+            nc.vector.tensor_scalar_max(out=r, in0=r, scalar1=EPS)
+            nc.vector.reciprocal(out=ris[:, :, w0:w1, 1:3].rearrange("p s w a -> p s a w"), in_=rs[:, :, :, 0:nw])
+            nc.vector.reciprocal(
+                out=ris[:, :, 2 * m0 + 1 : 2 * m1 + 1, 0].rearrange("p s (m a) -> p s a m", a=2), in_=rs[:, :, :, nw:ncol]
+            )
+            for t in range(2):
+                hs = slice(64 * t, 64 * t + 64)
+                nc.vector.tensor_tensor(
+                    out=usum[hs, w0:w1, :], in0=usum[hs, w0:w1, :],
+                    in1=ris[hs, 2, w0:w1, 1 + t].unsqueeze(2).to_broadcast([64, nw, 25]), op=ALU.mult,
                 )
-            lt = ps_v.tile([P, 3, P], F32, name="lt", tag="vp")
-            for ty in range(3):
-                nc.tensor.transpose(lt[:, ty, :], tiss[si][:, ty, :], ident_f[:])
-            lts = chain.tile([P, 3, P], F32, name="lts")
-            nc.scalar.copy(out=lts[0:nm], in_=lt[0:nm])
-            ru = chain.tile([P, P], F32, name="ru")
-            nc.scalar.activation(out=ru[0:nm], in_=lts[0:nm, 0, :], func=ACT.Sqrt)
-            nc.vector.tensor_scalar_max(out=ru[0:nm], in0=ru[0:nm], scalar1=EPS)
-            nc.vector.reciprocal(out=ru[0:nm], in_=ru[0:nm])
-            for yy in range(2):
-                n = nm if 6 * (m1 - 1) + 3 * yy + 1 < 64 else nm - 1
-                b0 = RIB + (6 * m0 + 3 * yy + 1 + 4) * RP + LP
-                v = flat[b0 : b0 + 5 * (IMG - RP)].rearrange("(d c) -> d c", c=IMG - RP)
-                v = v[:, 0 : n * 6 * RP].rearrange("d (m c) -> m d c", c=6 * RP)[:, :, 0:64]
-                nc.sync.dma_start(out=v, in_=ru[0:n, 64 * yy : 64 * yy + 64].unsqueeze(1).to_broadcast([n, 5, 64]))
-            for ty, e, sh in ((0, 2, 0), (1, 3, 0), (1, 1, 1), (2, 4, 0), (2, 0, 2)):
-                b0 = VRB + (5 * e + 2) * IMG + (6 * m0 + 1 + 2) * RP + LP + sh
-                v = flat[b0 : b0 + nm * 6 * RP].rearrange("(m y c) -> m y c", y=2, c=3 * RP)[:, :, 0:64]
-                nc.sync.dma_start(out=v, in_=lts[0:nm, ty, :].rearrange("m (y x) -> m y x", x=64))
-            nc.sync.dma_start(out=rows3(VRB + (3 * w0 + 2) * RP + LP, w1 - w0, 32, IMG), in_=vraw[0:32, 2 * w0 + 1 : 2 * w1 : 2, :])
-            nc.sync.dma_start(out=rows3(VRB + IMG + (3 * wa - 1 + 2) * RP + LP, w1 - wa, 32, IMG), in_=vraw[0:32, 2 * wa : 2 * w1 : 2, :])
-            for tt, s, dyt, sh, wf, wl in (
-                (1, 0, 4, -2, w0, w1), (1, 3, 1, 1, w0, w1), (1, 4, 0, 2, max(w0 - 1, 0), w1 - 1), (0, 0, 3, -1, wa, w1), (0, 3, 0, 2, wa, w1),
-            ):
-                yt = 3 * wf - 1 + tt + sh
-                nc.sync.dma_start(
-                    out=rows3(VRB + dyt * IMG + (yt + 2) * RP + LP + 2, wl - wf, 8, 5 * IMG - 1),
-                    in_=vraw[64 + s : 64 + s + 36 : 5, 2 * wf + tt : 2 * wl : 2, :],
+            lt = nbt[:, b + nw : b + nw + 3 * nm].rearrange("p (d m) -> p d m", d=3)
+            nc.vector.tensor_tensor(out=lt, in0=lt, in1=valid[:].unsqueeze(2).to_broadcast([P, 3, nm]), op=ALU.mult)
+            for h in range(2):
+                hs = slice(64 * h, 64 * h + 64)
+                g = ris[hs, :, 2 * m0 + 1 + h : 2 * m1 + h : 2, 0]
+                lh = nbt[hs, b + nw : b + nw + 3 * nm].rearrange("p (d m) -> p d m", d=3)
+                nc.vector.tensor_tensor(out=lh, in0=lh, in1=g[:, 2:5, :], op=ALU.mult)
+                nc.vector.tensor_tensor(
+                    out=asm[hs, NWIN + m0 : NWIN + m1, 12:23:5].rearrange("p m d -> p d m"), in0=lh,
+                    in1=g[:, 2, :].unsqueeze(1).to_broadcast([64, 3, nm]), op=ALU.mult,
                 )
 
-        def back(si):
-            w0, w1, m0, m1, blocks = STAGES[si]
+        def finish(si):
+            f0, f1, blocks = FIN[si]
+            w0, w1, m0, m1, k0, k1 = ranges[si]
+            nm = m1 - m0
+            for t in range(2):
+                hs = slice(64 * t, 64 * t + 64)
+                uv = usum[hs, f0:f1, :].rearrange("p w (s r) -> p w s r", r=5)
+                av = asm[hs, f0:f1, 0:25].rearrange("p w (s y) -> p w s y", y=5)
+                for ra, rb, wo in ((0, 3, 0), (3, 4 + t, 1)):
+                    nc.vector.tensor_tensor(
+                        out=av[:, :, :, ra + 1 - t : rb + 1 - t], in0=uv[:, :, :, ra:rb],
+                        in1=ris[hs, :, f0 + wo : f1 + wo, ra - 3 * wo : rb - 3 * wo].rearrange("p s w r -> p w s r"), op=ALU.mult,
+                    )
+            s0 = max(f0 - 1, 0)
+            ns = f1 - s0
+            mf = ps_f.tile([P, NB], F32, name="mf", tag="f")
+            mp = mf[:, 0 : 50 * NSMAX].rearrange("p (q a w r) -> p q a w r", q=5, a=2, r=5)
+            ml = mf[:, 50 * NSMAX : 50 * NSMAX + 2 * NMMAX].rearrange("p (e m) -> p e m", e=2)
+            for e in range(2):
+                nc.tensor.matmul(
+                    ml[:, e, 0:nm], lhsT=shk[:, e, :], rhs=asm[:, NWIN + m0 : NWIN + m1, 22 - 5 * e], start=True, stop=True
+                )
+            nc.vector.tensor_copy(out=asm[:, NWIN + m0 : NWIN + m1, 2:8:5].rearrange("p m e -> p e m"), in_=ml[:, :, 0:nm])
+            for s in range(5):
+                c = 5 * (4 - s)
+                nc.tensor.matmul(mp[:, s, 0, 0:ns, 0:4], lhsT=shb[:, 0, s, :], rhs=asm[:, s0:f1, c + 1 : c + 5], start=True, stop=True)
+                nc.tensor.matmul(mp[:, s, 1, 0:ns, 0:5], lhsT=shb[:, 1, s, :], rhs=asm[:, s0:f1, c : c + 5], start=True, stop=True)
+            halves = []
+            for h in range(2):
+                ks = [k for k in range(k0, k1) if k % 2 == h]
+                if ks:
+                    halves.append((h, ks[0], len(ks)))
+            for h, ka, n in halves:
+                hs = slice(64 * h, 64 * h + 64)
+                av = asm[hs, NWIN + ka // 2 : NWIN + ka // 2 + n, 0:25].rearrange("p m (s y) -> p s y m", y=5)
+                nc.vector.tensor_copy(out=av[:, :, 0:2, :], in_=mp[hs, :, :, ka - s0 : ka - s0 + 2 * n - 1 : 2, 3])
+                nc.vector.tensor_copy(out=av[:, :, 3:5, :], in_=mp[hs, :, :, ka + 1 - s0 : ka - s0 + 2 * n : 2, 0])
+            ta = max(f0, 1)
+            nc.vector.tensor_copy(
+                out=asm[0:64, ta:f1, 0:25:5].rearrange("p w s -> p s w"), in_=mp[0:64, :, 1, ta - 1 - s0 : f1 - 1 - s0, 4]
+            )
+            for c0 in range(f0, f1, 8):
+                c1 = min(c0 + 8, f1)
+                tp = ps_f.tile([P, 8, P], BF16, name="tp", tag="f")
+                for w in range(c0, c1):
+                    nc.tensor.transpose(tp[:, w - c0, :], asm[:, w, :], ident_b[:])
+                nc.scalar.copy(
+                    out=lrow[:, 3 * c0 * 64 : 3 * c1 * 64].rearrange("p (w c) -> p w c", c=192)[:, :, 0:P], in_=tp[0:32, 0 : c1 - c0, :]
+                )
+            ma = k0 // 2
+            mb = (k1 - 1) // 2 + 1
+            tq = ps_f.tile([P, 8, P], BF16, name="tq", tag="f")
+            for m in range(ma, mb):
+                nc.tensor.transpose(tq[:, m - ma, :], asm[:, NWIN + m, :], ident_b[:])
+            for h, ka, n in halves:
+                st = (3 * ka + 2) * 64
+                nc.scalar.copy(
+                    out=lrow[:, st : st + n * 384].rearrange("p (k c) -> p k c", c=384)[:, :, 0:64],
+                    in_=tq[0:32, ka // 2 - ma : ka // 2 - ma + n, 64 * h : 64 * h + 64],
+                )
             y0 = 8 * blocks[0]
             nr = 8 * len(blocks)
-            r2 = chain1.tile([32, NRMAX, 64], F32, name="r2")
-            for e in range(5):
-                b0 = RIB + (y0 + 2) * RP + LP + e - 2
-                v = flat[b0 : b0 + 5 * IMG].rearrange("(d c) -> d c", c=IMG)[:, 0 : nr * RP].rearrange("d (r c) -> d r c", c=RP)[:, :, 0:64]
-                nc.sync.dma_start(out=r2[5 * e : 5 * e + 5, 0:nr, :], in_=v)
-            rb = chain1.tile([32, NRMAX * RP], F32, name="rb")
-            b0 = RIB + 2 * IMG + (y0 + 2) * RP
-            nc.sync.dma_start(out=rb[:, 0 : nr * RP], in_=flat[b0 : b0 + nr * RP].partition_broadcast(32))
-            vf = chain1.tile([32, NRMAX, 64], F32, name="vf")
-            b0 = VRB + (y0 + 2) * RP + LP
-            v = flat[b0 : b0 + 32 * IMG].rearrange("(v c) -> v c", c=IMG)[:, 0 : nr * RP].rearrange("v (r c) -> v r c", c=RP)[:, :, 0:64]
-            nc.sync.dma_start(out=vf[:, 0:nr, :], in_=v)
-            nc.vector.tensor_tensor(out=vf[0:25, 0:nr, :], in0=vf[0:25, 0:nr, :], in1=r2[0:25, 0:nr, :], op=ALU.mult)
-            vb = chain1.tile([32, NRMAX, 64], BF16, name="vb")
-            nc.vector.tensor_tensor(
-                out=vb[0:25, 0:nr, :], in0=vf[0:25, 0:nr, :],
-                in1=rb[0:25, 0 : nr * RP].rearrange("p (r c) -> p r c", c=RP)[:, :, LP : LP + 64], op=ALU.mult,
-            )
             cols = slice(y0 * 64, (y0 + nr) * 64)
-            vbf = vb[:, 0:nr, :].rearrange("p r x -> p (r x)")
-            nc.sync.dma_start(out=raw1[0:1, 0, cols], in_=vbf[0:1, :])
+            lc = slice((y0 + 1) * 64, (y0 + nr + 1) * 64)
+            nc.sync.dma_start(out=raw1[0:1, 0, cols], in_=lrow[0:1, lc])
             for t in range(1, 4):
-                nc.sync.dma_start(out=raw1[0:8, t, cols], in_=vbf[t : t + 22 : 3, :])
+                nc.sync.dma_start(out=raw1[0:8, t, cols], in_=lrow[t : t + 22 : 3, lc])
 
         def weights():
             wv = conv_w.rearrange("(m p) k -> p m k", p=P)
             nc.sync.dma_start(out=b_in[0:8, :], in_=conv_b.rearrange("(m p) -> m p", p=P))
-            b_ps = ps_v.tile([P, P], BF16, name="b_ps", tag="vp")
+            b_ps = ps_f.tile([P, P], BF16, name="b_ps", tag="f")
             nc.tensor.transpose(b_ps[:], b_in[:], ident_b[:])
             nc.vector.tensor_copy(out=bias[:], in_=b_ps[:, 0:8])
             for mp in range(4):
@@ -379,7 +442,7 @@ def tile_spatialcontext_kernel(tc, feature, conv_w, conv_b, out):
                         in_=wg[:, g, :],
                     )
 
-        def conv_block(n, hold_last):
+        def conv_block(n):
             cols = slice(n * NB, (n + 1) * NB)
             x_codes = codes.tile([P, 2, NB], U32, name="x_codes", align_bytes=64)
             x_scales = codes.tile([P, 2, NB], U8, name="x_scales", align_bytes=64)
@@ -406,29 +469,23 @@ def tile_spatialcontext_kernel(tc, feature, conv_w, conv_b, out):
                         start=(g == 0),
                         stop=(g == 1),
                     )
-                if m == 7 and hold_last:
-                    nc.scalar.activation(out=held[:, n, :], in_=acc[:], func=ACT.Relu, bias=bias[:, m : m + 1], scale=1.0)
-                else:
-                    ot = outs.tile([P, NB], F32, name="ot")
-                    nc.scalar.activation(out=ot[:], in_=acc[:], func=ACT.Relu, bias=bias[:, m : m + 1], scale=1.0)
-                    nc.scalar.dma_start(out=out2[m * P : (m + 1) * P, cols], in_=ot[:])
+                ot = outs.tile([P, NB], F32, name="ot")
+                nc.scalar.activation(out=ot[:], in_=acc[:], func=ACT.Relu, bias=bias[:, m : m + 1], scale=1.0)
+                nc.scalar.dma_start(out=out2[m * P : (m + 1) * P, cols], in_=ot[:])
 
-        def front(si):
+        def sums(si):
             prep(si)
-            gram_fold(si)
+            gram(si)
             lanes(si)
-            writes(si)
+            norms(si)
 
-        ns = len(STAGES)
-        front(0)
+        ns_ = len(FIN)
+        sums(0)
         weights()
-        for si in range(1, min(AHEAD, ns)):
-            front(si)
-        for si in range(ns):
-            if si + AHEAD < ns:
-                front(si + AHEAD)
-            back(si)
-            if si == ns - 1:
-                nc.scalar.dma_start(out=out2[7 * P : 8 * P, 0 : 6 * NB], in_=held[:].rearrange("p n w -> p (n w)"))
-            for n in STAGES[si][4]:
-                conv_block(n, si < ns - 1)
+        finish(0)
+        for si in range(ns_):
+            if si + 1 < ns_:
+                sums(si + 1)
+                finish(si + 1)
+            for n in FIN[si][2]:
+                conv_block(n)

@@ -29,50 +29,28 @@ XHI = (22, 42, 64)
 NWIN = 22
 NLAN = 11
 
-LOAD_ROWS = (0, 15, 21, 39, 54, 64)
-FIN = ((0, 4, (0,)), (4, 6, (1,)), (6, 12, (2, 3)), (12, 17, (4, 5)), (17, 22, (6, 7)))
+LOAD_ROWS = (0, 15, 33, 48, 64)
+CHUNKS = ((0, 5, 0, 2), (5, 11, 2, 5), (11, 16, 5, 8), (16, 22, 8, 11))
 NWMAX = 6
 NMMAX = 3
-NSMAX = 7
+NHALF = 11
 NOUT = 8
-
-
-def stage_ranges():
-    res = []
-    w0 = 0
-    m0 = 0
-    k0 = 0
-    for f0, f1, blocks in FIN:
-        w1 = min(f1 + 1, NWIN)
-        m1 = -(-f1 // 2)
-        k1 = f1 - 1 if f1 < NWIN else 21
-        res.append((w0, w1, m0, m1, k0, k1))
-        w0 = w1
-        m0 = m1
-        k0 = k1
-    return res
 
 
 def tile_spatialcontext_kernel(tc, feature, conv_w, conv_b, out):
     nc = tc.nc
     feat = feature.rearrange("b c h w -> (b c) (h w)")
     out2 = out.rearrange("b o h w -> (b o) (h w)")
-    ranges = stage_ranges()
 
     with ExitStack() as ctx:
         keep = ctx.enter_context(tc.tile_pool(name="keep", bufs=1))
-        stage = ctx.enter_context(tc.tile_pool(name="stage", bufs=2))
+        stage = ctx.enter_context(tc.tile_pool(name="stage", bufs=4))
         patch = ctx.enter_context(tc.tile_pool(name="patch", bufs=2))
         chain = ctx.enter_context(tc.tile_pool(name="chain", bufs=2))
         codes = ctx.enter_context(tc.tile_pool(name="codes", bufs=2))
         outs = ctx.enter_context(tc.tile_pool(name="outs", bufs=NOUT))
         lan = ctx.enter_context(tc.tile_pool(name="lan", bufs=1))
         lan2 = ctx.enter_context(tc.tile_pool(name="lan2", bufs=2))
-        ps_acc = ctx.enter_context(tc.psum_pool(name="ps_acc", bufs=2))
-        ps_g = ctx.enter_context(tc.psum_pool(name="ps_g", bufs=1))
-        ps_s = ctx.enter_context(tc.psum_pool(name="ps_s", bufs=1))
-        ps_f = ctx.enter_context(tc.psum_pool(name="ps_f", bufs=1))
-        ps_x = ctx.enter_context(tc.psum_pool(name="ps_x", bufs=1))
 
         ident_f = keep.tile([P, P], F32, name="ident_f")
         make_identity(nc, ident_f[:])
@@ -103,7 +81,7 @@ def tile_spatialcontext_kernel(tc, feature, conv_w, conv_b, out):
             nc.sync.dma_start(out=raw1[8:128, :, cols], in_=feat[512:992, cols].rearrange("(p j) w -> p j w", j=4))
             nc.sync.dma_start(out=raw1[1:8, 0, cols], in_=feat[992:999, cols])
 
-        for c in range(5):
+        for c in range(4):
             load(c)
 
         def row_iota(name, n, pattern, base):
@@ -198,9 +176,10 @@ def tile_spatialcontext_kernel(tc, feature, conv_w, conv_b, out):
 
         sbts = {}
         ubts = {}
+        ps = {}
 
-        def prep(si):
-            w0, w1, m0, m1, k0, k1 = ranges[si]
+        def prep(ci):
+            w0, w1, m0, m1 = CHUNKS[ci]
             ylo = 3 * w0 - 2
             nr = 3 * (w1 - w0) + 2
             ya = max(0, ylo)
@@ -217,7 +196,7 @@ def tile_spatialcontext_kernel(tc, feature, conv_w, conv_b, out):
                         out=sbt[:, 4 * g : 4 * g + 4, sg, (ya - ylo) * SW : (yb - ylo) * SW].rearrange("p t (y x) -> p t y x", x=SW),
                         in_=img[:, :, ya:yb, X0[sg] : X0[sg] + SW],
                     )
-            sbts[si] = sbt
+            sbts[ci] = sbt
             ka = 2 * m0
             kb = min(2 * m1, 21)
             ubt = patch.tile([P, 8, NMMAX * P + 8], BF16, name="ubt")
@@ -228,19 +207,15 @@ def tile_spatialcontext_kernel(tc, feature, conv_w, conv_b, out):
                     out=ubt[:, 4 * g : 4 * g + 4, 0 : (kb - ka) * 64].rearrange("p t (k x) -> p t k x", x=64),
                     in_=rows[:, :, ka:kb, 0:64],
                 )
-            ubts[si] = ubt
+            ubts[ci] = ubt
 
-        bases = {}
-        nbase = [0]
-
-        def gram(si):
-            w0, w1, m0, m1, k0, k1 = ranges[si]
-            nw = w1 - w0
-            sbt = sbts[si]
-            pp = ps_s.tile([P, NWMAX, 45], F32, name="pp", tag="s")
+        def gram(ci):
+            w0, w1, m0, m1 = CHUNKS[ci]
+            sbt = sbts[ci]
+            pp = ps["pp%d" % (w0 // NHALF)]
             for c0 in range(w0, w1, 4):
                 c1 = min(c0 + 4, w1)
-                gp = ps_g.tile([P, 4, 2, 64], F32, name="gp")
+                gp = ps["g"].tile([P, 4, 2, 64], F32, name="gp")
                 gm = chain.tile([P, 4, 2, 64], F32, name="gm")
                 for wi in range(c0, c1):
                     t0 = 1 if wi == 0 else 0
@@ -266,152 +241,131 @@ def tile_spatialcontext_kernel(tc, feature, conv_w, conv_b, out):
                 )
                 for wi in range(c0, c1):
                     nc.tensor.matmul(
-                        pp[:, wi - w0, :], lhsT=gm[:, wi - c0].rearrange("p t x -> p (t x)"), rhs=sel[:], start=True, stop=True
+                        pp[:, wi % NHALF, :], lhsT=gm[:, wi - c0].rearrange("p t x -> p (t x)"), rhs=sel[:], start=True, stop=True
                     )
-            u = usum[:, w0:w1, :]
-            nc.vector.tensor_scalar(out=u, in0=pp[:, 0:nw, 0:25], scalar1=ind[:, 0:1], scalar2=None, op0=ALU.mult)
+
+        def unrotate(j):
+            pp = ps["pp%d" % j]
+            u = usum[:, NHALF * j : NHALF * (j + 1), :]
+            nc.vector.tensor_scalar(out=u, in0=pp[:, :, 0:25], scalar1=ind[:, 0:1], scalar2=None, op0=ALU.mult)
             for s in range(1, 5):
                 nc.vector.scalar_tensor_tensor(
-                    out=u, in0=pp[:, 0:nw, 5 * s : 5 * s + 25], scalar=ind[:, s : s + 1], in1=u, op0=ALU.mult, op1=ALU.add
+                    out=u, in0=pp[:, :, 5 * s : 5 * s + 25], scalar=ind[:, s : s + 1], in1=u, op0=ALU.mult, op1=ALU.add
                 )
-            b = nbase[0]
-            bases[si] = b
-            nbase[0] = b + nw + 3 * (m1 - m0)
             for t in range(2):
                 hs = slice(64 * t, 64 * t + 64)
-                nc.vector.tensor_copy(out=nbt[hs, b : b + nw], in_=usum[hs, w0:w1, 11 + t])
+                nc.vector.tensor_copy(out=nbt[hs, NHALF * j : NHALF * (j + 1)], in_=usum[hs, NHALF * j : NHALF * (j + 1), 11 + t])
 
-        def lanes(si):
-            w0, w1, m0, m1, k0, k1 = ranges[si]
-            ubt = ubts[si]
-            nm = m1 - m0
-            b = bases[si] + (w1 - w0)
-            for ml in range(nm):
+        def lanes(ci):
+            w0, w1, m0, m1 = CHUNKS[ci]
+            ubt = ubts[ci]
+            for m in range(m0, m1):
+                ml = m - m0
                 xs = []
                 for d in range(3):
-                    xt = ps_x.tile([P, 1024], BF16, name="x%d" % d)
+                    xt = ps["x"].tile([P, 1024], BF16, name="x%d" % d)
                     for s in range(8):
                         nc.tensor.transpose(xt[:, P * s : P * (s + 1)], ubt[:, s, P * ml + d : P * ml + d + P], ident_b[:])
                     xs.append(xt)
                 x0s = lan2.tile([P, 1024], BF16, name="x0s")
                 nc.scalar.copy(out=x0s[:], in_=xs[0][:])
                 js = lan.tile([P, 1024], BF16, name="js")
-                nc.scalar.activation(out=js[:], in_=xs[0][:], func=ACT.Square, accum_out=nbt[:, b + ml : b + ml + 1])
+                nc.scalar.activation(out=js[:], in_=xs[0][:], func=ACT.Square, accum_out=nbt[:, NWIN + m : NWIN + m + 1])
                 for d in (1, 2):
                     jv = lan.tile([P, 1024], BF16, name="jv")
                     nc.vector.scalar_tensor_tensor(
                         out=jv[:], in0=xs[d][:], scalar=1.0, in1=x0s[:], op0=ALU.mult, op1=ALU.mult,
-                        accum_out=nbt[:, b + d * nm + ml : b + d * nm + ml + 1],
+                        accum_out=nbt[:, NWIN + d * NLAN + m : NWIN + d * NLAN + m + 1],
                     )
 
-        def norms(si):
-            w0, w1, m0, m1, k0, k1 = ranges[si]
-            nw = w1 - w0
-            nm = m1 - m0
-            ncol = nw + nm
-            b = bases[si]
-            rn = ps_s.tile([P, 5, 2, NWMAX + NMMAX], F32, name="rn", tag="s")
+        def norms():
+            ncol = NWIN + NLAN
+            rn = ps["s"].tile([P, 5, 2, ncol], F32, name="rn")
             for s in range(5):
                 for a in range(2):
-                    nc.tensor.matmul(rn[:, s, a, 0:ncol], lhsT=shf[:, a, s, :], rhs=nbt[:, b : b + ncol], start=True, stop=True)
-            rs = chain.tile([P, 5, 2, NWMAX + NMMAX], F32, name="rs")
-            r = rs[:, :, :, 0:ncol]
-            nc.scalar.activation(out=r, in_=rn[:, :, :, 0:ncol], func=ACT.Sqrt)
-            nc.vector.tensor_scalar_max(out=r, in0=r, scalar1=EPS)
-            nc.vector.reciprocal(out=ris[:, :, w0:w1, 1:3].rearrange("p s w a -> p s a w"), in_=rs[:, :, :, 0:nw])
-            nc.vector.reciprocal(
-                out=ris[:, :, 2 * m0 + 1 : 2 * m1 + 1, 0].rearrange("p s (m a) -> p s a m", a=2), in_=rs[:, :, :, nw:ncol]
-            )
+                    nc.tensor.matmul(rn[:, s, a, :], lhsT=shf[:, a, s, :], rhs=nbt[:, 0:ncol], start=True, stop=True)
+            rs = keep.tile([P, 5, 2, ncol], F32, name="rs")
+            nc.scalar.activation(out=rs[:], in_=rn[:], func=ACT.Sqrt)
+            nc.vector.tensor_scalar_max(out=rs[:], in0=rs[:], scalar1=EPS)
+            nc.vector.reciprocal(out=ris[:, :, 0:NWIN, 1:3].rearrange("p s w a -> p s a w"), in_=rs[:, :, :, 0:NWIN])
+            nc.vector.reciprocal(out=ris[:, :, 1:23, 0].rearrange("p s (m a) -> p s a m", a=2), in_=rs[:, :, :, NWIN:ncol])
             for t in range(2):
                 hs = slice(64 * t, 64 * t + 64)
                 nc.vector.tensor_tensor(
-                    out=usum[hs, w0:w1, :], in0=usum[hs, w0:w1, :],
-                    in1=ris[hs, 2, w0:w1, 1 + t].unsqueeze(2).to_broadcast([64, nw, 25]), op=ALU.mult,
+                    out=usum[hs], in0=usum[hs], in1=ris[hs, 2, 0:NWIN, 1 + t].unsqueeze(2).to_broadcast([64, NWIN, 25]), op=ALU.mult
                 )
-            lt = nbt[:, b + nw : b + nw + 3 * nm].rearrange("p (d m) -> p d m", d=3)
-            nc.vector.tensor_tensor(out=lt, in0=lt, in1=valid[:].unsqueeze(2).to_broadcast([P, 3, nm]), op=ALU.mult)
+            lt = nbt[:, NWIN : NWIN + 3 * NLAN].rearrange("p (d m) -> p d m", d=3)
+            nc.vector.tensor_tensor(out=lt, in0=lt, in1=valid[:].unsqueeze(2).to_broadcast([P, 3, NLAN]), op=ALU.mult)
             for h in range(2):
                 hs = slice(64 * h, 64 * h + 64)
-                g = ris[hs, :, 2 * m0 + 1 + h : 2 * m1 + h : 2, 0]
-                lh = nbt[hs, b + nw : b + nw + 3 * nm].rearrange("p (d m) -> p d m", d=3)
+                g = ris[hs, :, 1 + h : 22 + h : 2, 0]
+                lh = nbt[hs, NWIN : NWIN + 3 * NLAN].rearrange("p (d m) -> p d m", d=3)
                 nc.vector.tensor_tensor(out=lh, in0=lh, in1=g[:, 2:5, :], op=ALU.mult)
                 nc.vector.tensor_tensor(
-                    out=asm[hs, NWIN + m0 : NWIN + m1, 12:23:5].rearrange("p m d -> p d m"), in0=lh,
-                    in1=g[:, 2, :].unsqueeze(1).to_broadcast([64, 3, nm]), op=ALU.mult,
+                    out=asm[hs, NWIN : NWIN + NLAN, 12:23:5].rearrange("p m d -> p d m"), in0=lh,
+                    in1=g[:, 2, :].unsqueeze(1).to_broadcast([64, 3, NLAN]), op=ALU.mult,
                 )
 
-        def finish(si):
-            f0, f1, blocks = FIN[si]
-            w0, w1, m0, m1, k0, k1 = ranges[si]
-            nm = m1 - m0
+        def finish():
             for t in range(2):
                 hs = slice(64 * t, 64 * t + 64)
-                uv = usum[hs, f0:f1, :].rearrange("p w (s r) -> p w s r", r=5)
-                av = asm[hs, f0:f1, 0:25].rearrange("p w (s y) -> p w s y", y=5)
+                uv = usum[hs].rearrange("p w (s r) -> p w s r", r=5)
+                av = asm[hs, 0:NWIN, 0:25].rearrange("p w (s y) -> p w s y", y=5)
                 for ra, rb, wo in ((0, 3, 0), (3, 4 + t, 1)):
                     nc.vector.tensor_tensor(
                         out=av[:, :, :, ra + 1 - t : rb + 1 - t], in0=uv[:, :, :, ra:rb],
-                        in1=ris[hs, :, f0 + wo : f1 + wo, ra - 3 * wo : rb - 3 * wo].rearrange("p s w r -> p w s r"), op=ALU.mult,
+                        in1=ris[hs, :, wo : NWIN + wo, ra - 3 * wo : rb - 3 * wo].rearrange("p s w r -> p w s r"), op=ALU.mult,
                     )
-            s0 = max(f0 - 1, 0)
-            ns = f1 - s0
-            mf = ps_f.tile([P, NB], F32, name="mf", tag="f")
-            mp = mf[:, 0 : 50 * NSMAX].rearrange("p (q a w r) -> p q a w r", q=5, a=2, r=5)
-            ml = mf[:, 50 * NSMAX : 50 * NSMAX + 2 * NMMAX].rearrange("p (e m) -> p e m", e=2)
+            mf = ps["f"].tile([P, 5, 2, NWIN, 2], F32, name="mf")
+            m2 = ps["f"].tile([P, 5 * NWIN + 2 * NLAN], F32, name="m2")
+            t2 = m2[:, 0 : 5 * NWIN].rearrange("p (q w) -> p q w", q=5)
+            ml = m2[:, 5 * NWIN : 5 * NWIN + 2 * NLAN].rearrange("p (e m) -> p e m", e=2)
             for e in range(2):
-                nc.tensor.matmul(
-                    ml[:, e, 0:nm], lhsT=shk[:, e, :], rhs=asm[:, NWIN + m0 : NWIN + m1, 22 - 5 * e], start=True, stop=True
-                )
-            nc.vector.tensor_copy(out=asm[:, NWIN + m0 : NWIN + m1, 2:8:5].rearrange("p m e -> p e m"), in_=ml[:, :, 0:nm])
+                nc.tensor.matmul(ml[:, e, :], lhsT=shk[:, e, :], rhs=asm[:, NWIN : NWIN + NLAN, 22 - 5 * e], start=True, stop=True)
+            nc.vector.tensor_copy(out=asm[:, NWIN : NWIN + NLAN, 2:8:5].rearrange("p m e -> p e m"), in_=ml)
             for s in range(5):
                 c = 5 * (4 - s)
-                nc.tensor.matmul(mp[:, s, 0, 0:ns, 0:4], lhsT=shb[:, 0, s, :], rhs=asm[:, s0:f1, c + 1 : c + 5], start=True, stop=True)
-                nc.tensor.matmul(mp[:, s, 1, 0:ns, 0:5], lhsT=shb[:, 1, s, :], rhs=asm[:, s0:f1, c : c + 5], start=True, stop=True)
-            halves = []
-            for h in range(2):
-                ks = [k for k in range(k0, k1) if k % 2 == h]
-                if ks:
-                    halves.append((h, ks[0], len(ks)))
-            for h, ka, n in halves:
+                nc.tensor.matmul(mf[:, s, 0], lhsT=shb[:, 0, s, :], rhs=asm[:, 0:NWIN, c + 1 : c + 5 : 3], start=True, stop=True)
+                nc.tensor.matmul(mf[:, s, 1], lhsT=shb[:, 1, s, :], rhs=asm[:, 0:NWIN, c : c + 4 : 3], start=True, stop=True)
+                nc.tensor.matmul(t2[:, s, :], lhsT=shb[:, 1, s, :], rhs=asm[:, 0:NWIN, c + 4], start=True, stop=True)
+            halves = ((0, 11), (1, 10))
+            for h, n in halves:
                 hs = slice(64 * h, 64 * h + 64)
-                av = asm[hs, NWIN + ka // 2 : NWIN + ka // 2 + n, 0:25].rearrange("p m (s y) -> p s y m", y=5)
-                nc.vector.tensor_copy(out=av[:, :, 0:2, :], in_=mp[hs, :, :, ka - s0 : ka - s0 + 2 * n - 1 : 2, 3])
-                nc.vector.tensor_copy(out=av[:, :, 3:5, :], in_=mp[hs, :, :, ka + 1 - s0 : ka - s0 + 2 * n : 2, 0])
-            ta = max(f0, 1)
-            nc.vector.tensor_copy(
-                out=asm[0:64, ta:f1, 0:25:5].rearrange("p w s -> p s w"), in_=mp[0:64, :, 1, ta - 1 - s0 : f1 - 1 - s0, 4]
-            )
-            for c0 in range(f0, f1, 8):
-                c1 = min(c0 + 8, f1)
-                tp = ps_f.tile([P, 8, P], BF16, name="tp", tag="f")
+                av = asm[hs, NWIN : NWIN + n, 0:25].rearrange("p m (s y) -> p s y m", y=5)
+                nc.vector.tensor_copy(out=av[:, :, 0:2, :], in_=mf[hs, :, :, h : h + 2 * n - 1 : 2, 1])
+                nc.vector.tensor_copy(out=av[:, :, 3:5, :], in_=mf[hs, :, :, h + 1 : h + 2 * n : 2, 0])
+            nc.vector.tensor_copy(out=asm[0:64, 1:NWIN, 0:25:5].rearrange("p w s -> p s w"), in_=t2[0:64, :, 0 : NWIN - 1])
+            for c0 in range(0, NWIN, 8):
+                c1 = min(c0 + 8, NWIN)
+                tp = ps["t"].tile([P, 8, P], BF16, name="tp")
                 for w in range(c0, c1):
                     nc.tensor.transpose(tp[:, w - c0, :], asm[:, w, :], ident_b[:])
                 nc.scalar.copy(
                     out=lrow[:, 3 * c0 * 64 : 3 * c1 * 64].rearrange("p (w c) -> p w c", c=192)[:, :, 0:P], in_=tp[0:32, 0 : c1 - c0, :]
                 )
-            ma = k0 // 2
-            mb = (k1 - 1) // 2 + 1
-            tq = ps_f.tile([P, 8, P], BF16, name="tq", tag="f")
-            for m in range(ma, mb):
-                nc.tensor.transpose(tq[:, m - ma, :], asm[:, NWIN + m, :], ident_b[:])
-            for h, ka, n in halves:
-                st = (3 * ka + 2) * 64
-                nc.scalar.copy(
-                    out=lrow[:, st : st + n * 384].rearrange("p (k c) -> p k c", c=384)[:, :, 0:64],
-                    in_=tq[0:32, ka // 2 - ma : ka // 2 - ma + n, 64 * h : 64 * h + 64],
-                )
-            y0 = 8 * blocks[0]
-            nr = 8 * len(blocks)
-            cols = slice(y0 * 64, (y0 + nr) * 64)
-            lc = slice((y0 + 1) * 64, (y0 + nr + 1) * 64)
-            nc.sync.dma_start(out=raw1[0:1, 0, cols], in_=lrow[0:1, lc])
-            for t in range(1, 4):
-                nc.sync.dma_start(out=raw1[0:8, t, cols], in_=lrow[t : t + 22 : 3, lc])
+            for c0 in range(0, NLAN, 8):
+                c1 = min(c0 + 8, NLAN)
+                tp = ps["t"].tile([P, 8, P], BF16, name="tp")
+                for m in range(c0, c1):
+                    nc.tensor.transpose(tp[:, m - c0, :], asm[:, NWIN + m, :], ident_b[:])
+                for h, n in halves:
+                    cn = min(c1, n) - c0
+                    st = (3 * (2 * c0 + h) + 2) * 64
+                    nc.scalar.copy(
+                        out=lrow[:, st : st + cn * 384].rearrange("p (k c) -> p k c", c=384)[:, :, 0:64],
+                        in_=tp[0:32, 0:cn, 64 * h : 64 * h + 64],
+                    )
+            for y0 in range(0, 64, 16):
+                cols = slice(y0 * 64, (y0 + 16) * 64)
+                lc = slice((y0 + 1) * 64, (y0 + 17) * 64)
+                nc.sync.dma_start(out=raw1[0:1, 0, cols], in_=lrow[0:1, lc])
+                for t in range(1, 4):
+                    nc.sync.dma_start(out=raw1[0:8, t, cols], in_=lrow[t : t + 22 : 3, lc])
 
         def weights():
             wv = conv_w.rearrange("(m p) k -> p m k", p=P)
             nc.sync.dma_start(out=b_in[0:8, :], in_=conv_b.rearrange("(m p) -> m p", p=P))
-            b_ps = ps_f.tile([P, P], BF16, name="b_ps", tag="f")
+            b_ps = ps["w"].tile([P, P], BF16, name="b_ps", tag="wt")
             nc.tensor.transpose(b_ps[:], b_in[:], ident_b[:])
             nc.vector.tensor_copy(out=bias[:], in_=b_ps[:, 0:8])
             for mp in range(4):
@@ -428,7 +382,7 @@ def tile_spatialcontext_kernel(tc, feature, conv_w, conv_b, out):
                 w32 = w_sb[:].rearrange("p m k -> p (m k)").bitcast(F32).rearrange("p (m k) -> p m k", m=2)
                 wg = stage.tile([P, 2, 1024], BF16, name="wg", tag="grouped", align_bytes=64)
                 for g in range(2):
-                    wt = ps_acc.tile([P, 2, 2, P], F32, name="wt", tag="acc")
+                    wt = ps["w"].tile([P, 2, 2, P], F32, name="wt", tag="wt")
                     for m2 in range(2):
                         for u in range(2):
                             nc.tensor.transpose(wt[:, m2, u, :], w32[:, m2, 256 * g + u : 256 * (g + 1) : 2], ident_f[:])
@@ -450,15 +404,12 @@ def tile_spatialcontext_kernel(tc, feature, conv_w, conv_b, out):
                 grouped = stage.tile([P, NB, 4], BF16, name="grouped", tag="grouped", align_bytes=64)
                 view = raws[g][:, :, cols].rearrange("p j (c i) -> p c j i", i=4)
                 gview = grouped[:].rearrange("p (c i) j -> p c j i", i=4)
-                if g == 0:
-                    nc.scalar.copy(out=gview, in_=view)
-                else:
-                    nc.vector.tensor_copy(out=gview, in_=view)
+                nc.vector.tensor_copy(out=gview, in_=view)
                 nc.vector.quantize_mx(
                     out=x_codes[:, g, :].bitcast(FP8X4), scales=x_scales[:, g, :], in_=grouped[:].rearrange("p w j -> p (w j)")
                 )
             for m in range(8):
-                acc = ps_acc.tile([P, NB], F32, name="acc", tag="acc")
+                acc = ps["acc"].tile([P, NB], F32, name="acc")
                 for g in range(2):
                     nc.tensor.matmul_mx(
                         out=acc[:],
@@ -471,21 +422,29 @@ def tile_spatialcontext_kernel(tc, feature, conv_w, conv_b, out):
                     )
                 ot = outs.tile([P, NB], F32, name="ot")
                 nc.scalar.activation(out=ot[:], in_=acc[:], func=ACT.Relu, bias=bias[:, m : m + 1], scale=1.0)
-                nc.scalar.dma_start(out=out2[m * P : (m + 1) * P, cols], in_=ot[:])
+                nc.sync.dma_start(out=out2[m * P : (m + 1) * P, cols], in_=ot[:])
 
-        def sums(si):
-            prep(si)
-            gram(si)
-            lanes(si)
-            norms(si)
-
-        ns_ = len(FIN)
-        sums(0)
-        weights()
-        finish(0)
-        for si in range(ns_):
-            if si + 1 < ns_:
-                sums(si + 1)
-                finish(si + 1)
-            for n in FIN[si][2]:
+        with ExitStack() as c1:
+            ps["g"] = c1.enter_context(tc.psum_pool(name="ps_g", bufs=2))
+            ps_p = c1.enter_context(tc.psum_pool(name="ps_p", bufs=1))
+            ps["x"] = c1.enter_context(tc.psum_pool(name="ps_x", bufs=1))
+            ps["pp0"] = ps_p.tile([P, NHALF, 45], F32, name="pp0")
+            ps["pp1"] = ps_p.tile([P, NHALF, 45], F32, name="pp1")
+            for ci in range(len(CHUNKS)):
+                prep(ci)
+                gram(ci)
+                lanes(ci)
+                if ci % 2 == 1:
+                    unrotate(ci // 2)
+        with ExitStack() as c2:
+            ps["s"] = c2.enter_context(tc.psum_pool(name="ps_s", bufs=1))
+            ps["f"] = c2.enter_context(tc.psum_pool(name="ps_f", bufs=1))
+            ps["t"] = c2.enter_context(tc.psum_pool(name="ps_t", bufs=3))
+            ps["w"] = c2.enter_context(tc.psum_pool(name="ps_w", bufs=2))
+            norms()
+            finish()
+            weights()
+        with ExitStack() as c3:
+            ps["acc"] = c3.enter_context(tc.psum_pool(name="ps_acc", bufs=8))
+            for n in range(8):
                 conv_block(n)

@@ -35,6 +35,10 @@ NWMAX = 6
 NMMAX = 3
 NHALF = 11
 NOUT = 8
+RUNS = ((0, 11, 0, 5, 0, 10, 0, 9, (0, 1, 2)), (11, 22, 5, 11, 10, 22, 9, 21, (3, 4, 5, 6, 7)))
+NBASE = (0, 26)
+NSMAX = 13
+NMRUN = 6
 
 
 def tile_spatialcontext_kernel(tc, feature, conv_w, conv_b, out):
@@ -81,98 +85,27 @@ def tile_spatialcontext_kernel(tc, feature, conv_w, conv_b, out):
             nc.sync.dma_start(out=raw1[8:128, :, cols], in_=feat[512:992, cols].rearrange("(p j) w -> p j w", j=4))
             nc.sync.dma_start(out=raw1[1:8, 0, cols], in_=feat[992:999, cols])
 
-        for c in range(4):
-            load(c)
+        wv = conv_w.rearrange("(m p) k -> p m k", p=P)
+        w_sbs = []
+        w_tails = []
 
-        def row_iota(name, n, pattern, base):
-            t = keep.tile([P, n], F32, name=name)
-            nc.gpsimd.iota(t[:], pattern=pattern, base=base, channel_multiplier=0, allow_small_or_imprecise_dtypes=True)
-            return t
+        def load_weights():
+            nc.sync.dma_start(out=b_in[0:8, :], in_=conv_b.rearrange("(m p) -> m p", p=P))
+            for mp in range(4):
+                w_sb = stage.tile([P, 2, OC], BF16, name="w_sb", tag="grouped", align_bytes=64)
+                w_tail = stage.tile([P, 2, 32], BF16, name="w_tail")
+                ms = slice(2 * mp, 2 * mp + 2)
+                nc.sync.dma_start(out=w_sb[:, :, 0:512], in_=wv[:, ms, 0:512])
+                nc.sync.dma_start(out=w_sb[:, :, 544:1024], in_=wv[:, ms, 512:992])
+                nc.sync.dma_start(out=w_tail[:], in_=wv[:, ms, 992:1024])
+                w_sbs.append(w_sb)
+                w_tails.append(w_tail)
 
-        def col(name, n=1):
-            return keep.tile([P, n], F32, name=name)
-
-        iop = col("iop")
-        nc.gpsimd.iota(iop[:], pattern=[[0, 1]], base=0, channel_multiplier=1, allow_small_or_imprecise_dtypes=True)
-        t24 = row_iota("t24", 5, [[24, 5]], 24)
-        t5 = row_iota("t5", 13, [[5, 13]], 5)
-        r5 = row_iota("r5", 5, [[1, 5]], 0)
-        j45 = keep.tile([P, 45], F32, name="j45")
-        nc.gpsimd.iota(j45[:, 0:25], pattern=[[1, 25]], base=0, channel_multiplier=0, allow_small_or_imprecise_dtypes=True)
-        nc.gpsimd.iota(j45[:, 25:45], pattern=[[1, 20]], base=0, channel_multiplier=0, allow_small_or_imprecise_dtypes=True)
-        xrel = keep.tile([P, 64], F32, name="xrel")
-        for sg in range(3):
-            nc.gpsimd.iota(
-                xrel[:, XLO[sg] : XHI[sg]], pattern=[[1, XHI[sg] - XLO[sg]]], base=XLO[sg] - X0[sg], channel_multiplier=0,
-                allow_small_or_imprecise_dtypes=True,
-            )
-        jsh = keep.tile([P, 5, 2, 64], F32, name="jsh")
-        nc.gpsimd.iota(jsh[:], pattern=[[1, 5], [0, 2], [1, 64]], base=0, channel_multiplier=0, allow_small_or_imprecise_dtypes=True)
-
-        def count_le(name, thresholds, value):
-            n = thresholds.shape[1]
-            g = col(name + "_g", n)
-            nc.vector.tensor_scalar(out=g[:], in0=thresholds[:], scalar1=value[:, 0:1], scalar2=None, op0=ALU.is_le)
-            c = col(name)
-            nc.vector.tensor_reduce(out=c[:], in_=g[:], axis=AX.X, op=ALU.add)
-            return c
-
-        def fma(name, a, k, b):
-            t = col(name)
-            nc.vector.scalar_tensor_tensor(out=t[:], in0=a[:], scalar=k, in1=b[:], op0=ALU.mult, op1=ALU.add)
-            return t
-
-        s5 = count_le("s5", t24, iop)
-        ii = fma("ii", s5, -24.0, iop)
-        c5 = count_le("c5", t5[:, 0:4], ii)
-        cls = fma("cls", c5, -5.0, ii)
-        pen = col("pen")
-        nc.vector.tensor_scalar(out=pen[:], in0=s5[:], scalar1=5.0, scalar2=1000.0, op0=ALU.is_ge, op1=ALU.mult)
-        sp = col("sp")
-        nc.vector.tensor_tensor(out=sp[:], in0=s5[:], in1=pen[:], op=ALU.add)
-        key = fma("key", cls, 5.0, sp)
-        sel = keep.tile([P, 45], F32, name="sel")
-        nc.vector.tensor_scalar(out=sel[:], in0=j45[:], scalar1=key[:, 0:1], scalar2=None, op0=ALU.is_equal)
-
-        dd = col("dd", 64)
-        nc.vector.tensor_scalar(out=dd[:], in0=xrel[:], scalar1=ii[:, 0:1], scalar2=None, op0=ALU.subtract)
-        d2 = col("d2", 64)
-        nc.vector.tensor_tensor(out=d2[:], in0=dd[:], in1=dd[:], op=ALU.mult)
-        lt120 = col("lt120")
-        nc.vector.tensor_scalar(out=lt120[:], in0=iop[:], scalar1=120.0, scalar2=None, op0=ALU.is_lt)
-        mask = keep.tile([P, 2, 64], F32, name="mask")
-        for t in range(2):
-            nc.vector.tensor_scalar(out=mask[:, t, :], in0=d2[:], scalar1=4.5, scalar2=lt120[:, 0:1], op0=ALU.is_le, op1=ALU.mult)
-
-        h64 = col("h64")
-        nc.vector.tensor_scalar(out=h64[:], in0=iop[:], scalar1=64.0, scalar2=None, op0=ALU.is_ge)
-        px = fma("px", h64, -64.0, iop)
-        px3 = col("px3")
-        nc.vector.tensor_scalar(out=px3[:], in0=px[:], scalar1=3.0, scalar2=None, op0=ALU.add)
-        q5 = count_le("q5", t5, px3)
-        sx = fma("sx", q5, -5.0, px3)
-        ind = col("ind", 5)
-        nc.vector.tensor_scalar(out=ind[:], in0=r5[:], scalar1=sx[:, 0:1], scalar2=None, op0=ALU.is_equal)
-        room = col("room")
-        nc.vector.tensor_scalar(out=room[:], in0=px[:], scalar1=-1.0, scalar2=63.0, op0=ALU.mult, op1=ALU.add)
-        valid = col("valid", 3)
-        nc.vector.tensor_scalar(out=valid[:], in0=r5[:, 0:3], scalar1=room[:, 0:1], scalar2=None, op0=ALU.is_le)
-        tg0 = col("tg0")
-        nc.vector.tensor_scalar(out=tg0[:], in0=h64[:], scalar1=1000.0, scalar2=2.0, op0=ALU.mult, op1=ALU.add)
-        tga = col("tga")
-        nc.vector.tensor_tensor(out=tga[:], in0=tg0[:], in1=iop[:], op=ALU.add)
-        tgb = col("tgb")
-        nc.vector.tensor_scalar(out=tgb[:], in0=tga[:], scalar1=-1064.0, scalar2=None, op0=ALU.add)
-        shf = keep.tile([P, 2, 5, P], F32, name="shf")
-        shb = keep.tile([P, 2, 5, P], BF16, name="shb")
-        jshv = jsh[:].rearrange("p s h x -> p s (h x)")
-        for a, tg in ((0, tga), (1, tgb)):
-            nc.vector.tensor_scalar(out=shf[:, a], in0=jshv, scalar1=tg[:, 0:1], scalar2=None, op0=ALU.is_equal)
-            nc.vector.tensor_scalar(out=shb[:, a], in0=jshv, scalar1=tg[:, 0:1], scalar2=None, op0=ALU.is_equal)
-        shk = keep.tile([P, 2, P], BF16, name="shk")
-        for a in range(2):
-            nc.vector.tensor_copy(out=shk[:, :, 64 * a : 64 * a + 64], in_=shb[:, a, 0:2, 64 * a : 64 * a + 64])
-        nc.vector.memset(asm[:], 0.0)
+        load(0)
+        load(1)
+        load_weights()
+        load(2)
+        load(3)
 
         sbts = {}
         ubts = {}
@@ -254,13 +187,16 @@ def tile_spatialcontext_kernel(tc, feature, conv_w, conv_b, out):
                 )
             for t in range(2):
                 hs = slice(64 * t, 64 * t + 64)
-                nc.vector.tensor_copy(out=nbt[hs, NHALF * j : NHALF * (j + 1)], in_=usum[hs, NHALF * j : NHALF * (j + 1), 11 + t])
+                nc.vector.tensor_copy(out=nbt[hs, NBASE[j] : NBASE[j] + NHALF], in_=usum[hs, NHALF * j : NHALF * (j + 1), 11 + t])
 
         def lanes(ci):
             w0, w1, m0, m1 = CHUNKS[ci]
             ubt = ubts[ci]
             for m in range(m0, m1):
                 ml = m - m0
+                j = 0 if m < RUNS[0][3] else 1
+                nm = RUNS[j][3] - RUNS[j][2]
+                b = NBASE[j] + NHALF + m - RUNS[j][2]
                 xs = []
                 for d in range(3):
                     xt = ps["x"].tile([P, 1024], BF16, name="x%d" % d)
@@ -270,130 +206,147 @@ def tile_spatialcontext_kernel(tc, feature, conv_w, conv_b, out):
                 x0s = lan2.tile([P, 1024], BF16, name="x0s")
                 nc.scalar.copy(out=x0s[:], in_=xs[0][:])
                 js = lan.tile([P, 1024], BF16, name="js")
-                nc.scalar.activation(out=js[:], in_=xs[0][:], func=ACT.Square, accum_out=nbt[:, NWIN + m : NWIN + m + 1])
+                nc.scalar.activation(out=js[:], in_=xs[0][:], func=ACT.Square, accum_out=nbt[:, b : b + 1])
                 for d in (1, 2):
                     jv = lan.tile([P, 1024], BF16, name="jv")
                     nc.vector.scalar_tensor_tensor(
                         out=jv[:], in0=xs[d][:], scalar=1.0, in1=x0s[:], op0=ALU.mult, op1=ALU.mult,
-                        accum_out=nbt[:, NWIN + d * NLAN + m : NWIN + d * NLAN + m + 1],
+                        accum_out=nbt[:, b + d * nm : b + d * nm + 1],
                     )
 
-        def norms():
-            ncol = NWIN + NLAN
-            rn = ps["s"].tile([P, 5, 2, ncol], F32, name="rn")
+        def norms(j):
+            w0, w1, m0, m1, f0, f1, k0, k1, blocks = RUNS[j]
+            nw = w1 - w0
+            nm = m1 - m0
+            ncol = nw + nm
+            b = NBASE[j]
+            rn = ps["c"].tile([P, 5, 2, NHALF + NMRUN], F32, name="rn", tag="c")
             for s in range(5):
                 for a in range(2):
-                    nc.tensor.matmul(rn[:, s, a, :], lhsT=shf[:, a, s, :], rhs=nbt[:, 0:ncol], start=True, stop=True)
-            rs = keep.tile([P, 5, 2, ncol], F32, name="rs")
-            nc.scalar.activation(out=rs[:], in_=rn[:], func=ACT.Sqrt)
-            nc.vector.tensor_scalar_max(out=rs[:], in0=rs[:], scalar1=EPS)
-            nc.vector.reciprocal(out=ris[:, :, 0:NWIN, 1:3].rearrange("p s w a -> p s a w"), in_=rs[:, :, :, 0:NWIN])
-            nc.vector.reciprocal(out=ris[:, :, 1:23, 0].rearrange("p s (m a) -> p s a m", a=2), in_=rs[:, :, :, NWIN:ncol])
+                    nc.tensor.matmul(rn[:, s, a, 0:ncol], lhsT=shf[:, a, s, :], rhs=nbt[:, b : b + ncol], start=True, stop=True)
+            rs = chain.tile([P, 5, 2, NHALF + NMRUN], F32, name="rs")
+            r = rs[:, :, :, 0:ncol]
+            nc.scalar.activation(out=r, in_=rn[:, :, :, 0:ncol], func=ACT.Sqrt)
+            nc.vector.tensor_scalar_max(out=r, in0=r, scalar1=EPS)
+            nc.vector.reciprocal(out=ris[:, :, w0:w1, 1:3].rearrange("p s w a -> p s a w"), in_=rs[:, :, :, 0:nw])
+            nc.vector.reciprocal(
+                out=ris[:, :, 2 * m0 + 1 : 2 * m1 + 1, 0].rearrange("p s (m a) -> p s a m", a=2), in_=rs[:, :, :, nw:ncol]
+            )
             for t in range(2):
                 hs = slice(64 * t, 64 * t + 64)
                 nc.vector.tensor_tensor(
-                    out=usum[hs], in0=usum[hs], in1=ris[hs, 2, 0:NWIN, 1 + t].unsqueeze(2).to_broadcast([64, NWIN, 25]), op=ALU.mult
+                    out=usum[hs, w0:w1, :], in0=usum[hs, w0:w1, :],
+                    in1=ris[hs, 2, w0:w1, 1 + t].unsqueeze(2).to_broadcast([64, nw, 25]), op=ALU.mult,
                 )
-            lt = nbt[:, NWIN : NWIN + 3 * NLAN].rearrange("p (d m) -> p d m", d=3)
-            nc.vector.tensor_tensor(out=lt, in0=lt, in1=valid[:].unsqueeze(2).to_broadcast([P, 3, NLAN]), op=ALU.mult)
+            lt = nbt[:, b + nw : b + nw + 3 * nm].rearrange("p (d m) -> p d m", d=3)
+            nc.vector.tensor_tensor(out=lt, in0=lt, in1=valid[:].unsqueeze(2).to_broadcast([P, 3, nm]), op=ALU.mult)
             for h in range(2):
                 hs = slice(64 * h, 64 * h + 64)
-                g = ris[hs, :, 1 + h : 22 + h : 2, 0]
-                lh = nbt[hs, NWIN : NWIN + 3 * NLAN].rearrange("p (d m) -> p d m", d=3)
+                g = ris[hs, :, 2 * m0 + 1 + h : 2 * m1 + h : 2, 0]
+                lh = nbt[hs, b + nw : b + nw + 3 * nm].rearrange("p (d m) -> p d m", d=3)
                 nc.vector.tensor_tensor(out=lh, in0=lh, in1=g[:, 2:5, :], op=ALU.mult)
                 nc.vector.tensor_tensor(
-                    out=asm[hs, NWIN : NWIN + NLAN, 12:23:5].rearrange("p m d -> p d m"), in0=lh,
-                    in1=g[:, 2, :].unsqueeze(1).to_broadcast([64, 3, NLAN]), op=ALU.mult,
+                    out=asm[hs, NWIN + m0 : NWIN + m1, 12:23:5].rearrange("p m d -> p d m"), in0=lh,
+                    in1=g[:, 2, :].unsqueeze(1).to_broadcast([64, 3, nm]), op=ALU.mult,
                 )
 
-        def finish():
+        def finish(j):
+            w0, w1, m0, m1, f0, f1, k0, k1, blocks = RUNS[j]
+            nm = m1 - m0
             for t in range(2):
                 hs = slice(64 * t, 64 * t + 64)
-                uv = usum[hs].rearrange("p w (s r) -> p w s r", r=5)
-                av = asm[hs, 0:NWIN, 0:25].rearrange("p w (s y) -> p w s y", y=5)
+                uv = usum[hs, f0:f1, :].rearrange("p w (s r) -> p w s r", r=5)
+                av = asm[hs, f0:f1, 0:25].rearrange("p w (s y) -> p w s y", y=5)
                 for ra, rb, wo in ((0, 3, 0), (3, 4 + t, 1)):
                     nc.vector.tensor_tensor(
                         out=av[:, :, :, ra + 1 - t : rb + 1 - t], in0=uv[:, :, :, ra:rb],
-                        in1=ris[hs, :, wo : NWIN + wo, ra - 3 * wo : rb - 3 * wo].rearrange("p s w r -> p w s r"), op=ALU.mult,
+                        in1=ris[hs, :, f0 + wo : f1 + wo, ra - 3 * wo : rb - 3 * wo].rearrange("p s w r -> p w s r"), op=ALU.mult,
                     )
-            mf = ps["f"].tile([P, 5, 2, NWIN, 2], F32, name="mf")
-            m2 = ps["f"].tile([P, 5 * NWIN + 2 * NLAN], F32, name="m2")
-            t2 = m2[:, 0 : 5 * NWIN].rearrange("p (q w) -> p q w", q=5)
-            ml = m2[:, 5 * NWIN : 5 * NWIN + 2 * NLAN].rearrange("p (e m) -> p e m", e=2)
+            s0 = max(f0 - 1, 0)
+            ns = f1 - s0
+            cf = ps["c"].tile([P, NB], F32, name="cf", tag="c")
+            mf = cf[:, 0 : 20 * NSMAX].rearrange("p (q a w r) -> p q a w r", q=5, a=2, r=2)
+            t2 = cf[:, 20 * NSMAX : 25 * NSMAX].rearrange("p (q w) -> p q w", q=5)
+            ml = cf[:, 25 * NSMAX : 25 * NSMAX + 2 * NMRUN].rearrange("p (e m) -> p e m", e=2)
             for e in range(2):
-                nc.tensor.matmul(ml[:, e, :], lhsT=shk[:, e, :], rhs=asm[:, NWIN : NWIN + NLAN, 22 - 5 * e], start=True, stop=True)
-            nc.vector.tensor_copy(out=asm[:, NWIN : NWIN + NLAN, 2:8:5].rearrange("p m e -> p e m"), in_=ml)
+                nc.tensor.matmul(
+                    ml[:, e, 0:nm], lhsT=shk[:, e, :], rhs=asm[:, NWIN + m0 : NWIN + m1, 22 - 5 * e], start=True, stop=True
+                )
             for s in range(5):
                 c = 5 * (4 - s)
-                nc.tensor.matmul(mf[:, s, 0], lhsT=shb[:, 0, s, :], rhs=asm[:, 0:NWIN, c + 1 : c + 5 : 3], start=True, stop=True)
-                nc.tensor.matmul(mf[:, s, 1], lhsT=shb[:, 1, s, :], rhs=asm[:, 0:NWIN, c : c + 4 : 3], start=True, stop=True)
-                nc.tensor.matmul(t2[:, s, :], lhsT=shb[:, 1, s, :], rhs=asm[:, 0:NWIN, c + 4], start=True, stop=True)
-            halves = ((0, 11), (1, 10))
-            for h, n in halves:
+                nc.tensor.matmul(mf[:, s, 0, 0:ns, :], lhsT=shb[:, 0, s, :], rhs=asm[:, s0:f1, c + 1 : c + 5 : 3], start=True, stop=True)
+                nc.tensor.matmul(mf[:, s, 1, 0:ns, :], lhsT=shb[:, 1, s, :], rhs=asm[:, s0:f1, c : c + 4 : 3], start=True, stop=True)
+                nc.tensor.matmul(t2[:, s, 0:ns], lhsT=shb[:, 1, s, :], rhs=asm[:, s0:f1, c + 4], start=True, stop=True)
+            nc.vector.tensor_copy(out=asm[:, NWIN + m0 : NWIN + m1, 2:8:5].rearrange("p m e -> p e m"), in_=ml[:, :, 0:nm])
+            halves = []
+            for h in range(2):
+                ks = [k for k in range(k0, k1) if k % 2 == h]
+                halves.append((h, ks[0], len(ks)))
+            for h, ka, n in halves:
                 hs = slice(64 * h, 64 * h + 64)
-                av = asm[hs, NWIN : NWIN + n, 0:25].rearrange("p m (s y) -> p s y m", y=5)
-                nc.vector.tensor_copy(out=av[:, :, 0:2, :], in_=mf[hs, :, :, h : h + 2 * n - 1 : 2, 1])
-                nc.vector.tensor_copy(out=av[:, :, 3:5, :], in_=mf[hs, :, :, h + 1 : h + 2 * n : 2, 0])
-            nc.vector.tensor_copy(out=asm[0:64, 1:NWIN, 0:25:5].rearrange("p w s -> p s w"), in_=t2[0:64, :, 0 : NWIN - 1])
-            for c0 in range(0, NWIN, 8):
-                c1 = min(c0 + 8, NWIN)
-                tp = ps["t"].tile([P, 8, P], BF16, name="tp")
+                av = asm[hs, NWIN + ka // 2 : NWIN + ka // 2 + n, 0:25].rearrange("p m (s y) -> p s y m", y=5)
+                nc.vector.tensor_copy(out=av[:, :, 0:2, :], in_=mf[hs, :, :, ka - s0 : ka - s0 + 2 * n - 1 : 2, 1])
+                nc.vector.tensor_copy(out=av[:, :, 3:5, :], in_=mf[hs, :, :, ka + 1 - s0 : ka - s0 + 2 * n : 2, 0])
+            ta = max(f0, 1)
+            nc.vector.tensor_copy(
+                out=asm[0:64, ta:f1, 0:25:5].rearrange("p w s -> p s w"), in_=t2[0:64, :, ta - 1 - s0 : f1 - 1 - s0]
+            )
+            for c0 in range(f0, f1, 8):
+                c1 = min(c0 + 8, f1)
+                tp = ps["c"].tile([P, 8, P], BF16, name="tp", tag="c")
                 for w in range(c0, c1):
                     nc.tensor.transpose(tp[:, w - c0, :], asm[:, w, :], ident_b[:])
                 nc.scalar.copy(
                     out=lrow[:, 3 * c0 * 64 : 3 * c1 * 64].rearrange("p (w c) -> p w c", c=192)[:, :, 0:P], in_=tp[0:32, 0 : c1 - c0, :]
                 )
-            for c0 in range(0, NLAN, 8):
-                c1 = min(c0 + 8, NLAN)
-                tp = ps["t"].tile([P, 8, P], BF16, name="tp")
-                for m in range(c0, c1):
-                    nc.tensor.transpose(tp[:, m - c0, :], asm[:, NWIN + m, :], ident_b[:])
-                for h, n in halves:
-                    cn = min(c1, n) - c0
-                    st = (3 * (2 * c0 + h) + 2) * 64
-                    nc.scalar.copy(
-                        out=lrow[:, st : st + cn * 384].rearrange("p (k c) -> p k c", c=384)[:, :, 0:64],
-                        in_=tp[0:32, 0:cn, 64 * h : 64 * h + 64],
-                    )
-            for y0 in range(0, 64, 16):
-                cols = slice(y0 * 64, (y0 + 16) * 64)
-                lc = slice((y0 + 1) * 64, (y0 + 17) * 64)
+            ma = k0 // 2
+            mb = (k1 - 1) // 2 + 1
+            tq = ps["c"].tile([P, 8, P], BF16, name="tq", tag="c")
+            for m in range(ma, mb):
+                nc.tensor.transpose(tq[:, m - ma, :], asm[:, NWIN + m, :], ident_b[:])
+            for h, ka, n in halves:
+                st = (3 * ka + 2) * 64
+                nc.scalar.copy(
+                    out=lrow[:, st : st + n * 384].rearrange("p (k c) -> p k c", c=384)[:, :, 0:64],
+                    in_=tq[0:32, ka // 2 - ma : ka // 2 - ma + n, 64 * h : 64 * h + 64],
+                )
+        def hop(j):
+            blocks = RUNS[j][8]
+            na = blocks[0]
+            for nb in (na + 1, blocks[-1] + 1):
+                cols = slice(na * NB, nb * NB)
+                lc = slice(na * NB + 64, nb * NB + 64)
                 nc.sync.dma_start(out=raw1[0:1, 0, cols], in_=lrow[0:1, lc])
                 for t in range(1, 4):
                     nc.sync.dma_start(out=raw1[0:8, t, cols], in_=lrow[t : t + 22 : 3, lc])
+                na = nb
 
         def weights():
-            wv = conv_w.rearrange("(m p) k -> p m k", p=P)
-            nc.sync.dma_start(out=b_in[0:8, :], in_=conv_b.rearrange("(m p) -> m p", p=P))
-            b_ps = ps["w"].tile([P, P], BF16, name="b_ps", tag="wt")
+            b_ps = ps["c"].tile([P, P], BF16, name="b_ps", tag="c")
             nc.tensor.transpose(b_ps[:], b_in[:], ident_b[:])
             nc.vector.tensor_copy(out=bias[:], in_=b_ps[:, 0:8])
             for mp in range(4):
-                w_sb = stage.tile([P, 2, OC], BF16, name="w_sb", tag="grouped", align_bytes=64)
-                w_tail = stage.tile([P, 2, 32], BF16, name="w_tail")
-                ms = slice(2 * mp, 2 * mp + 2)
-                nc.sync.dma_start(out=w_sb[:, :, 0:512], in_=wv[:, ms, 0:512])
-                nc.sync.dma_start(out=w_sb[:, :, 544:1024], in_=wv[:, ms, 512:992])
-                nc.sync.dma_start(out=w_tail[:], in_=wv[:, ms, 992:1024])
+                w_sb = w_sbs[mp]
+                w_tail = w_tails[mp]
                 oct_w = w_sb[:, :, 512:544].rearrange("p m (q t) -> p m q t", t=4)
                 nc.vector.tensor_copy(out=oct_w[:, :, :, 1:4], in_=w_tail[:, :, 8:32].rearrange("p m (q t) -> p m q t", t=3))
                 nc.vector.tensor_copy(out=oct_w[:, :, 1:8, 0], in_=w_tail[:, :, 0:7])
                 nc.vector.tensor_copy(out=oct_w[:, :, 0:1, 0], in_=w_tail[:, :, 7:8])
                 w32 = w_sb[:].rearrange("p m k -> p (m k)").bitcast(F32).rearrange("p (m k) -> p m k", m=2)
-                wg = stage.tile([P, 2, 1024], BF16, name="wg", tag="grouped", align_bytes=64)
                 for g in range(2):
-                    wt = ps["w"].tile([P, 2, 2, P], F32, name="wt", tag="wt")
+                    wg = outs.tile([P, 1024], BF16, name="wg", tag="ot", align_bytes=64)
+                    wt = ps["c"].tile([P, 2, 2, P], F32, name="wt", tag="c")
                     for m2 in range(2):
                         for u in range(2):
                             nc.tensor.transpose(wt[:, m2, u, :], w32[:, m2, 256 * g + u : 256 * (g + 1) : 2], ident_f[:])
                     nc.scalar.copy(
-                        out=wg[:, g, :].bitcast(F32).rearrange("p (m o u) -> p m o u", m=2, u=2),
+                        out=wg[:].bitcast(F32).rearrange("p (m o u) -> p m o u", m=2, u=2),
                         in_=wt[:].rearrange("p m u o -> p m o u"),
                     )
                     nc.vector.quantize_mx(
                         out=w_codes[:, g, 256 * mp : 256 * (mp + 1)].bitcast(FP8X4),
                         scales=w_scales[:, g, 256 * mp : 256 * (mp + 1)],
-                        in_=wg[:, g, :],
+                        in_=wg[:],
                     )
 
         def conv_block(n):
@@ -409,7 +362,8 @@ def tile_spatialcontext_kernel(tc, feature, conv_w, conv_b, out):
                     out=x_codes[:, g, :].bitcast(FP8X4), scales=x_scales[:, g, :], in_=grouped[:].rearrange("p w j -> p (w j)")
                 )
             for m in range(8):
-                acc = ps["acc"].tile([P, NB], F32, name="acc")
+                pool, tag = banks[(8 * n + m) % len(banks)]
+                acc = pool.tile([P, NB], F32, name="acc", tag=tag)
                 for g in range(2):
                     nc.tensor.matmul_mx(
                         out=acc[:],
@@ -420,31 +374,125 @@ def tile_spatialcontext_kernel(tc, feature, conv_w, conv_b, out):
                         start=(g == 0),
                         stop=(g == 1),
                     )
-                ot = outs.tile([P, NB], F32, name="ot")
+                ot = outs.tile([P, NB], F32, name="ot", tag="ot", align_bytes=64)
                 nc.scalar.activation(out=ot[:], in_=acc[:], func=ACT.Relu, bias=bias[:, m : m + 1], scale=1.0)
                 nc.sync.dma_start(out=out2[m * P : (m + 1) * P, cols], in_=ot[:])
 
-        with ExitStack() as c1:
-            ps["g"] = c1.enter_context(tc.psum_pool(name="ps_g", bufs=2))
-            ps_p = c1.enter_context(tc.psum_pool(name="ps_p", bufs=1))
-            ps["x"] = c1.enter_context(tc.psum_pool(name="ps_x", bufs=1))
-            ps["pp0"] = ps_p.tile([P, NHALF, 45], F32, name="pp0")
-            ps["pp1"] = ps_p.tile([P, NHALF, 45], F32, name="pp1")
-            for ci in range(len(CHUNKS)):
-                prep(ci)
-                gram(ci)
-                lanes(ci)
-                if ci % 2 == 1:
-                    unrotate(ci // 2)
-        with ExitStack() as c2:
-            ps["s"] = c2.enter_context(tc.psum_pool(name="ps_s", bufs=1))
-            ps["f"] = c2.enter_context(tc.psum_pool(name="ps_f", bufs=1))
-            ps["t"] = c2.enter_context(tc.psum_pool(name="ps_t", bufs=3))
-            ps["w"] = c2.enter_context(tc.psum_pool(name="ps_w", bufs=2))
-            norms()
-            finish()
-            weights()
-        with ExitStack() as c3:
-            ps["acc"] = c3.enter_context(tc.psum_pool(name="ps_acc", bufs=8))
-            for n in range(8):
-                conv_block(n)
+        ps["g"] = ctx.enter_context(tc.psum_pool(name="ps_g", bufs=1))
+        ps_p = ctx.enter_context(tc.psum_pool(name="ps_p", bufs=1))
+        ps["x"] = ctx.enter_context(tc.psum_pool(name="ps_x", bufs=1))
+        ps["c"] = ctx.enter_context(tc.psum_pool(name="ps_c", bufs=2))
+        ps["pp0"] = ps_p.tile([P, NHALF, 45], F32, name="pp0")
+        ps["pp1"] = ps_p.tile([P, NHALF, 45], F32, name="pp1")
+        banks = ((ps["g"], "gp"), (ps_p, "pp0"), (ps_p, "pp1"), (ps["x"], "x0"), (ps["x"], "x1"), (ps["x"], "x2"))
+        prep(0)
+
+        def row_iota(name, n, pattern, base):
+            t = keep.tile([P, n], F32, name=name)
+            nc.gpsimd.iota(t[:], pattern=pattern, base=base, channel_multiplier=0, allow_small_or_imprecise_dtypes=True)
+            return t
+
+        def col(name, n=1):
+            return keep.tile([P, n], F32, name=name)
+
+        iop = col("iop")
+        nc.gpsimd.iota(iop[:], pattern=[[0, 1]], base=0, channel_multiplier=1, allow_small_or_imprecise_dtypes=True)
+        t24 = row_iota("t24", 5, [[24, 5]], 24)
+        t5 = row_iota("t5", 13, [[5, 13]], 5)
+        r5 = row_iota("r5", 5, [[1, 5]], 0)
+        j45 = keep.tile([P, 45], F32, name="j45")
+        nc.gpsimd.iota(j45[:, 0:25], pattern=[[1, 25]], base=0, channel_multiplier=0, allow_small_or_imprecise_dtypes=True)
+        nc.gpsimd.iota(j45[:, 25:45], pattern=[[1, 20]], base=0, channel_multiplier=0, allow_small_or_imprecise_dtypes=True)
+        xrel = keep.tile([P, 64], F32, name="xrel")
+        for sg in range(3):
+            nc.gpsimd.iota(
+                xrel[:, XLO[sg] : XHI[sg]], pattern=[[1, XHI[sg] - XLO[sg]]], base=XLO[sg] - X0[sg], channel_multiplier=0,
+                allow_small_or_imprecise_dtypes=True,
+            )
+        jsh = keep.tile([P, 5, 2, 64], F32, name="jsh")
+        nc.gpsimd.iota(jsh[:], pattern=[[1, 5], [0, 2], [1, 64]], base=0, channel_multiplier=0, allow_small_or_imprecise_dtypes=True)
+
+        def count_le(name, thresholds, value):
+            n = thresholds.shape[1]
+            g = col(name + "_g", n)
+            nc.vector.tensor_scalar(out=g[:], in0=thresholds[:], scalar1=value[:, 0:1], scalar2=None, op0=ALU.is_le)
+            c = col(name)
+            nc.vector.tensor_reduce(out=c[:], in_=g[:], axis=AX.X, op=ALU.add)
+            return c
+
+        def fma(name, a, k, b):
+            t = col(name)
+            nc.vector.scalar_tensor_tensor(out=t[:], in0=a[:], scalar=k, in1=b[:], op0=ALU.mult, op1=ALU.add)
+            return t
+
+        s5 = count_le("s5", t24, iop)
+        ii = fma("ii", s5, -24.0, iop)
+        c5 = count_le("c5", t5[:, 0:4], ii)
+        cls = fma("cls", c5, -5.0, ii)
+        pen = col("pen")
+        nc.vector.tensor_scalar(out=pen[:], in0=s5[:], scalar1=5.0, scalar2=1000.0, op0=ALU.is_ge, op1=ALU.mult)
+        sp = col("sp")
+        nc.vector.tensor_tensor(out=sp[:], in0=s5[:], in1=pen[:], op=ALU.add)
+        key = fma("key", cls, 5.0, sp)
+        sel = keep.tile([P, 45], F32, name="sel")
+        nc.vector.tensor_scalar(out=sel[:], in0=j45[:], scalar1=key[:, 0:1], scalar2=None, op0=ALU.is_equal)
+
+        dd = col("dd", 64)
+        nc.vector.tensor_scalar(out=dd[:], in0=xrel[:], scalar1=ii[:, 0:1], scalar2=None, op0=ALU.subtract)
+        d2 = col("d2", 64)
+        nc.vector.tensor_tensor(out=d2[:], in0=dd[:], in1=dd[:], op=ALU.mult)
+        lt120 = col("lt120")
+        nc.vector.tensor_scalar(out=lt120[:], in0=iop[:], scalar1=120.0, scalar2=None, op0=ALU.is_lt)
+        mask = keep.tile([P, 2, 64], F32, name="mask")
+        for t in range(2):
+            nc.vector.tensor_scalar(out=mask[:, t, :], in0=d2[:], scalar1=4.5, scalar2=lt120[:, 0:1], op0=ALU.is_le, op1=ALU.mult)
+
+        gram(0)
+        lanes(0)
+
+        h64 = col("h64")
+        nc.vector.tensor_scalar(out=h64[:], in0=iop[:], scalar1=64.0, scalar2=None, op0=ALU.is_ge)
+        px = fma("px", h64, -64.0, iop)
+        px3 = col("px3")
+        nc.vector.tensor_scalar(out=px3[:], in0=px[:], scalar1=3.0, scalar2=None, op0=ALU.add)
+        q5 = count_le("q5", t5, px3)
+        sx = fma("sx", q5, -5.0, px3)
+        ind = col("ind", 5)
+        nc.vector.tensor_scalar(out=ind[:], in0=r5[:], scalar1=sx[:, 0:1], scalar2=None, op0=ALU.is_equal)
+        room = col("room")
+        nc.vector.tensor_scalar(out=room[:], in0=px[:], scalar1=-1.0, scalar2=63.0, op0=ALU.mult, op1=ALU.add)
+        valid = col("valid", 3)
+        nc.vector.tensor_scalar(out=valid[:], in0=r5[:, 0:3], scalar1=room[:, 0:1], scalar2=None, op0=ALU.is_le)
+        tg0 = col("tg0")
+        nc.vector.tensor_scalar(out=tg0[:], in0=h64[:], scalar1=1000.0, scalar2=2.0, op0=ALU.mult, op1=ALU.add)
+        tga = col("tga")
+        nc.vector.tensor_tensor(out=tga[:], in0=tg0[:], in1=iop[:], op=ALU.add)
+        tgb = col("tgb")
+        nc.vector.tensor_scalar(out=tgb[:], in0=tga[:], scalar1=-1064.0, scalar2=None, op0=ALU.add)
+        shf = keep.tile([P, 2, 5, P], F32, name="shf")
+        shb = keep.tile([P, 2, 5, P], BF16, name="shb")
+        jshv = jsh[:].rearrange("p s h x -> p s (h x)")
+        for a, tg in ((0, tga), (1, tgb)):
+            nc.vector.tensor_scalar(out=shf[:, a], in0=jshv, scalar1=tg[:, 0:1], scalar2=None, op0=ALU.is_equal)
+            nc.vector.tensor_scalar(out=shb[:, a], in0=jshv, scalar1=tg[:, 0:1], scalar2=None, op0=ALU.is_equal)
+        shk = keep.tile([P, 2, P], BF16, name="shk")
+        for a in range(2):
+            nc.vector.tensor_copy(out=shk[:, :, 64 * a : 64 * a + 64], in_=shb[:, a, 0:2, 64 * a : 64 * a + 64])
+        nc.vector.memset(asm[:], 0.0)
+
+        weights()
+        for ci in range(1, len(CHUNKS)):
+            prep(ci)
+            if ci == 3:
+                hop(0)
+            gram(ci)
+            lanes(ci)
+            if ci % 2 == 1:
+                unrotate(ci // 2)
+                norms(ci // 2)
+                finish(ci // 2)
+        for n in RUNS[0][8]:
+            conv_block(n)
+        hop(1)
+        for n in RUNS[1][8]:
+            conv_block(n)

@@ -206,7 +206,7 @@ def tile_spatialcontext_kernel(tc, feature, conv_w, conv_b, out):
                 x0s = lan2.tile([P, 1024], BF16, name="x0s")
                 nc.scalar.copy(out=x0s[:], in_=xs[0][:])
                 js = lan.tile([P, 1024], BF16, name="js")
-                nc.scalar.activation(out=js[:], in_=xs[0][:], func=ACT.Square, accum_out=nbt[:, b : b + 1])
+                nc.scalar.activation(out=js[:], in_=x0s[:], func=ACT.Square, accum_out=nbt[:, b : b + 1])
                 for d in (1, 2):
                     jv = lan.tile([P, 1024], BF16, name="jv")
                     nc.vector.scalar_tensor_tensor(

@@ -30,7 +30,8 @@ NWIN = 22
 NLAN = 11
 
 LOAD_ROWS = (0, 15, 33, 48, 64)
-CHUNKS = ((0, 5, 0, 2), (5, 11, 2, 5), (11, 16, 5, 8), (16, 22, 8, 11))
+CHUNKS = ((0, 5, 2, 2), (5, 11, 2, 5), (11, 16, 5, 8), (16, 22, 8, 11))
+NGRAM = 2
 NWMAX = 6
 NMMAX = 3
 NHALF = 11
@@ -110,6 +111,7 @@ def tile_spatialcontext_kernel(tc, feature, conv_w, conv_b, out):
         sbts = {}
         ubts = {}
         ps = {}
+        live = {}
 
         def prep(ci):
             w0, w1, m0, m1 = CHUNKS[ci]
@@ -130,6 +132,8 @@ def tile_spatialcontext_kernel(tc, feature, conv_w, conv_b, out):
                         in_=img[:, :, ya:yb, X0[sg] : X0[sg] + SW],
                     )
             sbts[ci] = sbt
+            if m0 == m1:
+                return
             ka = 2 * m0
             kb = min(2 * m1, 21)
             ubt = patch.tile([P, 8, NMMAX * P + 8], BF16, name="ubt")
@@ -176,6 +180,42 @@ def tile_spatialcontext_kernel(tc, feature, conv_w, conv_b, out):
                     nc.tensor.matmul(
                         pp[:, wi % NHALF, :], lhsT=gm[:, wi - c0].rearrange("p t x -> p (t x)"), rhs=sel[:], start=True, stop=True
                     )
+
+        def still_gram():
+            sbt = sbts[0]
+            gp = ps["g"].tile([P, 4, 2, 64], F32, name="gp")
+            gm = chain.tile([P, 4, 2, 64], F32, name="gm")
+            for m in range(NGRAM):
+                for h in range(2):
+                    wi = 2 * m + h
+                    for sg in range(3):
+                        for s in range(8):
+                            img = raws[s // 4][:, s % 4, 0:HW].rearrange("p (y x) -> p y x", x=64)
+                            nc.tensor.matmul(
+                                gp[:, m, h : h + 1, XLO[sg] : XHI[sg]],
+                                lhsT=sbt[:, s, sg, 3 * wi * SW : 3 * wi * SW + P],
+                                rhs=img[:, 3 * wi + 1 : 3 * wi + 2, XLO[sg] : XHI[sg]],
+                                start=(s == 0),
+                                stop=(s == 7),
+                            )
+            nc.vector.tensor_tensor(
+                out=gm[:, 0:NGRAM], in0=gp[:, 0:NGRAM], in1=mask[:].unsqueeze(1).to_broadcast([P, NGRAM, 2, 64]), op=ALU.mult
+            )
+            p3 = ps["c"].tile([P, NGRAM, 9], F32, name="p3", tag="c")
+            for m in range(NGRAM):
+                nc.tensor.matmul(p3[:, m, :], lhsT=gm[:, m].rearrange("p t x -> p (t x)"), rhs=sel[:, 3:45:5], start=True, stop=True)
+            live["p3"] = p3
+
+        def still_unrotate():
+            nm = RUNS[0][3] - RUNS[0][2]
+            b = NBASE[0] + NHALF
+            o = nbt[:, b : b + 3 * nm].rearrange("p (d m) -> p d m", d=3)[:, :, 0:NGRAM]
+            p3 = live["p3"]
+            nc.vector.tensor_scalar(out=o, in0=p3[:, :, 2:5].rearrange("p m d -> p d m"), scalar1=ind[:, 0:1], scalar2=None, op0=ALU.mult)
+            for s in range(1, 5):
+                nc.vector.scalar_tensor_tensor(
+                    out=o, in0=p3[:, :, s + 2 : s + 5].rearrange("p m d -> p d m"), scalar=ind[:, s : s + 1], in1=o, op0=ALU.mult, op1=ALU.add
+                )
 
         def unrotate(j):
             pp = ps["pp%d" % j]
@@ -448,7 +488,7 @@ def tile_spatialcontext_kernel(tc, feature, conv_w, conv_b, out):
             nc.vector.tensor_scalar(out=mask[:, t, :], in0=d2[:], scalar1=4.5, scalar2=lt120[:, 0:1], op0=ALU.is_le, op1=ALU.mult)
 
         gram(0)
-        lanes(0)
+        still_gram()
 
         h64 = col("h64")
         nc.vector.tensor_scalar(out=h64[:], in0=iop[:], scalar1=64.0, scalar2=None, op0=ALU.is_ge)
@@ -480,6 +520,7 @@ def tile_spatialcontext_kernel(tc, feature, conv_w, conv_b, out):
             nc.vector.tensor_copy(out=shk[:, :, 64 * a : 64 * a + 64], in_=shb[:, a, 0:2, 64 * a : 64 * a + 64])
         nc.vector.memset(asm[:], 0.0)
 
+        still_unrotate()
         weights()
         for ci in range(1, len(CHUNKS)):
             prep(ci)

@@ -30,7 +30,8 @@ NWIN = 22
 NLAN = 11
 
 LOAD_ROWS = (0, 15, 33, 48, 64)
-CHUNKS = ((0, 5, 2, 2), (5, 11, 2, 5), (11, 16, 5, 8), (16, 22, 8, 11))
+CHUNKS = ((0, 5, 0, 2), (5, 11, 2, 5), (11, 16, 5, 8), (16, 22, 10, 11))
+GTILES = (8, 9)
 NGRAM = 2
 NWMAX = 6
 NMMAX = 3
@@ -182,18 +183,19 @@ def tile_spatialcontext_kernel(tc, feature, conv_w, conv_b, out):
                     )
 
         def still_gram():
-            sbt = sbts[0]
+            sbt = sbts[3]
+            w0 = CHUNKS[3][0]
             gp = ps["g"].tile([P, 4, 2, 64], F32, name="gp")
             gm = chain.tile([P, 4, 2, 64], F32, name="gm")
             for m in range(NGRAM):
                 for h in range(2):
-                    wi = 2 * m + h
+                    wi = 2 * GTILES[m] + h
                     for sg in range(3):
                         for s in range(8):
                             img = raws[s // 4][:, s % 4, 0:HW].rearrange("p (y x) -> p y x", x=64)
                             nc.tensor.matmul(
                                 gp[:, m, h : h + 1, XLO[sg] : XHI[sg]],
-                                lhsT=sbt[:, s, sg, 3 * wi * SW : 3 * wi * SW + P],
+                                lhsT=sbt[:, s, sg, 3 * (wi - w0) * SW : 3 * (wi - w0) * SW + P],
                                 rhs=img[:, 3 * wi + 1 : 3 * wi + 2, XLO[sg] : XHI[sg]],
                                 start=(s == 0),
                                 stop=(s == 7),
@@ -207,9 +209,10 @@ def tile_spatialcontext_kernel(tc, feature, conv_w, conv_b, out):
             live["p3"] = p3
 
         def still_unrotate():
-            nm = RUNS[0][3] - RUNS[0][2]
-            b = NBASE[0] + NHALF
-            o = nbt[:, b : b + 3 * nm].rearrange("p (d m) -> p d m", d=3)[:, :, 0:NGRAM]
+            nm = RUNS[1][3] - RUNS[1][2]
+            b = NBASE[1] + NHALF
+            ma = GTILES[0] - RUNS[1][2]
+            o = nbt[:, b : b + 3 * nm].rearrange("p (d m) -> p d m", d=3)[:, :, ma : ma + NGRAM]
             p3 = live["p3"]
             nc.vector.tensor_scalar(out=o, in0=p3[:, :, 2:5].rearrange("p m d -> p d m"), scalar1=ind[:, 0:1], scalar2=None, op0=ALU.mult)
             for s in range(1, 5):
@@ -488,7 +491,7 @@ def tile_spatialcontext_kernel(tc, feature, conv_w, conv_b, out):
             nc.vector.tensor_scalar(out=mask[:, t, :], in0=d2[:], scalar1=4.5, scalar2=lt120[:, 0:1], op0=ALU.is_le, op1=ALU.mult)
 
         gram(0)
-        still_gram()
+        lanes(0)
 
         h64 = col("h64")
         nc.vector.tensor_scalar(out=h64[:], in0=iop[:], scalar1=64.0, scalar2=None, op0=ALU.is_ge)
@@ -520,14 +523,17 @@ def tile_spatialcontext_kernel(tc, feature, conv_w, conv_b, out):
             nc.vector.tensor_copy(out=shk[:, :, 64 * a : 64 * a + 64], in_=shb[:, a, 0:2, 64 * a : 64 * a + 64])
         nc.vector.memset(asm[:], 0.0)
 
-        still_unrotate()
         weights()
         for ci in range(1, len(CHUNKS)):
             prep(ci)
             if ci == 3:
                 hop(0)
             gram(ci)
+            if ci == 3:
+                still_gram()
             lanes(ci)
+            if ci == 3:
+                still_unrotate()
             if ci % 2 == 1:
                 unrotate(ci // 2)
                 norms(ci // 2)

from contextlib import ExitStack

import concourse.mybir as mybir
from concourse.masks import make_identity

FLOPS = 2 * 1024 * 1024 * 4096 + 2 * 25 * 999 * 4096

BF16 = mybir.dt.bfloat16
F32 = mybir.dt.float32
U32 = mybir.dt.uint32
U8 = mybir.dt.uint8
I32 = mybir.dt.int32
FP8X4 = mybir.dt.float8_e4m3fn_x4
ACT = mybir.ActivationFunctionType
ALU = mybir.AluOpType
AX = mybir.AxisListType

P = 128
HW = 4096
HWP = 4112
OC = 1024
NB = 512
EPS = 1e-12

SW = 24
X0 = (0, 20, 40)
XLO = (0, 22, 42)
XHI = (22, 42, 64)
NWIN = 22
NLAN = 11

LOAD_ROWS = (0, 15, 33, 48, 64)
CHUNKS = ((0, 5, 0, 2), (5, 11, 2, 5), (11, 16, 5, 8), (16, 22, 10, 11))
GTILES = (8, 9)
NGRAM = 2
NWMAX = 6
NMMAX = 3
NHALF = 11
NOUT = 8
RUNS = ((0, 11, 0, 5, 0, 10, 0, 9, (0, 1, 2)), (11, 22, 5, 11, 10, 22, 9, 21, (3, 4, 5, 6, 7)))
NBASE = (0, 26)
NSMAX = 13
NMRUN = 6


def tile_spatialcontext_kernel(tc, feature, conv_w, conv_b, out):
    nc = tc.nc
    feat = feature.rearrange("b c h w -> (b c) (h w)")
    out2 = out.rearrange("b o h w -> (b o) (h w)")

    with ExitStack() as ctx:
        keep = ctx.enter_context(tc.tile_pool(name="keep", bufs=1))
        stage = ctx.enter_context(tc.tile_pool(name="stage", bufs=4))
        patch = ctx.enter_context(tc.tile_pool(name="patch", bufs=2))
        chain = ctx.enter_context(tc.tile_pool(name="chain", bufs=2))
        codes = ctx.enter_context(tc.tile_pool(name="codes", bufs=2))
        outs = ctx.enter_context(tc.tile_pool(name="outs", bufs=NOUT))
        lan = ctx.enter_context(tc.tile_pool(name="lan", bufs=1))
        lan2 = ctx.enter_context(tc.tile_pool(name="lan2", bufs=2))

        ident_f = keep.tile([P, P], F32, name="ident_f")
        make_identity(nc, ident_f[:])
        ident_b = keep.tile([P, P], BF16, name="ident_b")
        make_identity(nc, ident_b[:])

        raw0 = keep.tile([P, 4, HWP], BF16, name="raw0")
        raw1 = keep.tile([P, 4, HWP], BF16, name="raw1")
        raws = [raw0, raw1]
        w_codes = keep.tile([P, 2, OC], U32, name="w_codes", align_bytes=64)
        w_scales = keep.tile([P, 2, OC], U8, name="w_scales", align_bytes=64)
        bias = keep.tile([P, 8], F32, name="bias")
        b_in = keep.tile([P, P], BF16, name="b_in")
        usum = keep.tile([P, NWIN, 25], F32, name="usum")
        nbt = keep.tile([P, NWIN + 3 * NLAN], F32, name="nbt")
        ris = keep.tile([P, 5, 23, 3], F32, name="ris")
        asm = keep.tile([P, NWIN + NLAN, P], BF16, name="asm")
        lrow = keep.tile([32, 69 * 64], BF16, name="lrow")

        nc.gpsimd.memset(b_in[:], 0.0)
        nc.gpsimd.memset(nbt[:], 0.0)
        nc.gpsimd.memset(ris[:], 0.0)

        def load(c):
            cols = slice(LOAD_ROWS[c] * 64, LOAD_ROWS[c + 1] * 64)
            nc.vector.memset(raw1[0:8, :, cols].bitcast(I32), 0)
            nc.sync.dma_start(out=raw0[:, :, cols], in_=feat[0:512, cols].rearrange("(p j) w -> p j w", j=4))
            nc.sync.dma_start(out=raw1[8:128, :, cols], in_=feat[512:992, cols].rearrange("(p j) w -> p j w", j=4))
            nc.sync.dma_start(out=raw1[1:8, 0, cols], in_=feat[992:999, cols])

        wv = conv_w.rearrange("(m p) k -> p m k", p=P)
        w_sbs = []
        w_tails = []

        def load_weights():
            nc.sync.dma_start(out=b_in[0:8, :], in_=conv_b.rearrange("(m p) -> m p", p=P))
            for mp in range(4):
                w_sb = stage.tile([P, 2, OC], BF16, name="w_sb", tag="grouped", align_bytes=64)
                w_tail = stage.tile([P, 2, 32], BF16, name="w_tail")
                ms = slice(2 * mp, 2 * mp + 2)
                nc.sync.dma_start(out=w_sb[:, :, 0:512], in_=wv[:, ms, 0:512])
                nc.sync.dma_start(out=w_sb[:, :, 544:1024], in_=wv[:, ms, 512:992])
                nc.sync.dma_start(out=w_tail[:], in_=wv[:, ms, 992:1024])
                w_sbs.append(w_sb)
                w_tails.append(w_tail)

        load(0)
        load(1)
        load_weights()
        load(2)
        load(3)

        sbts = {}
        ubts = {}
        ps = {}
        live = {}

        def prep(ci):
            w0, w1, m0, m1 = CHUNKS[ci]
            ylo = 3 * w0 - 2
            nr = 3 * (w1 - w0) + 2
            ya = max(0, ylo)
            yb = min(64, ylo + nr)
            sbt = patch.tile([P, 8, 3, (3 * NWMAX + 2) * SW + 8], BF16, name="sbt")
            if ya > ylo:
                nc.vector.memset(sbt[:, :, :, 0 : (ya - ylo) * SW], 0.0)
            nc.vector.memset(sbt[:, :, :, (yb - ylo) * SW : nr * SW + 8], 0.0)
            for g in range(2):
                img = raws[g][:, :, 0:HW].rearrange("p t (y x) -> p t y x", x=64)
                for sg in range(3):
                    copy = nc.scalar.copy if (g, sg) == (1, 2) else nc.vector.tensor_copy
                    copy(
                        out=sbt[:, 4 * g : 4 * g + 4, sg, (ya - ylo) * SW : (yb - ylo) * SW].rearrange("p t (y x) -> p t y x", x=SW),
                        in_=img[:, :, ya:yb, X0[sg] : X0[sg] + SW],
                    )
            sbts[ci] = sbt
            if m0 == m1:
                return
            ka = 2 * m0
            kb = min(2 * m1, 21)
            ubt = patch.tile([P, 8, NMMAX * P + 8], BF16, name="ubt")
            nc.vector.memset(ubt[:, :, (kb - ka) * 64 : (m1 - m0) * P + 8], 0.0)
            for g in range(2):
                rows = raws[g][:, :, 64:HW].rearrange("p t (k r) -> p t k r", r=192)
                nc.scalar.copy(
                    out=ubt[:, 4 * g : 4 * g + 4, 0 : (kb - ka) * 64].rearrange("p t (k x) -> p t k x", x=64),
                    in_=rows[:, :, ka:kb, 0:64],
                )
            ubts[ci] = ubt

        def gram(ci):
            w0, w1, m0, m1 = CHUNKS[ci]
            sbt = sbts[ci]
            pp = ps["pp%d" % (w0 // NHALF)]
            for c0 in range(w0, w1, 4):
                c1 = min(c0 + 4, w1)
                gp = ps["g"].tile([P, 4, 2, 64], F32, name="gp")
                gm = chain.tile([P, 4, 2, 64], F32, name="gm")
                for wi in range(c0, c1):
                    t0 = 1 if wi == 0 else 0
                    off = 3 * (wi - w0) * SW
                    for sg in range(3):
                        for s in range(8):
                            img = raws[s // 4][:, s % 4, 0:HW].rearrange("p (y x) -> p y x", x=64)
                            nc.tensor.matmul(
                                gp[:, wi - c0, t0:2, XLO[sg] : XHI[sg]],
                                lhsT=sbt[:, s, sg, off : off + P],
                                rhs=img[:, 3 * wi - 1 + t0 : 3 * wi + 1, XLO[sg] : XHI[sg]],
                                start=(s == 0),
                                stop=(s == 7),
                            )
                la = 0
                if c0 == 0:
                    nc.vector.memset(gm[:, 0, 0, :], 0.0)
                    nc.vector.tensor_tensor(out=gm[:, 0, 1, :], in0=gp[:, 0, 1, :], in1=mask[:, 1, :], op=ALU.mult)
                    la = 1
                n = c1 - c0 - la
                nc.vector.tensor_tensor(
                    out=gm[:, la : la + n], in0=gp[:, la : la + n], in1=mask[:].unsqueeze(1).to_broadcast([P, n, 2, 64]), op=ALU.mult
                )
                for wi in range(c0, c1):
                    nc.tensor.matmul(
                        pp[:, wi % NHALF, :], lhsT=gm[:, wi - c0].rearrange("p t x -> p (t x)"), rhs=sel[:], start=True, stop=True
                    )

        def still_gram():
            sbt = sbts[3]
            w0 = CHUNKS[3][0]
            gp = ps["g"].tile([P, 4, 2, 64], F32, name="gp")
            gm = chain.tile([P, 4, 2, 64], F32, name="gm")
            for m in range(NGRAM):
                for h in range(2):
                    wi = 2 * GTILES[m] + h
                    for sg in range(3):
                        for s in range(8):
                            img = raws[s // 4][:, s % 4, 0:HW].rearrange("p (y x) -> p y x", x=64)
                            nc.tensor.matmul(
                                gp[:, m, h : h + 1, XLO[sg] : XHI[sg]],
                                lhsT=sbt[:, s, sg, 3 * (wi - w0) * SW : 3 * (wi - w0) * SW + P],
                                rhs=img[:, 3 * wi + 1 : 3 * wi + 2, XLO[sg] : XHI[sg]],
                                start=(s == 0),
                                stop=(s == 7),
                            )
            nc.vector.tensor_tensor(
                out=gm[:, 0:NGRAM], in0=gp[:, 0:NGRAM], in1=mask[:].unsqueeze(1).to_broadcast([P, NGRAM, 2, 64]), op=ALU.mult
            )
            p3 = ps["c"].tile([P, NGRAM, 9], F32, name="p3", tag="c")
            for m in range(NGRAM):
                nc.tensor.matmul(p3[:, m, :], lhsT=gm[:, m].rearrange("p t x -> p (t x)"), rhs=sel[:, 3:45:5], start=True, stop=True)
            live["p3"] = p3

        def still_unrotate():
            nm = RUNS[1][3] - RUNS[1][2]
            b = NBASE[1] + NHALF
            ma = GTILES[0] - RUNS[1][2]
            o = nbt[:, b : b + 3 * nm].rearrange("p (d m) -> p d m", d=3)[:, :, ma : ma + NGRAM]
            p3 = live["p3"]
            nc.vector.tensor_scalar(out=o, in0=p3[:, :, 2:5].rearrange("p m d -> p d m"), scalar1=ind[:, 0:1], scalar2=None, op0=ALU.mult)
            for s in range(1, 5):
                nc.vector.scalar_tensor_tensor(
                    out=o, in0=p3[:, :, s + 2 : s + 5].rearrange("p m d -> p d m"), scalar=ind[:, s : s + 1], in1=o, op0=ALU.mult, op1=ALU.add
                )

        def unrotate(j):
            pp = ps["pp%d" % j]
            u = usum[:, NHALF * j : NHALF * (j + 1), :]
            nc.vector.tensor_scalar(out=u, in0=pp[:, :, 0:25], scalar1=ind[:, 0:1], scalar2=None, op0=ALU.mult)
            for s in range(1, 5):
                nc.vector.scalar_tensor_tensor(
                    out=u, in0=pp[:, :, 5 * s : 5 * s + 25], scalar=ind[:, s : s + 1], in1=u, op0=ALU.mult, op1=ALU.add
                )
            for t in range(2):
                hs = slice(64 * t, 64 * t + 64)
                nc.vector.tensor_copy(out=nbt[hs, NBASE[j] : NBASE[j] + NHALF], in_=usum[hs, NHALF * j : NHALF * (j + 1), 11 + t])

        def lanes(ci):
            w0, w1, m0, m1 = CHUNKS[ci]
            ubt = ubts[ci]
            for m in range(m0, m1):
                ml = m - m0
                j = 0 if m < RUNS[0][3] else 1
                nm = RUNS[j][3] - RUNS[j][2]
                b = NBASE[j] + NHALF + m - RUNS[j][2]
                xs = []
                for d in range(3):
                    xt = ps["x"].tile([P, 1024], BF16, name="x%d" % d)
                    for s in range(8):
                        nc.tensor.transpose(xt[:, P * s : P * (s + 1)], ubt[:, s, P * ml + d : P * ml + d + P], ident_b[:])
                    xs.append(xt)
                x0s = lan2.tile([P, 1024], BF16, name="x0s")
                nc.scalar.copy(out=x0s[:], in_=xs[0][:])
                js = lan.tile([P, 1024], BF16, name="js")
                nc.scalar.activation(out=js[:], in_=x0s[:], func=ACT.Square, accum_out=nbt[:, b : b + 1])
                for d in (1, 2):
                    jv = lan.tile([P, 1024], BF16, name="jv")
                    nc.vector.scalar_tensor_tensor(
                        out=jv[:], in0=xs[d][:], scalar=1.0, in1=x0s[:], op0=ALU.mult, op1=ALU.mult,
                        accum_out=nbt[:, b + d * nm : b + d * nm + 1],
                    )

        def norms(j):
            w0, w1, m0, m1, f0, f1, k0, k1, blocks = RUNS[j]
            nw = w1 - w0
            nm = m1 - m0
            ncol = nw + nm
            b = NBASE[j]
            rn = ps["c"].tile([P, 5, 2, NHALF + NMRUN], F32, name="rn", tag="c")
            for s in range(5):
                for a in range(2):
                    nc.tensor.matmul(rn[:, s, a, 0:ncol], lhsT=shf[:, a, s, :], rhs=nbt[:, b : b + ncol], start=True, stop=True)
            rs = chain.tile([P, 5, 2, NHALF + NMRUN], F32, name="rs")
            r = rs[:, :, :, 0:ncol]
            nc.scalar.activation(out=r, in_=rn[:, :, :, 0:ncol], func=ACT.Sqrt)
            nc.vector.tensor_scalar_max(out=r, in0=r, scalar1=EPS)
            nc.vector.reciprocal(out=ris[:, :, w0:w1, 1:3].rearrange("p s w a -> p s a w"), in_=rs[:, :, :, 0:nw])
            nc.vector.reciprocal(
                out=ris[:, :, 2 * m0 + 1 : 2 * m1 + 1, 0].rearrange("p s (m a) -> p s a m", a=2), in_=rs[:, :, :, nw:ncol]
            )
            for t in range(2):
                hs = slice(64 * t, 64 * t + 64)
                nc.vector.tensor_tensor(
                    out=usum[hs, w0:w1, :], in0=usum[hs, w0:w1, :],
                    in1=ris[hs, 2, w0:w1, 1 + t].unsqueeze(2).to_broadcast([64, nw, 25]), op=ALU.mult,
                )
            lt = nbt[:, b + nw : b + nw + 3 * nm].rearrange("p (d m) -> p d m", d=3)
            nc.vector.tensor_tensor(out=lt, in0=lt, in1=valid[:].unsqueeze(2).to_broadcast([P, 3, nm]), op=ALU.mult)
            for h in range(2):
                hs = slice(64 * h, 64 * h + 64)
                g = ris[hs, :, 2 * m0 + 1 + h : 2 * m1 + h : 2, 0]
                lh = nbt[hs, b + nw : b + nw + 3 * nm].rearrange("p (d m) -> p d m", d=3)
                nc.vector.tensor_tensor(out=lh, in0=lh, in1=g[:, 2:5, :], op=ALU.mult)
                nc.vector.tensor_tensor(
                    out=asm[hs, NWIN + m0 : NWIN + m1, 12:23:5].rearrange("p m d -> p d m"), in0=lh,
                    in1=g[:, 2, :].unsqueeze(1).to_broadcast([64, 3, nm]), op=ALU.mult,
                )

        def finish(j):
            w0, w1, m0, m1, f0, f1, k0, k1, blocks = RUNS[j]
            nm = m1 - m0
            for t in range(2):
                hs = slice(64 * t, 64 * t + 64)
                uv = usum[hs, f0:f1, :].rearrange("p w (s r) -> p w s r", r=5)
                av = asm[hs, f0:f1, 0:25].rearrange("p w (s y) -> p w s y", y=5)
                for ra, rb, wo in ((0, 3, 0), (3, 4 + t, 1)):
                    nc.vector.tensor_tensor(
                        out=av[:, :, :, ra + 1 - t : rb + 1 - t], in0=uv[:, :, :, ra:rb],
                        in1=ris[hs, :, f0 + wo : f1 + wo, ra - 3 * wo : rb - 3 * wo].rearrange("p s w r -> p w s r"), op=ALU.mult,
                    )
            s0 = max(f0 - 1, 0)
            ns = f1 - s0
            cf = ps["c"].tile([P, NB], F32, name="cf", tag="c")
            mf = cf[:, 0 : 20 * NSMAX].rearrange("p (q a w r) -> p q a w r", q=5, a=2, r=2)
            t2 = cf[:, 20 * NSMAX : 25 * NSMAX].rearrange("p (q w) -> p q w", q=5)
            ml = cf[:, 25 * NSMAX : 25 * NSMAX + 2 * NMRUN].rearrange("p (e m) -> p e m", e=2)
            for e in range(2):
                nc.tensor.matmul(
                    ml[:, e, 0:nm], lhsT=shk[:, e, :], rhs=asm[:, NWIN + m0 : NWIN + m1, 22 - 5 * e], start=True, stop=True
                )
            for s in range(5):
                c = 5 * (4 - s)
                nc.tensor.matmul(mf[:, s, 0, 0:ns, :], lhsT=shb[:, 0, s, :], rhs=asm[:, s0:f1, c + 1 : c + 5 : 3], start=True, stop=True)
                nc.tensor.matmul(mf[:, s, 1, 0:ns, :], lhsT=shb[:, 1, s, :], rhs=asm[:, s0:f1, c : c + 4 : 3], start=True, stop=True)
                nc.tensor.matmul(t2[:, s, 0:ns], lhsT=shb[:, 1, s, :], rhs=asm[:, s0:f1, c + 4], start=True, stop=True)
            nc.vector.tensor_copy(out=asm[:, NWIN + m0 : NWIN + m1, 2:8:5].rearrange("p m e -> p e m"), in_=ml[:, :, 0:nm])
            halves = []
            for h in range(2):
                ks = [k for k in range(k0, k1) if k % 2 == h]
                halves.append((h, ks[0], len(ks)))
            for h, ka, n in halves:
                hs = slice(64 * h, 64 * h + 64)
                av = asm[hs, NWIN + ka // 2 : NWIN + ka // 2 + n, 0:25].rearrange("p m (s y) -> p s y m", y=5)
                nc.vector.tensor_copy(out=av[:, :, 0:2, :], in_=mf[hs, :, :, ka - s0 : ka - s0 + 2 * n - 1 : 2, 1])
                nc.vector.tensor_copy(out=av[:, :, 3:5, :], in_=mf[hs, :, :, ka + 1 - s0 : ka - s0 + 2 * n : 2, 0])
            ta = max(f0, 1)
            nc.vector.tensor_copy(
                out=asm[0:64, ta:f1, 0:25:5].rearrange("p w s -> p s w"), in_=t2[0:64, :, ta - 1 - s0 : f1 - 1 - s0]
            )
            for c0 in range(f0, f1, 8):
                c1 = min(c0 + 8, f1)
                tp = ps["c"].tile([P, 8, P], BF16, name="tp", tag="c")
                for w in range(c0, c1):
                    nc.tensor.transpose(tp[:, w - c0, :], asm[:, w, :], ident_b[:])
                nc.scalar.copy(
                    out=lrow[:, 3 * c0 * 64 : 3 * c1 * 64].rearrange("p (w c) -> p w c", c=192)[:, :, 0:P], in_=tp[0:32, 0 : c1 - c0, :]
                )
            ma = k0 // 2
            mb = (k1 - 1) // 2 + 1
            tq = ps["c"].tile([P, 8, P], BF16, name="tq", tag="c")
            for m in range(ma, mb):
                nc.tensor.transpose(tq[:, m - ma, :], asm[:, NWIN + m, :], ident_b[:])
            for h, ka, n in halves:
                st = (3 * ka + 2) * 64
                nc.scalar.copy(
                    out=lrow[:, st : st + n * 384].rearrange("p (k c) -> p k c", c=384)[:, :, 0:64],
                    in_=tq[0:32, ka // 2 - ma : ka // 2 - ma + n, 64 * h : 64 * h + 64],
                )
        def hop(j):
            blocks = RUNS[j][8]
            na = blocks[0]
            for nb in (na + 1, blocks[-1] + 1):
                cols = slice(na * NB, nb * NB)
                lc = slice(na * NB + 64, nb * NB + 64)
                nc.sync.dma_start(out=raw1[0:1, 0, cols], in_=lrow[0:1, lc])
                for t in range(1, 4):
                    nc.sync.dma_start(out=raw1[0:8, t, cols], in_=lrow[t : t + 22 : 3, lc])
                na = nb

        def weights():
            b_ps = ps["c"].tile([P, P], BF16, name="b_ps", tag="c")
            nc.tensor.transpose(b_ps[:], b_in[:], ident_b[:])
            nc.vector.tensor_copy(out=bias[:], in_=b_ps[:, 0:8])
            for mp in range(4):
                w_sb = w_sbs[mp]
                w_tail = w_tails[mp]
                oct_w = w_sb[:, :, 512:544].rearrange("p m (q t) -> p m q t", t=4)
                nc.vector.tensor_copy(out=oct_w[:, :, :, 1:4], in_=w_tail[:, :, 8:32].rearrange("p m (q t) -> p m q t", t=3))
                nc.vector.tensor_copy(out=oct_w[:, :, 1:8, 0], in_=w_tail[:, :, 0:7])
                nc.vector.tensor_copy(out=oct_w[:, :, 0:1, 0], in_=w_tail[:, :, 7:8])
                w32 = w_sb[:].rearrange("p m k -> p (m k)").bitcast(F32).rearrange("p (m k) -> p m k", m=2)
                for g in range(2):
                    wg = outs.tile([P, 1024], BF16, name="wg", tag="ot", align_bytes=64)
                    wt = ps["c"].tile([P, 2, 2, P], F32, name="wt", tag="c")
                    for m2 in range(2):
                        for u in range(2):
                            nc.tensor.transpose(wt[:, m2, u, :], w32[:, m2, 256 * g + u : 256 * (g + 1) : 2], ident_f[:])
                    nc.scalar.copy(
                        out=wg[:].bitcast(F32).rearrange("p (m o u) -> p m o u", m=2, u=2),
                        in_=wt[:].rearrange("p m u o -> p m o u"),
                    )
                    nc.vector.quantize_mx(
                        out=w_codes[:, g, 256 * mp : 256 * (mp + 1)].bitcast(FP8X4),
                        scales=w_scales[:, g, 256 * mp : 256 * (mp + 1)],
                        in_=wg[:],
                    )

        def conv_block(n):
            cols = slice(n * NB, (n + 1) * NB)
            x_codes = codes.tile([P, 2, NB], U32, name="x_codes", align_bytes=64)
            x_scales = codes.tile([P, 2, NB], U8, name="x_scales", align_bytes=64)
            for g in range(2):
                grouped = stage.tile([P, NB, 4], BF16, name="grouped", tag="grouped", align_bytes=64)
                view = raws[g][:, :, cols].rearrange("p j (c i) -> p c j i", i=4)
                gview = grouped[:].rearrange("p (c i) j -> p c j i", i=4)
                nc.vector.tensor_copy(out=gview, in_=view)
                nc.vector.quantize_mx(
                    out=x_codes[:, g, :].bitcast(FP8X4), scales=x_scales[:, g, :], in_=grouped[:].rearrange("p w j -> p (w j)")
                )
            for m in range(8):
                pool, tag = banks[(8 * n + m) % len(banks)]
                acc = pool.tile([P, NB], F32, name="acc", tag=tag)
                for g in range(2):
                    nc.tensor.matmul_mx(
                        out=acc[:],
                        lhsT=w_codes[:, g, m * P : (m + 1) * P].bitcast(FP8X4),
                        lhsT_scale=w_scales[:, g, m * P : (m + 1) * P],
                        rhs=x_codes[:, g, :].bitcast(FP8X4),
                        rhs_scale=x_scales[:, g, :],
                        start=(g == 0),
                        stop=(g == 1),
                    )
                ot = outs.tile([P, NB], F32, name="ot", tag="ot", align_bytes=64)
                nc.scalar.activation(out=ot[:], in_=acc[:], func=ACT.Relu, bias=bias[:, m : m + 1], scale=1.0)
                nc.sync.dma_start(out=out2[m * P : (m + 1) * P, cols], in_=ot[:])

        ps["g"] = ctx.enter_context(tc.psum_pool(name="ps_g", bufs=1))
        ps_p = ctx.enter_context(tc.psum_pool(name="ps_p", bufs=1))
        ps["x"] = ctx.enter_context(tc.psum_pool(name="ps_x", bufs=1))
        ps["c"] = ctx.enter_context(tc.psum_pool(name="ps_c", bufs=2))
        ps["pp0"] = ps_p.tile([P, NHALF, 45], F32, name="pp0")
        ps["pp1"] = ps_p.tile([P, NHALF, 45], F32, name="pp1")
        banks = ((ps["g"], "gp"), (ps_p, "pp0"), (ps_p, "pp1"), (ps["x"], "x0"), (ps["x"], "x1"), (ps["x"], "x2"))
        prep(0)

        def row_iota(name, n, pattern, base):
            t = keep.tile([P, n], F32, name=name)
            nc.gpsimd.iota(t[:], pattern=pattern, base=base, channel_multiplier=0, allow_small_or_imprecise_dtypes=True)
            return t

        def col(name, n=1):
            return keep.tile([P, n], F32, name=name)

        iop = col("iop")
        nc.gpsimd.iota(iop[:], pattern=[[0, 1]], base=0, channel_multiplier=1, allow_small_or_imprecise_dtypes=True)
        t24 = row_iota("t24", 5, [[24, 5]], 24)
        t5 = row_iota("t5", 13, [[5, 13]], 5)
        r5 = row_iota("r5", 5, [[1, 5]], 0)
        j45 = keep.tile([P, 45], F32, name="j45")
        nc.gpsimd.iota(j45[:, 0:25], pattern=[[1, 25]], base=0, channel_multiplier=0, allow_small_or_imprecise_dtypes=True)
        nc.gpsimd.iota(j45[:, 25:45], pattern=[[1, 20]], base=0, channel_multiplier=0, allow_small_or_imprecise_dtypes=True)
        xrel = keep.tile([P, 64], F32, name="xrel")
        for sg in range(3):
            nc.gpsimd.iota(
                xrel[:, XLO[sg] : XHI[sg]], pattern=[[1, XHI[sg] - XLO[sg]]], base=XLO[sg] - X0[sg], channel_multiplier=0,
                allow_small_or_imprecise_dtypes=True,
            )
        jsh = keep.tile([P, 5, 2, 64], F32, name="jsh")
        nc.gpsimd.iota(jsh[:], pattern=[[1, 5], [0, 2], [1, 64]], base=0, channel_multiplier=0, allow_small_or_imprecise_dtypes=True)

        def count_le(name, thresholds, value):
            n = thresholds.shape[1]
            g = col(name + "_g", n)
            nc.vector.tensor_scalar(out=g[:], in0=thresholds[:], scalar1=value[:, 0:1], scalar2=None, op0=ALU.is_le)
            c = col(name)
            nc.vector.tensor_reduce(out=c[:], in_=g[:], axis=AX.X, op=ALU.add)
            return c

        def fma(name, a, k, b):
            t = col(name)
            nc.vector.scalar_tensor_tensor(out=t[:], in0=a[:], scalar=k, in1=b[:], op0=ALU.mult, op1=ALU.add)
            return t

        s5 = count_le("s5", t24, iop)
        ii = fma("ii", s5, -24.0, iop)
        c5 = count_le("c5", t5[:, 0:4], ii)
        cls = fma("cls", c5, -5.0, ii)
        pen = col("pen")
        nc.vector.tensor_scalar(out=pen[:], in0=s5[:], scalar1=5.0, scalar2=1000.0, op0=ALU.is_ge, op1=ALU.mult)
        sp = col("sp")
        nc.vector.tensor_tensor(out=sp[:], in0=s5[:], in1=pen[:], op=ALU.add)
        key = fma("key", cls, 5.0, sp)
        sel = keep.tile([P, 45], F32, name="sel")
        nc.vector.tensor_scalar(out=sel[:], in0=j45[:], scalar1=key[:, 0:1], scalar2=None, op0=ALU.is_equal)

        dd = col("dd", 64)
        nc.vector.tensor_scalar(out=dd[:], in0=xrel[:], scalar1=ii[:, 0:1], scalar2=None, op0=ALU.subtract)
        d2 = col("d2", 64)
        nc.vector.tensor_tensor(out=d2[:], in0=dd[:], in1=dd[:], op=ALU.mult)
        lt120 = col("lt120")
        nc.vector.tensor_scalar(out=lt120[:], in0=iop[:], scalar1=120.0, scalar2=None, op0=ALU.is_lt)
        mask = keep.tile([P, 2, 64], F32, name="mask")
        for t in range(2):
            nc.vector.tensor_scalar(out=mask[:, t, :], in0=d2[:], scalar1=4.5, scalar2=lt120[:, 0:1], op0=ALU.is_le, op1=ALU.mult)

        gram(0)
        lanes(0)

        h64 = col("h64")
        nc.vector.tensor_scalar(out=h64[:], in0=iop[:], scalar1=64.0, scalar2=None, op0=ALU.is_ge)
        px = fma("px", h64, -64.0, iop)
        px3 = col("px3")
        nc.vector.tensor_scalar(out=px3[:], in0=px[:], scalar1=3.0, scalar2=None, op0=ALU.add)
        q5 = count_le("q5", t5, px3)
        sx = fma("sx", q5, -5.0, px3)
        ind = col("ind", 5)
        nc.vector.tensor_scalar(out=ind[:], in0=r5[:], scalar1=sx[:, 0:1], scalar2=None, op0=ALU.is_equal)
        room = col("room")
        nc.vector.tensor_scalar(out=room[:], in0=px[:], scalar1=-1.0, scalar2=63.0, op0=ALU.mult, op1=ALU.add)
        valid = col("valid", 3)
        nc.vector.tensor_scalar(out=valid[:], in0=r5[:, 0:3], scalar1=room[:, 0:1], scalar2=None, op0=ALU.is_le)
        tg0 = col("tg0")
        nc.vector.tensor_scalar(out=tg0[:], in0=h64[:], scalar1=1000.0, scalar2=2.0, op0=ALU.mult, op1=ALU.add)
        tga = col("tga")
        nc.vector.tensor_tensor(out=tga[:], in0=tg0[:], in1=iop[:], op=ALU.add)
        tgb = col("tgb")
        nc.vector.tensor_scalar(out=tgb[:], in0=tga[:], scalar1=-1064.0, scalar2=None, op0=ALU.add)
        shf = keep.tile([P, 2, 5, P], F32, name="shf")
        shb = keep.tile([P, 2, 5, P], BF16, name="shb")
        jshv = jsh[:].rearrange("p s h x -> p s (h x)")
        for a, tg in ((0, tga), (1, tgb)):
            nc.vector.tensor_scalar(out=shf[:, a], in0=jshv, scalar1=tg[:, 0:1], scalar2=None, op0=ALU.is_equal)
            nc.vector.tensor_scalar(out=shb[:, a], in0=jshv, scalar1=tg[:, 0:1], scalar2=None, op0=ALU.is_equal)
        shk = keep.tile([P, 2, P], BF16, name="shk")
        for a in range(2):
            nc.vector.tensor_copy(out=shk[:, :, 64 * a : 64 * a + 64], in_=shb[:, a, 0:2, 64 * a : 64 * a + 64])
        nc.vector.memset(asm[:], 0.0)

        weights()
        for ci in range(1, len(CHUNKS)):
            prep(ci)
            if ci == 3:
                hop(0)
            gram(ci)
            if ci == 3:
                still_gram()
            lanes(ci)
            if ci == 3:
                still_unrotate()
            if ci % 2 == 1:
                unrotate(ci // 2)
                norms(ci // 2)
                finish(ci // 2)
        for n in RUNS[0][8]:
            conv_block(n)
        hop(1)
        for n in RUNS[1][8]:
            conv_block(n)
